import numpy as np
import ml_dtypes


def mxq(x, axis, fmt="e4m3"):
    dtype, down = {"e4m3": (ml_dtypes.float8_e4m3fn, 7), "e5m2": (ml_dtypes.float8_e5m2, 14)}[fmt]
    v = np.moveaxis(np.asarray(x, np.float32).astype(ml_dtypes.bfloat16).astype(np.float64), axis, -1)
    blocks = v.reshape(v.shape[:-1] + (-1, 32))
    amax = np.abs(blocks).max(-1, keepdims=True)
    byte = np.maximum(np.where(amax > 0, np.frexp(amax)[1] - 1 + 127, 0) - down, 1)
    scale = np.exp2(byte - 127.0)
    codes = (blocks / scale).astype(np.float32).astype(dtype).astype(np.float64)
    return np.moveaxis((codes * scale).reshape(v.shape), -1, axis)


WIDE = False


def mx_kscale(k):
    if not WIDE:
        return np.ones(k)
    levels = np.array([10, -10, 5, -5, 0])
    a = np.random.permutation(np.resize(levels, k // 512 * 4)).reshape(k // 512, 4)
    idx = np.arange(k)
    return np.exp2(a[idx // 512, idx % 128 // 32])


BF16 = ml_dtypes.bfloat16


def bf(x):
    return np.asarray(x, np.float32).astype(BF16)


def f64(x):
    return np.asarray(x).astype(np.float64)


B, H, S, D, G, W, T = 1, 2, 4096, 256, 128, 768, 128
NT = (S - G) // T
C = G + T + W
ROWS = G + np.arange(NT * T).reshape(NT, T)
START = np.clip(ROWS[:, 0] - W // 2, G, S - T - W)
COLS = np.concatenate([np.broadcast_to(np.arange(G), (NT, G)), START[:, None] + np.arange(T + W)], axis=1)


def gl_mask(i, j):
    half = W // 2
    allowed = ((j >= i - half) & (j <= i + half)) | (j < G) | (i < G)
    return np.where(allowed, 0.0, -np.inf)


def setup_inputs():
    s = mx_kscale(S)
    s = np.roll(s, -np.argmax(s))
    q = np.random.standard_normal((B, H, S, D)) * 1.5
    k = np.random.standard_normal((B, H, S, D))
    v = np.random.standard_normal((B, H, S, D)) * 2.0
    q[..., 0] = 8.0
    k[..., 0] += np.log(s) * np.sqrt(D) / 8.0
    v *= (s.max() / s)[:, None]
    return {"q": bf(q), "k": bf(k), "v": bf(v)}


def reference(q, k, v):
    q, k, v = f64(q), f64(k), f64(v)
    scale = 1.0 / np.sqrt(D)
    vq = mxq(v, 2, "e4m3")
    sg = q[:, :, :G] @ k.transpose(0, 1, 3, 2) * scale + gl_mask(np.arange(G)[:, None], np.arange(S)[None, :])
    eg = np.exp(sg - sg.max(-1, keepdims=True))
    og = (mxq(eg, 3, "e4m3") @ vq) / eg.sum(-1, keepdims=True)
    qt = q[:, :, G:].reshape(B, H, NT, T, D)
    st = qt @ k[:, :, COLS].transpose(0, 1, 2, 4, 3) * scale + gl_mask(ROWS[:, :, None], COLS[:, None, :])
    et = np.exp(st - st.max(-1, keepdims=True))
    ot = (mxq(et, 4, "e4m3") @ vq[:, :, COLS]) / et.sum(-1, keepdims=True)
    return np.concatenate([og, ot.reshape(B, H, NT * T, D)], axis=2)

@@ -1,0 +1,435 @@
+from contextlib import ExitStack
+
+import concourse.mybir as mybir
+from concourse.masks import make_identity
+
+F32 = mybir.dt.float32
+BF16 = mybir.dt.bfloat16
+U32 = mybir.dt.uint32
+U8 = mybir.dt.uint8
+I32 = mybir.dt.int32
+FP8X4 = mybir.dt.float8_e4m3fn_x4
+ACT = mybir.ActivationFunctionType
+ALU = mybir.AluOpType
+AX = mybir.AxisListType
+
+P = 128
+H = 2
+S = 4096
+D = 256
+NCHUNK = S // P
+NSLAB = S // 512
+SCALE = 1.0 / 16.0
+NEG = -1.0e30
+FLOPS = 2 * 2 * P * 1024 * D * 70
+
+
+def slab_chunks(slab):
+    kind, n = slab
+    if kind == "L":
+        return [4 * n, 4 * n + 1, 4 * n + 2, 4 * n + 3]
+    return [4 * n + 4, 4 * n + 5, 4 * n - 2, 4 * n - 1]
+
+
+def unit_plan(g):
+    want = {}
+    for a in range(max(g - 3, 1), min(g + 3, NCHUNK - 1) + 1):
+        want[a] = "L" if a == g - 3 else ("U" if a == g + 3 else None)
+    if g <= 4:
+        want[0] = None
+    m, r = divmod(g - 1, 4)
+    if m == 0:
+        slabs = [("L", 0), ("L", 1)]
+    elif m == 7:
+        slabs = [("L", 7)] + ([("L", 6)] if r < 2 else [])
+    elif r < 2:
+        slabs = [("L", m), ("X", m)]
+    else:
+        slabs = [("L", m), ("L", m + 1)]
+    tiles = []
+    seen = []
+    for slab in slabs:
+        ent = []
+        for a in slab_chunks(slab):
+            if a in want and a not in seen:
+                ent.append((a, want[a]))
+                seen.append(a)
+            else:
+                ent.append(None)
+        tiles.append((slab, ent))
+    assert sorted(seen) == sorted(want)
+    return tiles
+
+
+def true_ranges(flags):
+    out = []
+    start = None
+    for i, f in enumerate(list(flags) + [False]):
+        if f and start is None:
+            start = i
+        if not f and start is not None:
+            out.append((start, i))
+            start = None
+    return out
+
+
+def tile_globallocalattention_t_kernel(tc, q, k, v, out):
+    nc = tc.nc
+    qf = q.flatten_outer_dims()
+    kf = k.flatten_outer_dims()
+    vf = v.flatten_outer_dims()
+    of = out.flatten_outer_dims()
+
+    with ExitStack() as ctx:
+        const = ctx.enter_context(tc.tile_pool(name="const", bufs=1))
+        raw = ctx.enter_context(tc.tile_pool(name="raw", bufs=3))
+        head = ctx.enter_context(tc.tile_pool(name="head", bufs=2))
+        fixed = ctx.enter_context(tc.tile_pool(name="fixed", bufs=1))
+        vstage = ctx.enter_context(tc.tile_pool(name="vstage", bufs=2))
+        gstage = ctx.enter_context(tc.tile_pool(name="gstage", bufs=3))
+        cpool = ctx.enter_context(tc.tile_pool(name="cpool", bufs=10))
+        opool = ctx.enter_context(tc.tile_pool(name="opool", bufs=2))
+        small = ctx.enter_context(tc.tile_pool(name="small", bufs=4))
+        ps_s = ctx.enter_context(tc.psum_pool(name="ps_s", bufs=4))
+        ps_t = ctx.enter_context(tc.psum_pool(name="ps_t", bufs=2))
+        ps_o = ctx.enter_context(tc.psum_pool(name="ps_o", bufs=2))
+
+        ident_bf = const.tile([P, P], BF16)
+        make_identity(nc, ident_bf[:])
+        ident_f = const.tile([P, P], F32)
+        make_identity(nc, ident_f[:])
+        mask_f = {}
+        mask_bf = {}
+        for kind, sign in (("U", 1), ("L", -1)):
+            mf = const.tile([P, P], F32, name="mask_f_%s" % kind)
+            nc.gpsimd.memset(mf[:], 0.0)
+            nc.gpsimd.affine_select(
+                out=mf[:], in_=mf[:], compare_op=ALU.is_ge, fill=NEG, base=0,
+                pattern=[[-sign, P]], channel_multiplier=sign,
+            )
+            mb = const.tile([P, P], BF16, name="mask_b_%s" % kind)
+            nc.vector.tensor_copy(out=mb[:], in_=mf[:])
+            mask_f[kind] = mf
+            mask_bf[kind] = mb
+
+        e_bufs = [fixed.tile([P, 2, 4, P], BF16, name="e_sb%d" % i) for i in range(8)]
+        eg_bufs = [fixed.tile([P, 4, P], BF16, name="eg_sb%d" % i) for i in range(2)]
+        is_zero = {}
+        vg_codes = fixed.tile([P, 4 * D], U32, align_bytes=64)
+        vg_scl = fixed.tile([P, 4 * D], U8, align_bytes=64)
+        tg_codes = fixed.tile([P, D], U32, align_bytes=64)
+        tg_scl = fixed.tile([P, D], U8, align_bytes=64)
+        nc.vector.memset(vg_codes[:].bitcast(I32), 0)
+        nc.vector.memset(vg_scl[:].bitcast(I32), 0)
+        nc.vector.memset(tg_scl[:].bitcast(I32), 0)
+        s_sb = fixed.tile([P, NSLAB, 4, P], F32)
+
+        hd = {}
+
+        def head_alloc(h):
+            qT = head.tile([P, S], F32, name="qT")
+            kT = head.tile([P, S], F32, name="kT")
+            vl = head.tile([P, NSLAB * D], U32, name="vl", align_bytes=64)
+            vls = head.tile([P, NSLAB * D], U8, name="vls", align_bytes=64)
+            vx = head.tile([P, 6 * D], U32, name="vx", align_bytes=64)
+            vxs = head.tile([P, 6 * D], U8, name="vxs", align_bytes=64)
+            nc.vector.memset(vls[:].bitcast(I32), 0)
+            hd[h] = {
+                "qT": qT, "kT": kT, "vl": vl, "vls": vls, "vx": vx, "vxs": vxs,
+                "qv": qT[:].bitcast(BF16).rearrange("p (r e) -> p e r", e=2),
+                "kv": kT[:].bitcast(BF16).rearrange("p (r e) -> p e r", e=2),
+            }
+
+        def regroup_quantise(v_raw, codes, scales):
+            vgrp = vstage.tile([P, 4 * D], BF16, name="vgrp", align_bytes=64)
+            nc.vector.tensor_copy(
+                out=vgrp[:].rearrange("p (d j) -> p d j", j=4),
+                in_=v_raw[:].rearrange("p (j d) -> p d j", j=4),
+            )
+            nc.vector.quantize_mx(out=codes.bitcast(FP8X4), scales=scales, in_=vgrp[:])
+
+        def setup(h, s):
+            t = hd[h]
+            r0 = h * S + 512 * s
+            q_raw = raw.tile([P, 4 * D], BF16, name="q_raw")
+            k_raw = raw.tile([P, 4 * D], BF16, name="k_raw")
+            v_raw = raw.tile([P, 4 * D], BF16, name="v_raw")
+            nc.sync.dma_start(
+                out=k_raw[:].rearrange("p (t d) -> p t d", t=4),
+                in_=kf[r0:r0 + 512, :].rearrange("(t p) d -> p t d", p=P),
+            )
+            nc.sync.dma_start(
+                out=q_raw[:].rearrange("p (t d) -> p t d", t=4),
+                in_=qf[r0:r0 + 512, :].rearrange("(t p) d -> p t d", p=P),
+            )
+            nc.sync.dma_start(
+                out=v_raw[:], in_=vf[r0:r0 + 512, :].rearrange("(p j) d -> p (j d)", j=4)
+            )
+            for src, dst, eng in ((k_raw, t["kT"], "v"), (q_raw, t["qT"], "s")):
+                ps = ps_s.tile([P, 512], F32, name="s_ps")
+                for i in range(4):
+                    nc.tensor.transpose(
+                        ps[:, P * i:P * (i + 1)], src[:].bitcast(F32)[:, P * i:P * (i + 1)], ident_f[:]
+                    )
+                if eng == "v":
+                    nc.vector.tensor_copy(out=dst[:, 512 * s:512 * (s + 1)], in_=ps[:])
+                else:
+                    nc.scalar.copy(out=dst[:, 512 * s:512 * (s + 1)], in_=ps[:])
+            regroup_quantise(v_raw, t["vl"][:, D * s:D * (s + 1)], t["vls"][:, D * s:D * (s + 1)])
+
+        def x_prep(h, m):
+            t = hd[h]
+            for lo, hi, s in ((0, 64, m + 1), (64, 128, m - 1)):
+                nc.vector.tensor_copy(
+                    out=t["vx"][lo:hi, D * (m - 1):D * m].bitcast(I32),
+                    in_=t["vl"][lo:hi, D * s:D * (s + 1)].bitcast(I32),
+                )
+                nc.vector.tensor_copy(
+                    out=t["vxs"][lo:hi, D * (m - 1):D * m].bitcast(I32),
+                    in_=t["vls"][lo:hi, D * s:D * (s + 1)].bitcast(I32),
+                )
+
+        def vg_prep(h):
+            g_raw = raw.tile([P, 4 * D], BF16, name="v_raw")
+            for qd in range(4):
+                nc.sync.dma_start(
+                    out=g_raw[32 * qd:32 * (qd + 1), :],
+                    in_=vf[h * S:h * S + P, :].rearrange("(p j) d -> p (j d)", j=4),
+                )
+            regroup_quantise(g_raw, tg_codes[:], tg_scl[:])
+            for u in range(4):
+                nc.vector.tensor_copy(
+                    out=vg_codes[32 * u:32 * (u + 1), D * u:D * (u + 1)].bitcast(I32),
+                    in_=tg_codes[32 * u:32 * (u + 1), :].bitcast(I32),
+                )
+                nc.vector.tensor_copy(
+                    out=vg_scl[32 * u:32 * (u + 1), D * u:D * (u + 1)].bitcast(I32),
+                    in_=tg_scl[32 * u:32 * (u + 1), :].bitcast(I32),
+                )
+
+        def qk_bank(h, g, chunks, masks):
+            t = hd[h]
+            ps = ps_s.tile([P, 512], F32, name="s_ps")
+            runs = []
+            for qd in range(4):
+                a = chunks[qd]
+                if a is None:
+                    continue
+                if runs and runs[-1][0] + runs[-1][1] == qd and runs[-1][2] + runs[-1][1] == a:
+                    runs[-1][1] += 1
+                else:
+                    runs.append([qd, 1, a])
+            for q0, n, a0 in runs:
+                dst = ps[:, P * q0:P * (q0 + n)]
+                nc.tensor.matmul(
+                    out=dst, lhsT=t["qv"][:, 0, P * g:P * (g + 1)], rhs=t["kv"][:, 0, P * a0:P * (a0 + n)],
+                    start=True, stop=False,
+                )
+                for qd in range(q0, q0 + n):
+                    if masks[qd] is not None:
+                        nc.tensor.matmul(
+                            out=ps[:, P * qd:P * (qd + 1)], lhsT=ident_bf[:], rhs=mask_bf[masks[qd]][:],
+                            start=False, stop=False,
+                        )
+                nc.tensor.matmul(
+                    out=dst, lhsT=t["qv"][:, 1, P * g:P * (g + 1)], rhs=t["kv"][:, 1, P * a0:P * (a0 + n)],
+                    start=False, stop=True,
+                )
+            return ps
+
+        def to_codes(e_view, nt, eng):
+            eT = ps_t.tile([P, 2, 4, P], BF16, name="eT")
+            for ti in range(nt):
+                for j in range(4):
+                    nc.tensor.transpose(eT[:, ti, j, :], e_view(ti, j), ident_bf[:])
+            grp = gstage.tile([P, 2, P, 4], BF16, name="grp", align_bytes=64)
+            src = eT[:, 0:nt].rearrange("p t j q -> p t q j")
+            if eng == "v":
+                nc.vector.tensor_copy(out=grp[:, 0:nt], in_=src)
+            else:
+                nc.scalar.copy(out=grp[:, 0:nt], in_=src)
+            codes = cpool.tile([P, 2 * P], U32, name="codes", align_bytes=64)
+            scl = cpool.tile([P, 2 * P], U8, name="scl", align_bytes=64)
+            nc.vector.quantize_mx(
+                out=codes[:, 0:nt * P].bitcast(FP8X4), scales=scl[:, 0:nt * P],
+                in_=grp[:, 0:nt].rearrange("p t q j -> p (t q j)"),
+            )
+            return codes, scl
+
+        def v_operand(h, slab):
+            t = hd[h]
+            kind, n = slab
+            if kind == "L":
+                return t["vl"][:, D * n:D * (n + 1)], t["vls"][:, D * n:D * (n + 1)]
+            if kind == "X":
+                return t["vx"][:, D * (n - 1):D * n], t["vxs"][:, D * (n - 1):D * n]
+            return vg_codes[:, D * n:D * (n + 1)], vg_scl[:, D * n:D * (n + 1)]
+
+        def mx_group(h, dst, passes):
+            for i, (codes, scl, ti, slab) in enumerate(passes):
+                vc, vs = v_operand(h, slab)
+                nc.tensor.matmul_mx(
+                    out=dst,
+                    lhsT=codes[:, P * ti:P * (ti + 1)].bitcast(FP8X4), lhsT_scale=scl[:, P * ti:P * (ti + 1)],
+                    rhs=vc.bitcast(FP8X4), rhs_scale=vs,
+                    start=(i == 0), stop=(i == len(passes) - 1),
+                )
+
+        def super_unit(h, m):
+            groups = [g for g in range(4 * m + 1, 4 * m + 5) if g < NCHUNK]
+            nu = len(groups)
+            acc = small.tile([P, 4, 4], F32, name="acc")
+            nc.vector.memset(acc[:], 0.0)
+            eg = eg_bufs[m % 2]
+            passes = []
+            for u, g in enumerate(groups):
+                tiles = unit_plan(g)
+                bi = 4 * (m % 2) + u
+                e_sb = e_bufs[bi]
+                layout = [[(en[0] if en is not None else None) for en in ent] for slab, ent in tiles]
+                msk = [[(en[1] if en is not None else None) for en in ent] for slab, ent in tiles]
+                g_slot = None
+                if g >= 5:
+                    for ti in range(len(layout)):
+                        for qd in range(4):
+                            if g_slot is None and layout[ti][qd] is None:
+                                g_slot = (ti, qd)
+                    if g_slot is None:
+                        layout.append([None, None, None, None])
+                        msk.append([None, None, None, None])
+                        g_slot = (len(layout) - 1, 0)
+                    layout[g_slot[0]][g_slot[1]] = 0
+                banks = [qk_bank(h, g, layout[ti], msk[ti]) for ti in range(len(layout))]
+                pieces = []
+                for ti in range(len(layout)):
+                    for q0, q1 in true_ranges([a is not None for a in layout[ti]]):
+                        pieces.append((ti, q0, q1))
+                mx = small.tile([P, 8], F32, name="mx")
+                for i, (ti, q0, q1) in enumerate(pieces):
+                    nc.vector.tensor_reduce(
+                        out=mx[:, i:i + 1], in_=banks[ti][:, P * q0:P * q1], axis=AX.X, op=ALU.max
+                    )
+                negm = small.tile([P, 1], F32, name="negm")
+                if len(pieces) == 2:
+                    nc.vector.tensor_scalar(
+                        out=negm[:], in0=mx[:, 0:1], scalar1=mx[:, 1:2], scalar2=-SCALE,
+                        op0=ALU.max, op1=ALU.mult,
+                    )
+                else:
+                    mx1 = small.tile([P, 1], F32, name="mx1")
+                    nc.vector.tensor_reduce(out=mx1[:], in_=mx[:, 0:len(pieces)], axis=AX.X, op=ALU.max)
+                    nc.vector.tensor_scalar(
+                        out=negm[:], in0=mx1[:], scalar1=-SCALE, scalar2=None, op0=ALU.mult
+                    )
+                n_acc = 0
+                for ti, (slab, ent) in enumerate(tiles):
+                    for qd in range(4):
+                        if ent[qd] is None:
+                            if not is_zero.get((bi, ti, qd), False):
+                                nc.gpsimd.memset(e_sb[:, ti, :, 32 * qd:32 * (qd + 1)], 0.0)
+                                is_zero[(bi, ti, qd)] = True
+                        else:
+                            is_zero[(bi, ti, qd)] = False
+                    for q0, q1 in true_ranges([en is not None for en in ent]):
+                        nc.scalar.activation(
+                            out=e_sb[:, ti, :, 32 * q0:32 * q1],
+                            in_=banks[ti][:, P * q0:P * q1].rearrange("q (p j) -> q j p", j=4),
+                            func=ACT.Exp, bias=negm[:, 0:1], scale=SCALE,
+                            accum_out=acc[:, u, n_acc:n_acc + 1],
+                        )
+                        n_acc += 1
+                if g_slot is not None:
+                    ti, qd = g_slot
+                    nc.scalar.activation(
+                        out=eg[:, :, 32 * u:32 * (u + 1)],
+                        in_=banks[ti][:, P * qd:P * (qd + 1)].rearrange("q (p j) -> q j p", j=4),
+                        func=ACT.Exp, bias=negm[:, 0:1], scale=SCALE,
+                        accum_out=acc[:, u, n_acc:n_acc + 1],
+                    )
+                    n_acc += 1
+                assert n_acc <= 4
+                codes, scl = to_codes(
+                    lambda ti, j, e_sb=e_sb: e_sb[:, ti, j, :], len(tiles), "v" if u % 2 == 0 else "s"
+                )
+                passes.append([(codes, scl, ti, tiles[ti][0]) for ti in range(len(tiles))])
+            if m >= 1:
+                codes, scl = to_codes(lambda ti, j: eg[:, j, :], 1, "v")
+                for u in range(nu):
+                    passes[u].append((codes, scl, 0, ("G", u)))
+            tot = small.tile([P, 4], F32, name="tot")
+            nc.vector.tensor_reduce(out=tot[:, 0:nu], in_=acc[:, 0:nu, :], axis=AX.X, op=ALU.add)
+            rinv = small.tile([P, 4], F32, name="rinv")
+            nc.vector.reciprocal(out=rinv[:, 0:nu], in_=tot[:, 0:nu])
+            o_sb = opool.tile([P, 4, D], F32, name="o_sb")
+            o_ps = None
+            for u in range(nu):
+                if u % 2 == 0:
+                    o_ps = ps_o.tile([P, 2, D], F32, name="o_ps")
+                mx_group(h, o_ps[:, u % 2, :], passes[u])
+                nc.scalar.activation(
+                    out=o_sb[:, u, :], in_=o_ps[:, u % 2, :], func=ACT.Copy, scale=rinv[:, u:u + 1]
+                )
+            r0 = h * S + P * groups[0]
+            nc.scalar.dma_start(
+                out=of[r0:r0 + P * nu, :].rearrange("(u p) d -> p u d", p=P), in_=o_sb[:, 0:nu, :]
+            )
+
+        gl = {}
+
+        def global_scores(h, s):
+            if s == 0:
+                gl["mx"] = small.tile([P, NSLAB], F32, name="gmx")
+            ps = qk_bank(h, 0, [4 * s, 4 * s + 1, 4 * s + 2, 4 * s + 3], [None] * 4)
+            nc.vector.tensor_scalar(
+                out=s_sb[:, s], in0=ps[:].rearrange("q (p j) -> q j p", j=4),
+                scalar1=-SCALE, scalar2=None, op0=ALU.mult, op1=ALU.min,
+                accum_out=gl["mx"][:, s:s + 1],
+            )
+
+        def global_finish(h):
+            negm = small.tile([P, 1], F32, name="negm")
+            nc.vector.tensor_reduce(out=negm[:], in_=gl["mx"][:], axis=AX.X, op=ALU.min)
+            acc = small.tile([P, NSLAB], F32, name="gacc")
+            passes = []
+            for i in range(NSLAB // 2):
+                e_sb = e_bufs[i]
+                for ti in range(2):
+                    s = 2 * i + ti
+                    for qd in range(4):
+                        is_zero[(i, ti, qd)] = False
+                    nc.scalar.activation(
+                        out=e_sb[:, ti], in_=s_sb[:, s], func=ACT.Exp, bias=negm[:, 0:1], scale=-1.0,
+                        accum_out=acc[:, s:s + 1],
+                    )
+                codes, scl = to_codes(
+                    lambda ti, j, e_sb=e_sb: e_sb[:, ti, j, :], 2, "v" if i % 2 == 0 else "s"
+                )
+                passes.extend([(codes, scl, ti, ("L", 2 * i + ti)) for ti in range(2)])
+            tot = small.tile([P, 4], F32, name="tot")
+            nc.vector.tensor_reduce(out=tot[:, 0:1], in_=acc[:], axis=AX.X, op=ALU.add)
+            rinv = small.tile([P, 4], F32, name="rinv")
+            nc.vector.reciprocal(out=rinv[:, 0:1], in_=tot[:, 0:1])
+            o_ps = ps_o.tile([P, 2, D], F32, name="o_ps")
+            mx_group(h, o_ps[:, 0, :], passes)
+            o_sb = opool.tile([P, 4, D], F32, name="o_sb")
+            nc.scalar.activation(out=o_sb[:, 0, :], in_=o_ps[:, 0, :], func=ACT.Copy, scale=rinv[:, 0:1])
+            nc.scalar.dma_start(out=of[h * S:h * S + P, :], in_=o_sb[:, 0, :])
+
+        def head_start(h):
+            head_alloc(h)
+            setup(h, 0)
+            setup(h, 1)
+
+        head_start(0)
+        for h in range(H):
+            vg_prep(h)
+            for m in range(NSLAB):
+                if m + 2 < NSLAB:
+                    setup(h, m + 2)
+                if 1 <= m + 1 <= 6:
+                    x_prep(h, m + 1)
+                super_unit(h, m)
+                global_scores(h, m)
+            if h + 1 < H:
+                head_start(h + 1)
+            global_finish(h)

@@ -87,6 +87,7 @@ def tile_globallocalattention_t_kernel(tc, q, k, v, out):
         fixed = ctx.enter_context(tc.tile_pool(name="fixed", bufs=1))
         vstage = ctx.enter_context(tc.tile_pool(name="vstage", bufs=2))
         gstage = ctx.enter_context(tc.tile_pool(name="gstage", bufs=3))
+        sstage = ctx.enter_context(tc.tile_pool(name="sstage", bufs=4))
         cpool = ctx.enter_context(tc.tile_pool(name="cpool", bufs=10))
         opool = ctx.enter_context(tc.tile_pool(name="opool", bufs=2))
         small = ctx.enter_context(tc.tile_pool(name="small", bufs=4))
@@ -142,9 +143,10 @@ def tile_globallocalattention_t_kernel(tc, q, k, v, out):
 
         def regroup_quantise(v_raw, codes, scales):
             vgrp = vstage.tile([P, 4 * D], BF16, name="vgrp", align_bytes=64)
-            nc.vector.tensor_copy(
+            nc.gpsimd.tensor_scalar(
                 out=vgrp[:].rearrange("p (d j) -> p d j", j=4),
-                in_=v_raw[:].rearrange("p (j d) -> p d j", j=4),
+                in0=v_raw[:].rearrange("p (j d) -> p d j", j=4),
+                scalar1=1.0, scalar2=0.0, op0=ALU.mult, op1=ALU.add,
             )
             nc.vector.quantize_mx(out=codes.bitcast(FP8X4), scales=scales, in_=vgrp[:])
 
@@ -305,22 +307,19 @@ def tile_globallocalattention_t_kernel(tc, q, k, v, out):
                     for q0, q1 in true_ranges([a is not None for a in layout[ti]]):
                         pieces.append((ti, q0, q1))
                 mx = small.tile([P, 8], F32, name="mx")
+                s_u = sstage.tile([P, 2, 4, P], F32, name="s_u")
                 for i, (ti, q0, q1) in enumerate(pieces):
-                    nc.vector.tensor_reduce(
-                        out=mx[:, i:i + 1], in_=banks[ti][:, P * q0:P * q1], axis=AX.X, op=ALU.max
+                    nc.vector.tensor_scalar(
+                        out=s_u[:, ti, :, 32 * q0:32 * q1],
+                        in0=banks[ti][:, P * q0:P * q1].rearrange("q (p j) -> q j p", j=4),
+                        scalar1=-SCALE, scalar2=None, op0=ALU.mult, op1=ALU.min,
+                        accum_out=mx[:, i:i + 1],
                     )
                 negm = small.tile([P, 1], F32, name="negm")
                 if len(pieces) == 2:
-                    nc.vector.tensor_scalar(
-                        out=negm[:], in0=mx[:, 0:1], scalar1=mx[:, 1:2], scalar2=-SCALE,
-                        op0=ALU.max, op1=ALU.mult,
-                    )
+                    nc.vector.tensor_tensor(out=negm[:], in0=mx[:, 0:1], in1=mx[:, 1:2], op=ALU.min)
                 else:
-                    mx1 = small.tile([P, 1], F32, name="mx1")
-                    nc.vector.tensor_reduce(out=mx1[:], in_=mx[:, 0:len(pieces)], axis=AX.X, op=ALU.max)
-                    nc.vector.tensor_scalar(
-                        out=negm[:], in0=mx1[:], scalar1=-SCALE, scalar2=None, op0=ALU.mult
-                    )
+                    nc.vector.tensor_reduce(out=negm[:], in_=mx[:, 0:len(pieces)], axis=AX.X, op=ALU.min)
                 n_acc = 0
                 for ti, (slab, ent) in enumerate(tiles):
                     for qd in range(4):
@@ -333,8 +332,8 @@ def tile_globallocalattention_t_kernel(tc, q, k, v, out):
                     for q0, q1 in true_ranges([en is not None for en in ent]):
                         nc.scalar.activation(
                             out=e_sb[:, ti, :, 32 * q0:32 * q1],
-                            in_=banks[ti][:, P * q0:P * q1].rearrange("q (p j) -> q j p", j=4),
-                            func=ACT.Exp, bias=negm[:, 0:1], scale=SCALE,
+                            in_=s_u[:, ti, :, 32 * q0:32 * q1],
+                            func=ACT.Exp, bias=negm[:, 0:1], scale=-1.0,
                             accum_out=acc[:, u, n_acc:n_acc + 1],
                         )
                         n_acc += 1
@@ -342,8 +341,8 @@ def tile_globallocalattention_t_kernel(tc, q, k, v, out):
                     ti, qd = g_slot
                     nc.scalar.activation(
                         out=eg[:, :, 32 * u:32 * (u + 1)],
-                        in_=banks[ti][:, P * qd:P * (qd + 1)].rearrange("q (p j) -> q j p", j=4),
-                        func=ACT.Exp, bias=negm[:, 0:1], scale=SCALE,
+                        in_=s_u[:, ti, :, 32 * qd:32 * (qd + 1)],
+                        func=ACT.Exp, bias=negm[:, 0:1], scale=-1.0,
                         accum_out=acc[:, u, n_acc:n_acc + 1],
                     )
                     n_acc += 1

@@ -21,44 +21,58 @@ NCHUNK = S // P
 NSLAB = S // 512
 SCALE = 1.0 / 16.0
 NEG = -1.0e30
+VW = D + D // 4
 FLOPS = 2 * 2 * P * 1024 * D * 70
 
-
-def slab_chunks(slab):
-    kind, n = slab
-    if kind == "L":
-        return [4 * n, 4 * n + 1, 4 * n + 2, 4 * n + 3]
-    return [4 * n + 4, 4 * n + 5, 4 * n - 2, 4 * n - 1]
+PINNED = False
+COPY_ON_VECTOR = (0, 3, 6)
+LOAD_AHEAD = 6
 
 
 def unit_plan(g):
     want = {}
     for a in range(max(g - 3, 1), min(g + 3, NCHUNK - 1) + 1):
         want[a] = "L" if a == g - 3 else ("U" if a == g + 3 else None)
-    if g <= 4:
-        want[0] = None
+    want[0] = None
     m, r = divmod(g - 1, 4)
+    nat = lambda n: [4 * n, 4 * n + 1, 4 * n + 2, 4 * n + 3]
     if m == 0:
-        slabs = [("L", 0), ("L", 1)]
+        slabs = [(("L", 0), nat(0)), (("L", 1), nat(1))]
     elif m == 7:
-        slabs = [("L", 7)] + ([("L", 6)] if r < 2 else [])
-    elif r < 2:
-        slabs = [("L", m), ("X", m)]
+        if r < 2:
+            slabs = [(("L", 7), nat(7)), (("V", 0), [0, 25, 26, 27])]
+        else:
+            slabs = [(("L", 7), nat(7)), (("L", 0), nat(0))]
+    elif r == 0:
+        slabs = [(("L", m), nat(m)), (("V", 0), [4 * m + 4, 0, 4 * m - 2, 4 * m - 1])]
+    elif r == 1:
+        slabs = [(("L", m), nat(m)), (("V", 1), [4 * m + 4, 4 * m + 5, 0, 4 * m - 1])]
+    elif r == 2:
+        slabs = [(("L", m), nat(m)), (("V", 2), [4 * m + 4, 4 * m + 5, 4 * m + 6, 0])]
     else:
-        slabs = [("L", m), ("L", m + 1)]
+        slabs = [(("V", 3), [0, 4 * m + 1, 4 * m + 2, 4 * m + 3]), (("L", m + 1), nat(m + 1))]
     tiles = []
     seen = []
-    for slab in slabs:
+    for slab, chunks in slabs:
         ent = []
-        for a in slab_chunks(slab):
+        for a in chunks:
             if a in want and a not in seen:
                 ent.append((a, want[a]))
                 seen.append(a)
             else:
                 ent.append(None)
-        tiles.append((slab, ent))
+        tiles.append((slab, chunks, ent))
     assert sorted(seen) == sorted(want)
     return tiles
+
+
+def variant_slabs(m):
+    out = {}
+    for g in range(4 * m + 1, min(4 * m + 5, NCHUNK)):
+        for slab, chunks, ent in unit_plan(g):
+            if slab[0] == "V":
+                out[slab[1]] = chunks
+    return out
 
 
 def true_ranges(flags):
@@ -73,6 +87,40 @@ def true_ranges(flags):
     return out
 
 
+def build_items():
+    seq = [{"kind": "kq", "h": 0, "s": 0}, {"kind": "kq", "h": 0, "s": 1}, {"kind": "nop"}]
+    for h in range(H):
+        for m in range(NSLAB):
+            units = [{"kind": "unit", "h": h, "g": g} for g in range(4 * m + 1, min(4 * m + 5, NCHUNK))]
+            extra = []
+            if h == 0:
+                if m + 2 < NSLAB:
+                    extra.append({"kind": "kq", "h": 0, "s": m + 2})
+                else:
+                    extra.append({"kind": "kq", "h": 1, "s": m + 2 - NSLAB})
+                extra.append({"kind": "gs", "h": 0, "s": m})
+            else:
+                for s in (2 * m + 2, 2 * m + 3):
+                    if s < NSLAB:
+                        extra.append({"kind": "kq", "h": 1, "s": s})
+                if m < 2:
+                    extra.extend([{"kind": "gf", "h": 0, "i": 2 * m}, {"kind": "gf", "h": 0, "i": 2 * m + 1}])
+                if 2 <= m <= 5:
+                    extra.extend([{"kind": "gs", "h": 1, "s": 2 * m - 4}, {"kind": "gs", "h": 1, "s": 2 * m - 3}])
+                if m == 6:
+                    extra.extend([{"kind": "gf", "h": 1, "i": i} for i in range(4)])
+            merged = []
+            for i in range(max(len(units), len(extra))):
+                if i < len(units):
+                    merged.append(units[i])
+                if i < len(extra):
+                    merged.append(extra[i])
+            if m + 1 < NSLAB:
+                merged[-1]["variants"] = (h, m + 1)
+            seq.extend(merged)
+    return seq
+
+
 def tile_globallocalattention_t_kernel(tc, q, k, v, out):
     nc = tc.nc
     qf = q.flatten_outer_dims()
@@ -82,15 +130,16 @@ def tile_globallocalattention_t_kernel(tc, q, k, v, out):
 
     with ExitStack() as ctx:
         const = ctx.enter_context(tc.tile_pool(name="const", bufs=1))
-        raw = ctx.enter_context(tc.tile_pool(name="raw", bufs=3))
+        raw = ctx.enter_context(tc.tile_pool(name="raw", bufs=4))
         head = ctx.enter_context(tc.tile_pool(name="head", bufs=2))
         fixed = ctx.enter_context(tc.tile_pool(name="fixed", bufs=1))
         vstage = ctx.enter_context(tc.tile_pool(name="vstage", bufs=2))
+        vvpool = ctx.enter_context(tc.tile_pool(name="vvpool", bufs=3))
         gstage = ctx.enter_context(tc.tile_pool(name="gstage", bufs=3))
         sstage = ctx.enter_context(tc.tile_pool(name="sstage", bufs=4))
-        cpool = ctx.enter_context(tc.tile_pool(name="cpool", bufs=10))
-        opool = ctx.enter_context(tc.tile_pool(name="opool", bufs=2))
-        small = ctx.enter_context(tc.tile_pool(name="small", bufs=4))
+        cpool = ctx.enter_context(tc.tile_pool(name="cpool", bufs=8))
+        opool = ctx.enter_context(tc.tile_pool(name="opool", bufs=3))
+        small = ctx.enter_context(tc.tile_pool(name="small", bufs=8))
         ps_s = ctx.enter_context(tc.psum_pool(name="ps_s", bufs=4))
         ps_t = ctx.enter_context(tc.psum_pool(name="ps_t", bufs=2))
         ps_o = ctx.enter_context(tc.psum_pool(name="ps_o", bufs=2))
@@ -99,7 +148,6 @@ def tile_globallocalattention_t_kernel(tc, q, k, v, out):
         make_identity(nc, ident_bf[:])
         ident_f = const.tile([P, P], F32)
         make_identity(nc, ident_f[:])
-        mask_f = {}
         mask_bf = {}
         for kind, sign in (("U", 1), ("L", -1)):
             mf = const.tile([P, P], F32, name="mask_f_%s" % kind)
@@ -110,108 +158,92 @@ def tile_globallocalattention_t_kernel(tc, q, k, v, out):
             )
             mb = const.tile([P, P], BF16, name="mask_b_%s" % kind)
             nc.vector.tensor_copy(out=mb[:], in_=mf[:])
-            mask_f[kind] = mf
             mask_bf[kind] = mb
 
         e_bufs = [fixed.tile([P, 2, 4, P], BF16, name="e_sb%d" % i) for i in range(8)]
-        eg_bufs = [fixed.tile([P, 4, P], BF16, name="eg_sb%d" % i) for i in range(2)]
         is_zero = {}
-        vg_codes = fixed.tile([P, 4 * D], U32, align_bytes=64)
-        vg_scl = fixed.tile([P, 4 * D], U8, align_bytes=64)
-        tg_codes = fixed.tile([P, D], U32, align_bytes=64)
-        tg_scl = fixed.tile([P, D], U8, align_bytes=64)
-        nc.vector.memset(vg_codes[:].bitcast(I32), 0)
-        nc.vector.memset(vg_scl[:].bitcast(I32), 0)
-        nc.vector.memset(tg_scl[:].bitcast(I32), 0)
         s_sb = fixed.tile([P, NSLAB, 4, P], F32)
-
         hd = {}
+        vv = {}
+        gl = {}
 
         def head_alloc(h):
             qT = head.tile([P, S], F32, name="qT")
             kT = head.tile([P, S], F32, name="kT")
-            vl = head.tile([P, NSLAB * D], U32, name="vl", align_bytes=64)
-            vls = head.tile([P, NSLAB * D], U8, name="vls", align_bytes=64)
-            vx = head.tile([P, 6 * D], U32, name="vx", align_bytes=64)
-            vxs = head.tile([P, 6 * D], U8, name="vxs", align_bytes=64)
-            nc.vector.memset(vls[:].bitcast(I32), 0)
+            vl = head.tile([P, NSLAB * VW], U32, name="vl", align_bytes=64)
+            nc.vector.memset(vl[:].bitcast(I32).rearrange("p (s w) -> p s w", w=VW)[:, :, D:VW], 0)
             hd[h] = {
-                "qT": qT, "kT": kT, "vl": vl, "vls": vls, "vx": vx, "vxs": vxs,
+                "qT": qT, "kT": kT, "vl": vl,
                 "qv": qT[:].bitcast(BF16).rearrange("p (r e) -> p e r", e=2),
                 "kv": kT[:].bitcast(BF16).rearrange("p (r e) -> p e r", e=2),
             }
 
-        def regroup_quantise(v_raw, codes, scales):
-            vgrp = vstage.tile([P, 4 * D], BF16, name="vgrp", align_bytes=64)
-            nc.gpsimd.tensor_scalar(
-                out=vgrp[:].rearrange("p (d j) -> p d j", j=4),
-                in0=v_raw[:].rearrange("p (j d) -> p d j", j=4),
-                scalar1=1.0, scalar2=0.0, op0=ALU.mult, op1=ALU.add,
-            )
-            nc.vector.quantize_mx(out=codes.bitcast(FP8X4), scales=scales, in_=vgrp[:])
-
-        def setup(h, s):
-            t = hd[h]
+        def kq_load(it):
+            h, s = it["h"], it["s"]
+            if s == 0:
+                head_alloc(h)
             r0 = h * S + 512 * s
-            q_raw = raw.tile([P, 4 * D], BF16, name="q_raw")
-            k_raw = raw.tile([P, 4 * D], BF16, name="k_raw")
-            v_raw = raw.tile([P, 4 * D], BF16, name="v_raw")
+            it["k_raw"] = raw.tile([P, 4 * D], BF16, name="k_raw")
+            it["q_raw"] = raw.tile([P, 4 * D], BF16, name="q_raw")
+            it["v_raw"] = raw.tile([P, 4 * D], BF16, name="v_raw")
             nc.sync.dma_start(
-                out=k_raw[:].rearrange("p (t d) -> p t d", t=4),
+                out=it["k_raw"][:].rearrange("p (t d) -> p t d", t=4),
                 in_=kf[r0:r0 + 512, :].rearrange("(t p) d -> p t d", p=P),
             )
             nc.sync.dma_start(
-                out=q_raw[:].rearrange("p (t d) -> p t d", t=4),
+                out=it["q_raw"][:].rearrange("p (t d) -> p t d", t=4),
                 in_=qf[r0:r0 + 512, :].rearrange("(t p) d -> p t d", p=P),
             )
             nc.sync.dma_start(
-                out=v_raw[:], in_=vf[r0:r0 + 512, :].rearrange("(p j) d -> p (j d)", j=4)
+                out=it["v_raw"][:], in_=vf[r0:r0 + 512, :].rearrange("(p j) d -> p (j d)", j=4)
             )
-            for src, dst, eng in ((k_raw, t["kT"], "v"), (q_raw, t["qT"], "s")):
+
+        def kq_transpose(it):
+            it["banks"] = []
+            for src in (it["k_raw"], it["q_raw"]):
                 ps = ps_s.tile([P, 512], F32, name="s_ps")
                 for i in range(4):
                     nc.tensor.transpose(
                         ps[:, P * i:P * (i + 1)], src[:].bitcast(F32)[:, P * i:P * (i + 1)], ident_f[:]
                     )
-                if eng == "v":
-                    nc.vector.tensor_copy(out=dst[:, 512 * s:512 * (s + 1)], in_=ps[:])
-                else:
-                    nc.scalar.copy(out=dst[:, 512 * s:512 * (s + 1)], in_=ps[:])
-            regroup_quantise(v_raw, t["vl"][:, D * s:D * (s + 1)], t["vls"][:, D * s:D * (s + 1)])
+                it["banks"].append(ps)
 
-        def x_prep(h, m):
-            t = hd[h]
-            for lo, hi, s in ((0, 64, m + 1), (64, 128, m - 1)):
-                nc.vector.tensor_copy(
-                    out=t["vx"][lo:hi, D * (m - 1):D * m].bitcast(I32),
-                    in_=t["vl"][lo:hi, D * s:D * (s + 1)].bitcast(I32),
-                )
-                nc.vector.tensor_copy(
-                    out=t["vxs"][lo:hi, D * (m - 1):D * m].bitcast(I32),
-                    in_=t["vls"][lo:hi, D * s:D * (s + 1)].bitcast(I32),
-                )
+        def kq_regroup(it):
+            vgrp = vstage.tile([P, 4 * D], BF16, name="vgrp", align_bytes=64)
+            nc.gpsimd.tensor_scalar(
+                out=vgrp[:].rearrange("p (d j) -> p d j", j=4),
+                in0=it["v_raw"][:].rearrange("p (j d) -> p d j", j=4),
+                scalar1=1.0, scalar2=0.0, op0=ALU.mult, op1=ALU.add,
+            )
+            it["vgrp"] = vgrp
 
-        def vg_prep(h):
-            g_raw = raw.tile([P, 4 * D], BF16, name="v_raw")
-            for qd in range(4):
-                nc.sync.dma_start(
-                    out=g_raw[32 * qd:32 * (qd + 1), :],
-                    in_=vf[h * S:h * S + P, :].rearrange("(p j) d -> p (j d)", j=4),
-                )
-            regroup_quantise(g_raw, tg_codes[:], tg_scl[:])
-            for u in range(4):
-                nc.vector.tensor_copy(
-                    out=vg_codes[32 * u:32 * (u + 1), D * u:D * (u + 1)].bitcast(I32),
-                    in_=tg_codes[32 * u:32 * (u + 1), :].bitcast(I32),
-                )
-                nc.vector.tensor_copy(
-                    out=vg_scl[32 * u:32 * (u + 1), D * u:D * (u + 1)].bitcast(I32),
-                    in_=tg_scl[32 * u:32 * (u + 1), :].bitcast(I32),
-                )
+        def v_slab(h, slab, m):
+            kind, n = slab
+            t = hd[h]["vl"] if kind == "L" else vv[(h, m)]
+            return t[:, VW * n:VW * n + D], t[:, VW * n + D:VW * (n + 1)].bitcast(U8)
 
-        def qk_bank(h, g, chunks, masks):
-            t = hd[h]
-            ps = ps_s.tile([P, 512], F32, name="s_ps")
+        def kq_vquant(it):
+            codes, scales = v_slab(it["h"], ("L", it["s"]), None)
+            nc.vector.quantize_mx(out=codes.bitcast(FP8X4), scales=scales, in_=it["vgrp"][:])
+
+        def build_variants(h, m):
+            t = vvpool.tile([P, 4 * VW], U32, name="vvar", align_bytes=64)
+            vv[(h, m)] = t
+            vl = hd[h]["vl"]
+            for slot, chunks in sorted(variant_slabs(m).items()):
+                pieces = []
+                for qd, a in enumerate(chunks):
+                    if pieces and a != 0 and pieces[-1][2] == a // 4 and pieces[-1][3] + pieces[-1][1] == a % 4:
+                        pieces[-1][1] += 1
+                    else:
+                        pieces.append([qd, 1, a // 4, a % 4])
+                for q0, n, s, sq in pieces:
+                    nc.sync.dma_start(
+                        out=t[32 * q0:32 * (q0 + n), VW * slot:VW * (slot + 1)].bitcast(I32),
+                        in_=vl[32 * sq:32 * (sq + n), VW * s:VW * (s + 1)].bitcast(I32),
+                    )
+
+        def qk_runs(chunks):
             runs = []
             for qd in range(4):
                 a = chunks[qd]
@@ -221,7 +253,12 @@ def tile_globallocalattention_t_kernel(tc, q, k, v, out):
                     runs[-1][1] += 1
                 else:
                     runs.append([qd, 1, a])
-            for q0, n, a0 in runs:
+            return runs
+
+        def qk_bank(h, g, chunks, masks):
+            t = hd[h]
+            ps = ps_s.tile([P, 512], F32, name="s_ps")
+            for q0, n, a0 in qk_runs(chunks):
                 dst = ps[:, P * q0:P * (q0 + n)]
                 nc.tensor.matmul(
                     out=dst, lhsT=t["qv"][:, 0, P * g:P * (g + 1)], rhs=t["kv"][:, 0, P * a0:P * (a0 + n)],
@@ -239,196 +276,241 @@ def tile_globallocalattention_t_kernel(tc, q, k, v, out):
                 )
             return ps
 
-        def to_codes(e_view, nt, eng):
-            eT = ps_t.tile([P, 2, 4, P], BF16, name="eT")
-            for ti in range(nt):
-                for j in range(4):
-                    nc.tensor.transpose(eT[:, ti, j, :], e_view(ti, j), ident_bf[:])
-            grp = gstage.tile([P, 2, P, 4], BF16, name="grp", align_bytes=64)
-            src = eT[:, 0:nt].rearrange("p t j q -> p t q j")
-            if eng == "v":
-                nc.vector.tensor_copy(out=grp[:, 0:nt], in_=src)
-            else:
-                nc.scalar.copy(out=grp[:, 0:nt], in_=src)
-            codes = cpool.tile([P, 2 * P], U32, name="codes", align_bytes=64)
-            scl = cpool.tile([P, 2 * P], U8, name="scl", align_bytes=64)
-            nc.vector.quantize_mx(
-                out=codes[:, 0:nt * P].bitcast(FP8X4), scales=scl[:, 0:nt * P],
-                in_=grp[:, 0:nt].rearrange("p t q j -> p (t q j)"),
-            )
-            return codes, scl
-
-        def v_operand(h, slab):
-            t = hd[h]
-            kind, n = slab
-            if kind == "L":
-                return t["vl"][:, D * n:D * (n + 1)], t["vls"][:, D * n:D * (n + 1)]
-            if kind == "X":
-                return t["vx"][:, D * (n - 1):D * n], t["vxs"][:, D * (n - 1):D * n]
-            return vg_codes[:, D * n:D * (n + 1)], vg_scl[:, D * n:D * (n + 1)]
-
-        def mx_group(h, dst, passes):
-            for i, (codes, scl, ti, slab) in enumerate(passes):
-                vc, vs = v_operand(h, slab)
-                nc.tensor.matmul_mx(
-                    out=dst,
-                    lhsT=codes[:, P * ti:P * (ti + 1)].bitcast(FP8X4), lhsT_scale=scl[:, P * ti:P * (ti + 1)],
-                    rhs=vc.bitcast(FP8X4), rhs_scale=vs,
-                    start=(i == 0), stop=(i == len(passes) - 1),
+        def unit_pass(it):
+            pieces = []
+            for ti, (slab, chunks, ent) in enumerate(it["tiles"]):
+                for q0, q1 in true_ranges([en is not None for en in ent]):
+                    pieces.append((ti, q0, q1))
+            mn = small.tile([P, 8], F32, name="mn")
+            s_u = sstage.tile([P, 2, 4, P], F32, name="s_u")
+            for i, (ti, q0, q1) in enumerate(pieces):
+                nc.vector.tensor_scalar(
+                    out=s_u[:, ti, :, 32 * q0:32 * q1],
+                    in0=it["banks"][ti][:, P * q0:P * q1].rearrange("q (p j) -> q j p", j=4),
+                    scalar1=-SCALE, scalar2=None, op0=ALU.mult, op1=ALU.min,
+                    accum_out=mn[:, i:i + 1],
                 )
+            it["mn"] = mn
+            it["n_mn"] = len(pieces)
+            it["src"] = lambda ti: s_u[:, ti]
 
-        def super_unit(h, m):
-            groups = [g for g in range(4 * m + 1, 4 * m + 5) if g < NCHUNK]
-            nu = len(groups)
-            acc = small.tile([P, 4, 4], F32, name="acc")
-            nc.vector.memset(acc[:], 0.0)
-            eg = eg_bufs[m % 2]
-            passes = []
-            for u, g in enumerate(groups):
-                tiles = unit_plan(g)
-                bi = 4 * (m % 2) + u
-                e_sb = e_bufs[bi]
-                layout = [[(en[0] if en is not None else None) for en in ent] for slab, ent in tiles]
-                msk = [[(en[1] if en is not None else None) for en in ent] for slab, ent in tiles]
-                g_slot = None
-                if g >= 5:
-                    for ti in range(len(layout)):
-                        for qd in range(4):
-                            if g_slot is None and layout[ti][qd] is None:
-                                g_slot = (ti, qd)
-                    if g_slot is None:
-                        layout.append([None, None, None, None])
-                        msk.append([None, None, None, None])
-                        g_slot = (len(layout) - 1, 0)
-                    layout[g_slot[0]][g_slot[1]] = 0
-                banks = [qk_bank(h, g, layout[ti], msk[ti]) for ti in range(len(layout))]
-                pieces = []
-                for ti in range(len(layout)):
-                    for q0, q1 in true_ranges([a is not None for a in layout[ti]]):
-                        pieces.append((ti, q0, q1))
-                mx = small.tile([P, 8], F32, name="mx")
-                s_u = sstage.tile([P, 2, 4, P], F32, name="s_u")
-                for i, (ti, q0, q1) in enumerate(pieces):
-                    nc.vector.tensor_scalar(
-                        out=s_u[:, ti, :, 32 * q0:32 * q1],
-                        in0=banks[ti][:, P * q0:P * q1].rearrange("q (p j) -> q j p", j=4),
-                        scalar1=-SCALE, scalar2=None, op0=ALU.mult, op1=ALU.min,
-                        accum_out=mx[:, i:i + 1],
-                    )
-                negm = small.tile([P, 1], F32, name="negm")
-                if len(pieces) == 2:
-                    nc.vector.tensor_tensor(out=negm[:], in0=mx[:, 0:1], in1=mx[:, 1:2], op=ALU.min)
-                else:
-                    nc.vector.tensor_reduce(out=negm[:], in_=mx[:, 0:len(pieces)], axis=AX.X, op=ALU.min)
-                n_acc = 0
-                for ti, (slab, ent) in enumerate(tiles):
-                    for qd in range(4):
-                        if ent[qd] is None:
-                            if not is_zero.get((bi, ti, qd), False):
-                                nc.gpsimd.memset(e_sb[:, ti, :, 32 * qd:32 * (qd + 1)], 0.0)
-                                is_zero[(bi, ti, qd)] = True
-                        else:
-                            is_zero[(bi, ti, qd)] = False
-                    for q0, q1 in true_ranges([en is not None for en in ent]):
-                        nc.scalar.activation(
-                            out=e_sb[:, ti, :, 32 * q0:32 * q1],
-                            in_=s_u[:, ti, :, 32 * q0:32 * q1],
-                            func=ACT.Exp, bias=negm[:, 0:1], scale=-1.0,
-                            accum_out=acc[:, u, n_acc:n_acc + 1],
-                        )
-                        n_acc += 1
-                if g_slot is not None:
-                    ti, qd = g_slot
+        def unit_comb(it):
+            negm = small.tile([P, 1], F32, name="negm")
+            mn = it["mn"]
+            if it["n_mn"] == 2:
+                nc.vector.tensor_tensor(out=negm[:], in0=mn[:, 0:1], in1=mn[:, 1:2], op=ALU.min)
+            else:
+                nc.vector.tensor_reduce(out=negm[:], in_=mn[:, 0:it["n_mn"]], axis=AX.X, op=ALU.min)
+            it["negm"] = negm
+
+        def gs_pass(it):
+            s = it["s"]
+            if s == 0:
+                gl["mn"] = small.tile([P, NSLAB], F32, name="gmn")
+            nc.vector.tensor_scalar(
+                out=s_sb[:, s], in0=it["banks"][0][:].rearrange("q (p j) -> q j p", j=4),
+                scalar1=-SCALE, scalar2=None, op0=ALU.mult, op1=ALU.min,
+                accum_out=gl["mn"][:, s:s + 1],
+            )
+
+        def gs_comb(it):
+            gl["negm"] = small.tile([P, 1], F32, name="gnegm")
+            nc.vector.tensor_reduce(out=gl["negm"][:], in_=gl["mn"][:], axis=AX.X, op=ALU.min)
+
+        def acc_init(grp):
+            grp["acc"] = small.tile([P, 4, 4], F32, name="acc")
+            nc.gpsimd.memset(grp["acc"][:], 0.0)
+
+        def e_exp(it):
+            bi = it["buf"]
+            e_sb = e_bufs[bi]
+            acc = it["group"]["acc"]
+            negm = it["negm"] if it["kind"] == "unit" else gl["negm"]
+            n_acc = 0
+            for ti, (slab, chunks, ent) in enumerate(it["tiles"]):
+                for qd in range(4):
+                    if ent[qd] is None:
+                        if not is_zero.get((bi, ti, qd), False):
+                            nc.gpsimd.memset(e_sb[:, ti, :, 32 * qd:32 * (qd + 1)], 0.0)
+                            is_zero[(bi, ti, qd)] = True
+                    else:
+                        is_zero[(bi, ti, qd)] = False
+                for q0, q1 in true_ranges([en is not None for en in ent]):
                     nc.scalar.activation(
-                        out=eg[:, :, 32 * u:32 * (u + 1)],
-                        in_=s_u[:, ti, :, 32 * qd:32 * (qd + 1)],
+                        out=e_sb[:, ti, :, 32 * q0:32 * q1], in_=it["src"](ti)[:, :, 32 * q0:32 * q1],
                         func=ACT.Exp, bias=negm[:, 0:1], scale=-1.0,
-                        accum_out=acc[:, u, n_acc:n_acc + 1],
+                        accum_out=acc[:, it["gidx"], n_acc:n_acc + 1],
                     )
                     n_acc += 1
-                assert n_acc <= 4
-                codes, scl = to_codes(
-                    lambda ti, j, e_sb=e_sb: e_sb[:, ti, j, :], len(tiles), "v" if u % 2 == 0 else "s"
-                )
-                passes.append([(codes, scl, ti, tiles[ti][0]) for ti in range(len(tiles))])
-            if m >= 1:
-                codes, scl = to_codes(lambda ti, j: eg[:, j, :], 1, "v")
-                for u in range(nu):
-                    passes[u].append((codes, scl, 0, ("G", u)))
-            tot = small.tile([P, 4], F32, name="tot")
-            nc.vector.tensor_reduce(out=tot[:, 0:nu], in_=acc[:, 0:nu, :], axis=AX.X, op=ALU.add)
-            rinv = small.tile([P, 4], F32, name="rinv")
-            nc.vector.reciprocal(out=rinv[:, 0:nu], in_=tot[:, 0:nu])
-            o_sb = opool.tile([P, 4, D], F32, name="o_sb")
-            o_ps = None
-            for u in range(nu):
-                if u % 2 == 0:
-                    o_ps = ps_o.tile([P, 2, D], F32, name="o_ps")
-                mx_group(h, o_ps[:, u % 2, :], passes[u])
-                nc.scalar.activation(
-                    out=o_sb[:, u, :], in_=o_ps[:, u % 2, :], func=ACT.Copy, scale=rinv[:, u:u + 1]
-                )
-            r0 = h * S + P * groups[0]
-            nc.scalar.dma_start(
-                out=of[r0:r0 + P * nu, :].rearrange("(u p) d -> p u d", p=P), in_=o_sb[:, 0:nu, :]
+            assert n_acc <= 4
+
+        def e_transpose(it):
+            e_sb = e_bufs[it["buf"]]
+            eT = ps_t.tile([P, 2, 4, P], BF16, name="eT")
+            for ti in range(2):
+                for j in range(4):
+                    nc.tensor.transpose(eT[:, ti, j, :], e_sb[:, ti, j, :], ident_bf[:])
+            it["eT"] = eT
+
+        def e_copy(it):
+            grp = gstage.tile([P, 2, P, 4], BF16, name="grp", align_bytes=64)
+            src = it["eT"][:].rearrange("p t j q -> p t q j")
+            if it["copy_v"]:
+                nc.vector.tensor_copy(out=grp[:], in_=src)
+            else:
+                nc.scalar.copy(out=grp[:], in_=src)
+            it["grp"] = grp
+
+        def e_quant(it):
+            tag = "c" if it["kind"] == "unit" else "gc"
+            codes = cpool.tile([P, 2 * P], U32, name="%s_codes" % tag, align_bytes=64)
+            scl = cpool.tile([P, 2 * P], U8, name="%s_scl" % tag, align_bytes=64)
+            nc.vector.quantize_mx(
+                out=codes[:].bitcast(FP8X4), scales=scl[:], in_=it["grp"][:].rearrange("p t q j -> p (t q j)")
             )
+            it["codes"] = codes
+            it["scl"] = scl
 
-        gl = {}
-
-        def global_scores(h, s):
-            if s == 0:
-                gl["mx"] = small.tile([P, NSLAB], F32, name="gmx")
-            ps = qk_bank(h, 0, [4 * s, 4 * s + 1, 4 * s + 2, 4 * s + 3], [None] * 4)
-            nc.vector.tensor_scalar(
-                out=s_sb[:, s], in0=ps[:].rearrange("q (p j) -> q j p", j=4),
-                scalar1=-SCALE, scalar2=None, op0=ALU.mult, op1=ALU.min,
-                accum_out=gl["mx"][:, s:s + 1],
-            )
-
-        def global_finish(h):
-            negm = small.tile([P, 1], F32, name="negm")
-            nc.vector.tensor_reduce(out=negm[:], in_=gl["mx"][:], axis=AX.X, op=ALU.min)
-            acc = small.tile([P, NSLAB], F32, name="gacc")
-            passes = []
-            for i in range(NSLAB // 2):
-                e_sb = e_bufs[i]
-                for ti in range(2):
-                    s = 2 * i + ti
-                    for qd in range(4):
-                        is_zero[(i, ti, qd)] = False
-                    nc.scalar.activation(
-                        out=e_sb[:, ti], in_=s_sb[:, s], func=ACT.Exp, bias=negm[:, 0:1], scale=-1.0,
-                        accum_out=acc[:, s:s + 1],
-                    )
-                codes, scl = to_codes(
-                    lambda ti, j, e_sb=e_sb: e_sb[:, ti, j, :], 2, "v" if i % 2 == 0 else "s"
-                )
-                passes.extend([(codes, scl, ti, ("L", 2 * i + ti)) for ti in range(2)])
-            tot = small.tile([P, 4], F32, name="tot")
-            nc.vector.tensor_reduce(out=tot[:, 0:1], in_=acc[:], axis=AX.X, op=ALU.add)
-            rinv = small.tile([P, 4], F32, name="rinv")
-            nc.vector.reciprocal(out=rinv[:, 0:1], in_=tot[:, 0:1])
+        def fin_mx(grp):
             o_ps = ps_o.tile([P, 2, D], F32, name="o_ps")
-            mx_group(h, o_ps[:, 0, :], passes)
-            o_sb = opool.tile([P, 4, D], F32, name="o_sb")
-            nc.scalar.activation(out=o_sb[:, 0, :], in_=o_ps[:, 0, :], func=ACT.Copy, scale=rinv[:, 0:1])
-            nc.scalar.dma_start(out=of[h * S:h * S + P, :], in_=o_sb[:, 0, :])
+            grp["o_ps"] = o_ps
+            one = grp["kind"] == "gf"
+            mem = grp["members"]
+            for i, it in enumerate(mem):
+                for ti in range(2):
+                    m = (it["g"] - 1) // 4 if it["kind"] == "unit" else None
+                    vc, vs = v_slab(it["h"], it["tiles"][ti][0], m)
+                    nc.tensor.matmul_mx(
+                        out=o_ps[:, 0 if one else i, :],
+                        lhsT=it["codes"][:, P * ti:P * (ti + 1)].bitcast(FP8X4),
+                        lhsT_scale=it["scl"][:, P * ti:P * (ti + 1)],
+                        rhs=vc.bitcast(FP8X4), rhs_scale=vs,
+                        start=(ti == 0 and (i == 0 or not one)),
+                        stop=(ti == 1 and (i == len(mem) - 1 or not one)),
+                    )
 
-        def head_start(h):
-            head_alloc(h)
-            setup(h, 0)
-            setup(h, 1)
+        def fin_rinv(grp):
+            n = len(grp["members"])
+            tot = small.tile([P, 2], F32, name="tot")
+            rinv = small.tile([P, 2], F32, name="rinv")
+            if grp["kind"] == "gf":
+                n = 1
+                nc.vector.tensor_reduce(out=tot[:, 0:1], in_=grp["acc"][:], axis=AX.XY, op=ALU.add)
+            else:
+                nc.vector.tensor_reduce(out=tot[:, 0:n], in_=grp["acc"][:, 0:n, :], axis=AX.X, op=ALU.add)
+            nc.vector.reciprocal(out=rinv[:, 0:n], in_=tot[:, 0:n])
+            grp["rinv"] = rinv
+            grp["n_out"] = n
 
-        head_start(0)
-        for h in range(H):
-            vg_prep(h)
-            for m in range(NSLAB):
-                if m + 2 < NSLAB:
-                    setup(h, m + 2)
-                if 1 <= m + 1 <= 6:
-                    x_prep(h, m + 1)
-                super_unit(h, m)
-                global_scores(h, m)
-            if h + 1 < H:
-                head_start(h + 1)
-            global_finish(h)
+        def fin_out(grp):
+            n = grp["n_out"]
+            o_sb = opool.tile([P, 2, D], F32, name="o_sb")
+            for i in range(n):
+                nc.scalar.activation(
+                    out=o_sb[:, i, :], in_=grp["o_ps"][:, i, :], func=ACT.Copy, scale=grp["rinv"][:, i:i + 1]
+                )
+            first = grp["members"][0]
+            r0 = first["h"] * S + (P * first["g"] if grp["kind"] == "unit" else 0)
+            nc.scalar.dma_start(
+                out=of[r0:r0 + P * n, :].rearrange("(u p) d -> p u d", p=P), in_=o_sb[:, 0:n, :]
+            )
+
+        items = build_items()
+        groups = {}
+        cnt = 0
+        for it in items:
+            if it["kind"] not in ("unit", "gf"):
+                continue
+            it["buf"] = cnt % 8
+            it["copy_v"] = (cnt % 8) in COPY_ON_VECTOR
+            cnt += 1
+            if it["kind"] == "unit":
+                key = (it["h"], "unit", (it["g"] - 1) // 2)
+                it["tiles"] = unit_plan(it["g"])
+            else:
+                key = (it["h"], "gf", 0)
+                it["tiles"] = [
+                    (("L", s), None, [(4 * s + c, None) for c in range(4)]) for s in (2 * it["i"], 2 * it["i"] + 1)
+                ]
+                it["src"] = lambda ti, i=it["i"]: s_sb[:, 2 * i + ti]
+            if key not in groups:
+                groups[key] = {"kind": it["kind"], "members": []}
+            it["group"] = groups[key]
+            it["gidx"] = len(groups[key]["members"])
+            groups[key]["members"].append(it)
+
+        def at(i, kinds):
+            if 0 <= i < len(items) and items[i]["kind"] in kinds:
+                return items[i]
+            return None
+
+        def stream():
+            for t in range(len(items) + 6):
+                for i in (range(LOAD_AHEAD + 1) if t == 0 else [t + LOAD_AHEAD]):
+                    if at(i, ("kq",)):
+                        kq_load(items[i])
+                cur = at(t, ("unit", "gs", "kq"))
+                prev = at(t - 1, ("unit", "gs", "kq"))
+                ex = at(t - 2, ("unit", "gf"))
+                tr = at(t - 3, ("unit", "gf"))
+                qn = at(t - 4, ("unit", "gf"))
+                fin = at(t - 5, ("unit", "gf"))
+                fin = fin["group"] if fin and fin["group"]["members"][-1] is fin else None
+                if tr:
+                    e_transpose(tr)
+                if cur and cur["kind"] == "unit":
+                    ch = [[(en[0] if en else None) for en in ent] for slab, chunks, ent in cur["tiles"]]
+                    mk = [[(en[1] if en else None) for en in ent] for slab, chunks, ent in cur["tiles"]]
+                    cur["banks"] = [qk_bank(cur["h"], cur["g"], ch[0], mk[0])]
+                    if fin:
+                        fin_mx(fin)
+                    cur["banks"].append(qk_bank(cur["h"], cur["g"], ch[1], mk[1]))
+                else:
+                    if cur and cur["kind"] == "gs":
+                        s = cur["s"]
+                        cur["banks"] = [qk_bank(cur["h"], 0, [4 * s, 4 * s + 1, 4 * s + 2, 4 * s + 3], [None] * 4)]
+                    if cur and cur["kind"] == "kq":
+                        kq_transpose(cur)
+                    if fin:
+                        fin_mx(fin)
+                if cur and cur["kind"] == "kq":
+                    kq_regroup(cur)
+                nxt = at(t - 1, ("unit", "gf"))
+                if nxt and nxt["gidx"] == 0:
+                    acc_init(nxt["group"])
+                if prev and prev["kind"] == "unit":
+                    unit_pass(prev)
+                if prev and prev["kind"] == "gs":
+                    gs_pass(prev)
+                if prev and prev["kind"] == "kq":
+                    s = prev["s"]
+                    nc.vector.tensor_copy(out=hd[prev["h"]]["kT"][:, 512 * s:512 * (s + 1)], in_=prev["banks"][0][:])
+                if qn:
+                    e_quant(qn)
+                if at(t - 2, ("kq",)):
+                    kq_vquant(items[t - 2])
+                if prev and prev["kind"] == "unit":
+                    unit_comb(prev)
+                if prev and prev["kind"] == "gs" and prev["s"] == NSLAB - 1:
+                    gs_comb(prev)
+                if fin:
+                    fin_rinv(fin)
+                if tr and tr["copy_v"]:
+                    e_copy(tr)
+                if prev and prev["kind"] == "kq":
+                    s = prev["s"]
+                    nc.scalar.copy(out=hd[prev["h"]]["qT"][:, 512 * s:512 * (s + 1)], in_=prev["banks"][1][:])
+                if ex:
+                    e_exp(ex)
+                if tr and not tr["copy_v"]:
+                    e_copy(tr)
+                if fin:
+                    fin_out(fin)
+                if 0 <= t - 1 < len(items) and "variants" in items[t - 1]:
+                    build_variants(items[t - 1]["variants"][0], items[t - 1]["variants"][1])
+
+        if PINNED:
+            with tc.manual_schedule():
+                stream()
+        else:
+            stream()

@@ -24,7 +24,7 @@ NEG = -1.0e30
 VW = D + D // 4
 FLOPS = 2 * 2 * P * 1024 * D * 70
 
-PINNED = False
+PINNED = True
 COPY_ON_VECTOR = (0, 3, 6)
 LOAD_AHEAD = 6
 

@@ -25,8 +25,9 @@ VW = D + D // 4
 FLOPS = 2 * 2 * P * 1024 * D * 70
 
 PINNED = True
-COPY_ON_VECTOR = (0, 3, 6)
+COPY_ON_VECTOR = (0, 2, 4, 6)
 LOAD_AHEAD = 6
+LAGS = (1, 3, 5, 6, 8, 10, 11)
 
 
 def unit_plan(g):
@@ -185,7 +186,6 @@ def tile_globallocalattention_t_kernel(tc, q, k, v, out):
             r0 = h * S + 512 * s
             it["k_raw"] = raw.tile([P, 4 * D], BF16, name="k_raw")
             it["q_raw"] = raw.tile([P, 4 * D], BF16, name="q_raw")
-            it["v_raw"] = raw.tile([P, 4 * D], BF16, name="v_raw")
             nc.sync.dma_start(
                 out=it["k_raw"][:].rearrange("p (t d) -> p t d", t=4),
                 in_=kf[r0:r0 + 512, :].rearrange("(t p) d -> p t d", p=P),
@@ -194,6 +194,10 @@ def tile_globallocalattention_t_kernel(tc, q, k, v, out):
                 out=it["q_raw"][:].rearrange("p (t d) -> p t d", t=4),
                 in_=qf[r0:r0 + 512, :].rearrange("(t p) d -> p t d", p=P),
             )
+
+        def v_load(it):
+            r0 = it["h"] * S + 512 * it["s"]
+            it["v_raw"] = raw.tile([P, 4 * D], BF16, name="v_raw")
             nc.sync.dma_start(
                 out=it["v_raw"][:], in_=vf[r0:r0 + 512, :].rearrange("(p j) d -> p (j d)", j=4)
             )
@@ -293,6 +297,7 @@ def tile_globallocalattention_t_kernel(tc, q, k, v, out):
             it["mn"] = mn
             it["n_mn"] = len(pieces)
             it["src"] = lambda ti: s_u[:, ti]
+            it["src2"] = s_u[:]
 
         def unit_comb(it):
             negm = small.tile([P, 1], F32, name="negm")
@@ -317,9 +322,14 @@ def tile_globallocalattention_t_kernel(tc, q, k, v, out):
             gl["negm"] = small.tile([P, 1], F32, name="gnegm")
             nc.vector.tensor_reduce(out=gl["negm"][:], in_=gl["mn"][:], axis=AX.X, op=ALU.min)
 
+        def whole(it):
+            return all([en is not None for slab, chunks, ent in it["tiles"] for en in ent])
+
         def acc_init(grp):
             grp["acc"] = small.tile([P, 4, 4], F32, name="acc")
-            nc.gpsimd.memset(grp["acc"][:], 0.0)
+            grp["plain"] = all([whole(it) for it in grp["members"]])
+            if not grp["plain"]:
+                nc.gpsimd.memset(grp["acc"][:], 0.0)
 
         def e_exp(it):
             bi = it["buf"]
@@ -327,6 +337,15 @@ def tile_globallocalattention_t_kernel(tc, q, k, v, out):
             acc = it["group"]["acc"]
             negm = it["negm"] if it["kind"] == "unit" else gl["negm"]
             n_acc = 0
+            if whole(it):
+                for ti in range(2):
+                    for qd in range(4):
+                        is_zero[(bi, ti, qd)] = False
+                nc.scalar.activation(
+                    out=e_sb[:], in_=it["src2"], func=ACT.Exp, bias=negm[:, 0:1], scale=-1.0,
+                    accum_out=acc[:, it["gidx"], 0:1],
+                )
+                return
             for ti, (slab, chunks, ent) in enumerate(it["tiles"]):
                 for qd in range(4):
                     if ent[qd] is None:
@@ -391,14 +410,18 @@ def tile_globallocalattention_t_kernel(tc, q, k, v, out):
 
         def fin_rinv(grp):
             n = len(grp["members"])
-            tot = small.tile([P, 2], F32, name="tot")
             rinv = small.tile([P, 2], F32, name="rinv")
+            if grp["kind"] == "gf" or not grp["plain"]:
+                tot = small.tile([P, 2], F32, name="tot")
             if grp["kind"] == "gf":
+                nc.vector.tensor_reduce(out=tot[:, 0:1], in_=grp["acc"][:, 0:n, 0:1], axis=AX.XY, op=ALU.add)
                 n = 1
-                nc.vector.tensor_reduce(out=tot[:, 0:1], in_=grp["acc"][:], axis=AX.XY, op=ALU.add)
+                nc.vector.reciprocal(out=rinv[:, 0:1], in_=tot[:, 0:1])
+            elif grp["plain"]:
+                nc.vector.reciprocal(out=rinv[:, 0:n], in_=grp["acc"][:, 0:n, 0])
             else:
                 nc.vector.tensor_reduce(out=tot[:, 0:n], in_=grp["acc"][:, 0:n, :], axis=AX.X, op=ALU.add)
-            nc.vector.reciprocal(out=rinv[:, 0:n], in_=tot[:, 0:n])
+                nc.vector.reciprocal(out=rinv[:, 0:n], in_=tot[:, 0:n])
             grp["rinv"] = rinv
             grp["n_out"] = n
 
@@ -411,7 +434,7 @@ def tile_globallocalattention_t_kernel(tc, q, k, v, out):
                 )
             first = grp["members"][0]
             r0 = first["h"] * S + (P * first["g"] if grp["kind"] == "unit" else 0)
-            nc.scalar.dma_start(
+            nc.sync.dma_start(
                 out=of[r0:r0 + P * n, :].rearrange("(u p) d -> p u d", p=P), in_=o_sb[:, 0:n, :]
             )
 
@@ -432,7 +455,7 @@ def tile_globallocalattention_t_kernel(tc, q, k, v, out):
                 it["tiles"] = [
                     (("L", s), None, [(4 * s + c, None) for c in range(4)]) for s in (2 * it["i"], 2 * it["i"] + 1)
                 ]
-                it["src"] = lambda ti, i=it["i"]: s_sb[:, 2 * i + ti]
+                it["src2"] = s_sb[:, 2 * it["i"]:2 * it["i"] + 2]
             if key not in groups:
                 groups[key] = {"kind": it["kind"], "members": []}
             it["group"] = groups[key]
@@ -445,25 +468,35 @@ def tile_globallocalattention_t_kernel(tc, q, k, v, out):
             return None
 
         def stream():
-            for t in range(len(items) + 6):
-                for i in (range(LOAD_AHEAD + 1) if t == 0 else [t + LOAD_AHEAD]):
-                    if at(i, ("kq",)):
-                        kq_load(items[i])
+            l_pass, l_exp, l_tr, l_cp, l_qn, l_mx, l_out = LAGS
+            e_kinds = ("unit", "gf")
+
+            def group_done(i):
+                it = at(i, e_kinds)
+                return it["group"] if it and it["group"]["members"][-1] is it else None
+
+            for t in range(len(items) + l_out + 1):
+                ahead = [i for i in (range(LOAD_AHEAD + 1) if t == 0 else [t + LOAD_AHEAD]) if at(i, ("kq",))]
+                for i in ahead:
+                    kq_load(items[i])
+                for i in ahead:
+                    v_load(items[i])
                 cur = at(t, ("unit", "gs", "kq"))
-                prev = at(t - 1, ("unit", "gs", "kq"))
-                ex = at(t - 2, ("unit", "gf"))
-                tr = at(t - 3, ("unit", "gf"))
-                qn = at(t - 4, ("unit", "gf"))
-                fin = at(t - 5, ("unit", "gf"))
-                fin = fin["group"] if fin and fin["group"]["members"][-1] is fin else None
+                prev = at(t - l_pass, ("unit", "gs", "kq"))
+                ex = at(t - l_exp, e_kinds)
+                tr = at(t - l_tr, e_kinds)
+                cp = at(t - l_cp, e_kinds)
+                qn = at(t - l_qn, e_kinds)
+                mx = group_done(t - l_mx)
+                fo = group_done(t - l_out)
                 if tr:
                     e_transpose(tr)
                 if cur and cur["kind"] == "unit":
                     ch = [[(en[0] if en else None) for en in ent] for slab, chunks, ent in cur["tiles"]]
                     mk = [[(en[1] if en else None) for en in ent] for slab, chunks, ent in cur["tiles"]]
                     cur["banks"] = [qk_bank(cur["h"], cur["g"], ch[0], mk[0])]
-                    if fin:
-                        fin_mx(fin)
+                    if mx:
+                        fin_mx(mx)
                     cur["banks"].append(qk_bank(cur["h"], cur["g"], ch[1], mk[1]))
                 else:
                     if cur and cur["kind"] == "gs":
@@ -471,11 +504,11 @@ def tile_globallocalattention_t_kernel(tc, q, k, v, out):
                         cur["banks"] = [qk_bank(cur["h"], 0, [4 * s, 4 * s + 1, 4 * s + 2, 4 * s + 3], [None] * 4)]
                     if cur and cur["kind"] == "kq":
                         kq_transpose(cur)
-                    if fin:
-                        fin_mx(fin)
+                    if mx:
+                        fin_mx(mx)
                 if cur and cur["kind"] == "kq":
                     kq_regroup(cur)
-                nxt = at(t - 1, ("unit", "gf"))
+                nxt = at(t - l_exp + 1, e_kinds)
                 if nxt and nxt["gidx"] == 0:
                     acc_init(nxt["group"])
                 if prev and prev["kind"] == "unit":
@@ -487,27 +520,28 @@ def tile_globallocalattention_t_kernel(tc, q, k, v, out):
                     nc.vector.tensor_copy(out=hd[prev["h"]]["kT"][:, 512 * s:512 * (s + 1)], in_=prev["banks"][0][:])
                 if qn:
                     e_quant(qn)
-                if at(t - 2, ("kq",)):
-                    kq_vquant(items[t - 2])
+                if at(t - l_pass - 1, ("kq",)):
+                    kq_vquant(items[t - l_pass - 1])
+                if cp and cp["copy_v"]:
+                    e_copy(cp)
                 if prev and prev["kind"] == "unit":
                     unit_comb(prev)
                 if prev and prev["kind"] == "gs" and prev["s"] == NSLAB - 1:
                     gs_comb(prev)
-                if fin:
-                    fin_rinv(fin)
-                if tr and tr["copy_v"]:
-                    e_copy(tr)
+                if mx:
+                    fin_rinv(mx)
                 if prev and prev["kind"] == "kq":
                     s = prev["s"]
                     nc.scalar.copy(out=hd[prev["h"]]["qT"][:, 512 * s:512 * (s + 1)], in_=prev["banks"][1][:])
                 if ex:
                     e_exp(ex)
-                if tr and not tr["copy_v"]:
-                    e_copy(tr)
-                if fin:
-                    fin_out(fin)
-                if 0 <= t - 1 < len(items) and "variants" in items[t - 1]:
-                    build_variants(items[t - 1]["variants"][0], items[t - 1]["variants"][1])
+                if cp and not cp["copy_v"]:
+                    e_copy(cp)
+                if fo:
+                    fin_out(fo)
+                i = t - l_pass - 2
+                if 0 <= i < len(items) and "variants" in items[i]:
+                    build_variants(items[i]["variants"][0], items[i]["variants"][1])
 
         if PINNED:
             with tc.manual_schedule():

@@ -25,9 +25,11 @@ VW = D + D // 4
 FLOPS = 2 * 2 * P * 1024 * D * 70
 
 PINNED = True
-COPY_ON_VECTOR = (0, 2, 4, 6)
+COPY_ON_VECTOR = (3,)
 LOAD_AHEAD = 6
 LAGS = (1, 3, 5, 6, 8, 10, 11)
+OUT_ON_VECTOR = True
+QT_ON_VECTOR = True
 
 
 def unit_plan(g):
@@ -158,7 +160,9 @@ def tile_globallocalattention_t_kernel(tc, q, k, v, out):
                 pattern=[[-sign, P]], channel_multiplier=sign,
             )
             mb = const.tile([P, P], BF16, name="mask_b_%s" % kind)
-            nc.vector.tensor_copy(out=mb[:], in_=mf[:])
+            nc.vector.tensor_copy(
+                out=mb[:].rearrange("t (j y) -> t y j", j=4), in_=mf[:].rearrange("t (y j) -> t y j", j=4)
+            )
             mask_bf[kind] = mb
 
         e_bufs = [fixed.tile([P, 2, 4, P], BF16, name="e_sb%d" % i) for i in range(8)]
@@ -176,7 +180,7 @@ def tile_globallocalattention_t_kernel(tc, q, k, v, out):
             hd[h] = {
                 "qT": qT, "kT": kT, "vl": vl,
                 "qv": qT[:].bitcast(BF16).rearrange("p (r e) -> p e r", e=2),
-                "kv": kT[:].bitcast(BF16).rearrange("p (r e) -> p e r", e=2),
+                "kv": kT[:].bitcast(BF16).rearrange("p (c j y e) -> p e j c y", j=4, y=32, e=2),
             }
 
         def kq_load(it):
@@ -262,20 +266,22 @@ def tile_globallocalattention_t_kernel(tc, q, k, v, out):
         def qk_bank(h, g, chunks, masks):
             t = hd[h]
             ps = ps_s.tile([P, 512], F32, name="s_ps")
+            view = ps[:].rearrange("q (j c y) -> q j c y", j=4, y=32)
             for q0, n, a0 in qk_runs(chunks):
-                dst = ps[:, P * q0:P * (q0 + n)]
+                dst = view[:, :, q0:q0 + n, :]
                 nc.tensor.matmul(
-                    out=dst, lhsT=t["qv"][:, 0, P * g:P * (g + 1)], rhs=t["kv"][:, 0, P * a0:P * (a0 + n)],
+                    out=dst, lhsT=t["qv"][:, 0, P * g:P * (g + 1)], rhs=t["kv"][:, 0, :, a0:a0 + n, :],
                     start=True, stop=False,
                 )
                 for qd in range(q0, q0 + n):
                     if masks[qd] is not None:
                         nc.tensor.matmul(
-                            out=ps[:, P * qd:P * (qd + 1)], lhsT=ident_bf[:], rhs=mask_bf[masks[qd]][:],
+                            out=view[:, :, qd, :], lhsT=ident_bf[:],
+                            rhs=mask_bf[masks[qd]][:].rearrange("t (j y) -> t j y", j=4),
                             start=False, stop=False,
                         )
                 nc.tensor.matmul(
-                    out=dst, lhsT=t["qv"][:, 1, P * g:P * (g + 1)], rhs=t["kv"][:, 1, P * a0:P * (a0 + n)],
+                    out=dst, lhsT=t["qv"][:, 1, P * g:P * (g + 1)], rhs=t["kv"][:, 1, :, a0:a0 + n, :],
                     start=False, stop=True,
                 )
             return ps
@@ -290,7 +296,7 @@ def tile_globallocalattention_t_kernel(tc, q, k, v, out):
             for i, (ti, q0, q1) in enumerate(pieces):
                 nc.vector.tensor_scalar(
                     out=s_u[:, ti, :, 32 * q0:32 * q1],
-                    in0=it["banks"][ti][:, P * q0:P * q1].rearrange("q (p j) -> q j p", j=4),
+                    in0=it["banks"][ti][:].rearrange("q (j p) -> q j p", j=4)[:, :, 32 * q0:32 * q1],
                     scalar1=-SCALE, scalar2=None, op0=ALU.mult, op1=ALU.min,
                     accum_out=mn[:, i:i + 1],
                 )
@@ -313,7 +319,7 @@ def tile_globallocalattention_t_kernel(tc, q, k, v, out):
             if s == 0:
                 gl["mn"] = small.tile([P, NSLAB], F32, name="gmn")
             nc.vector.tensor_scalar(
-                out=s_sb[:, s], in0=it["banks"][0][:].rearrange("q (p j) -> q j p", j=4),
+                out=s_sb[:, s], in0=it["banks"][0][:].rearrange("q (j p) -> q j p", j=4),
                 scalar1=-SCALE, scalar2=None, op0=ALU.mult, op1=ALU.min,
                 accum_out=gl["mn"][:, s:s + 1],
             )
@@ -429,9 +435,15 @@ def tile_globallocalattention_t_kernel(tc, q, k, v, out):
             n = grp["n_out"]
             o_sb = opool.tile([P, 2, D], F32, name="o_sb")
             for i in range(n):
-                nc.scalar.activation(
-                    out=o_sb[:, i, :], in_=grp["o_ps"][:, i, :], func=ACT.Copy, scale=grp["rinv"][:, i:i + 1]
-                )
+                if OUT_ON_VECTOR:
+                    nc.vector.tensor_scalar(
+                        out=o_sb[:, i, :], in0=grp["o_ps"][:, i, :], scalar1=grp["rinv"][:, i:i + 1], scalar2=None,
+                        op0=ALU.mult,
+                    )
+                else:
+                    nc.scalar.activation(
+                        out=o_sb[:, i, :], in_=grp["o_ps"][:, i, :], func=ACT.Copy, scale=grp["rinv"][:, i:i + 1]
+                    )
             first = grp["members"][0]
             r0 = first["h"] * S + (P * first["g"] if grp["kind"] == "unit" else 0)
             nc.sync.dma_start(
@@ -517,7 +529,10 @@ def tile_globallocalattention_t_kernel(tc, q, k, v, out):
                     gs_pass(prev)
                 if prev and prev["kind"] == "kq":
                     s = prev["s"]
-                    nc.vector.tensor_copy(out=hd[prev["h"]]["kT"][:, 512 * s:512 * (s + 1)], in_=prev["banks"][0][:])
+                    nc.vector.tensor_copy(
+                        out=hd[prev["h"]]["kT"][:, 512 * s:512 * (s + 1)].rearrange("w (c j y) -> w c y j", j=4, y=32),
+                        in_=prev["banks"][0][:].rearrange("w (c y j) -> w c y j", y=32, j=4),
+                    )
                 if qn:
                     e_quant(qn)
                 if at(t - l_pass - 1, ("kq",)):
@@ -530,14 +545,19 @@ def tile_globallocalattention_t_kernel(tc, q, k, v, out):
                     gs_comb(prev)
                 if mx:
                     fin_rinv(mx)
-                if prev and prev["kind"] == "kq":
+                if fo and OUT_ON_VECTOR:
+                    fin_out(fo)
+                if prev and prev["kind"] == "kq" and QT_ON_VECTOR:
+                    s = prev["s"]
+                    nc.vector.tensor_copy(out=hd[prev["h"]]["qT"][:, 512 * s:512 * (s + 1)], in_=prev["banks"][1][:])
+                if prev and prev["kind"] == "kq" and not QT_ON_VECTOR:
                     s = prev["s"]
                     nc.scalar.copy(out=hd[prev["h"]]["qT"][:, 512 * s:512 * (s + 1)], in_=prev["banks"][1][:])
                 if ex:
                     e_exp(ex)
                 if cp and not cp["copy_v"]:
                     e_copy(cp)
-                if fo:
+                if fo and not OUT_ON_VECTOR:
                     fin_out(fo)
                 i = t - l_pass - 2
                 if 0 <= i < len(items) and "variants" in items[i]:

@@ -25,7 +25,7 @@ VW = D + D // 4
 FLOPS = 2 * 2 * P * 1024 * D * 70
 
 PINNED = True
-COPY_ON_VECTOR = (3,)
+COPY_ON_VECTOR = ()
 LOAD_AHEAD = 6
 LAGS = (1, 3, 5, 6, 8, 10, 11)
 OUT_ON_VECTOR = True
@@ -218,10 +218,9 @@ def tile_globallocalattention_t_kernel(tc, q, k, v, out):
 
         def kq_regroup(it):
             vgrp = vstage.tile([P, 4 * D], BF16, name="vgrp", align_bytes=64)
-            nc.gpsimd.tensor_scalar(
-                out=vgrp[:].rearrange("p (d j) -> p d j", j=4),
-                in0=it["v_raw"][:].rearrange("p (j d) -> p d j", j=4),
-                scalar1=1.0, scalar2=0.0, op0=ALU.mult, op1=ALU.add,
+            nc.vector.tensor_copy(
+                out=vgrp[:].rearrange("p (c i j) -> p c j i", i=4, j=4),
+                in_=it["v_raw"][:].rearrange("p (j c i) -> p c j i", j=4, i=4),
             )
             it["vgrp"] = vgrp
 
@@ -518,8 +517,6 @@ def tile_globallocalattention_t_kernel(tc, q, k, v, out):
                         kq_transpose(cur)
                     if mx:
                         fin_mx(mx)
-                if cur and cur["kind"] == "kq":
-                    kq_regroup(cur)
                 nxt = at(t - l_exp + 1, e_kinds)
                 if nxt and nxt["gidx"] == 0:
                     acc_init(nxt["group"])
@@ -535,6 +532,8 @@ def tile_globallocalattention_t_kernel(tc, q, k, v, out):
                     )
                 if qn:
                     e_quant(qn)
+                if prev and prev["kind"] == "kq":
+                    kq_regroup(prev)
                 if at(t - l_pass - 1, ("kq",)):
                     kq_vquant(items[t - l_pass - 1])
                 if cp and cp["copy_v"]:

@@ -161,13 +161,14 @@ def tile_globallocalattention_t_kernel(tc, q, k, v, out):
             )
             mb = const.tile([P, P], BF16, name="mask_b_%s" % kind)
             nc.vector.tensor_copy(
-                out=mb[:].rearrange("t (j y) -> t y j", j=4), in_=mf[:].rearrange("t (y j) -> t y j", j=4)
+                out=mb[:].rearrange("t (u y e) -> t y u e", u=2, e=2),
+                in_=mf[:].rearrange("t (y u e) -> t y u e", u=2, e=2),
             )
             mask_bf[kind] = mb
 
-        e_bufs = [fixed.tile([P, 2, 4, P], BF16, name="e_sb%d" % i) for i in range(8)]
+        e_bufs = [fixed.tile([P, 2, 2, 2 * P], BF16, name="e_sb%d" % i) for i in range(8)]
         is_zero = {}
-        s_sb = fixed.tile([P, NSLAB, 4, P], F32)
+        s_sb = fixed.tile([P, NSLAB, 2, 2 * P], F32)
         hd = {}
         vv = {}
         gl = {}
@@ -180,7 +181,7 @@ def tile_globallocalattention_t_kernel(tc, q, k, v, out):
             hd[h] = {
                 "qT": qT, "kT": kT, "vl": vl,
                 "qv": qT[:].bitcast(BF16).rearrange("p (r e) -> p e r", e=2),
-                "kv": kT[:].bitcast(BF16).rearrange("p (c j y e) -> p e j c y", j=4, y=32, e=2),
+                "kv": kT[:].bitcast(BF16).rearrange("p (c u x h) -> p h u c x", u=2, x=64, h=2),
             }
 
         def kq_load(it):
@@ -265,7 +266,7 @@ def tile_globallocalattention_t_kernel(tc, q, k, v, out):
         def qk_bank(h, g, chunks, masks):
             t = hd[h]
             ps = ps_s.tile([P, 512], F32, name="s_ps")
-            view = ps[:].rearrange("q (j c y) -> q j c y", j=4, y=32)
+            view = ps[:].rearrange("q (u c x) -> q u c x", u=2, x=64)
             for q0, n, a0 in qk_runs(chunks):
                 dst = view[:, :, q0:q0 + n, :]
                 nc.tensor.matmul(
@@ -276,7 +277,7 @@ def tile_globallocalattention_t_kernel(tc, q, k, v, out):
                     if masks[qd] is not None:
                         nc.tensor.matmul(
                             out=view[:, :, qd, :], lhsT=ident_bf[:],
-                            rhs=mask_bf[masks[qd]][:].rearrange("t (j y) -> t j y", j=4),
+                            rhs=mask_bf[masks[qd]][:].rearrange("t (u x) -> t u x", u=2),
                             start=False, stop=False,
                         )
                 nc.tensor.matmul(
@@ -291,11 +292,11 @@ def tile_globallocalattention_t_kernel(tc, q, k, v, out):
                 for q0, q1 in true_ranges([en is not None for en in ent]):
                     pieces.append((ti, q0, q1))
             mn = small.tile([P, 8], F32, name="mn")
-            s_u = sstage.tile([P, 2, 4, P], F32, name="s_u")
+            s_u = sstage.tile([P, 2, 2, 2 * P], F32, name="s_u")
             for i, (ti, q0, q1) in enumerate(pieces):
                 nc.vector.tensor_scalar(
-                    out=s_u[:, ti, :, 32 * q0:32 * q1],
-                    in0=it["banks"][ti][:].rearrange("q (j p) -> q j p", j=4)[:, :, 32 * q0:32 * q1],
+                    out=s_u[:, ti, :, 64 * q0:64 * q1],
+                    in0=it["banks"][ti][:].rearrange("q (u x) -> q u x", u=2)[:, :, 64 * q0:64 * q1],
                     scalar1=-SCALE, scalar2=None, op0=ALU.mult, op1=ALU.min,
                     accum_out=mn[:, i:i + 1],
                 )
@@ -318,7 +319,7 @@ def tile_globallocalattention_t_kernel(tc, q, k, v, out):
             if s == 0:
                 gl["mn"] = small.tile([P, NSLAB], F32, name="gmn")
             nc.vector.tensor_scalar(
-                out=s_sb[:, s], in0=it["banks"][0][:].rearrange("q (j p) -> q j p", j=4),
+                out=s_sb[:, s], in0=it["banks"][0][:].rearrange("q (u x) -> q u x", u=2),
                 scalar1=-SCALE, scalar2=None, op0=ALU.mult, op1=ALU.min,
                 accum_out=gl["mn"][:, s:s + 1],
             )
@@ -355,13 +356,13 @@ def tile_globallocalattention_t_kernel(tc, q, k, v, out):
                 for qd in range(4):
                     if ent[qd] is None:
                         if not is_zero.get((bi, ti, qd), False):
-                            nc.gpsimd.memset(e_sb[:, ti, :, 32 * qd:32 * (qd + 1)], 0.0)
+                            nc.gpsimd.memset(e_sb[:, ti, :, 64 * qd:64 * (qd + 1)], 0.0)
                             is_zero[(bi, ti, qd)] = True
                     else:
                         is_zero[(bi, ti, qd)] = False
                 for q0, q1 in true_ranges([en is not None for en in ent]):
                     nc.scalar.activation(
-                        out=e_sb[:, ti, :, 32 * q0:32 * q1], in_=it["src"](ti)[:, :, 32 * q0:32 * q1],
+                        out=e_sb[:, ti, :, 64 * q0:64 * q1], in_=it["src"](ti)[:, :, 64 * q0:64 * q1],
                         func=ACT.Exp, bias=negm[:, 0:1], scale=-1.0,
                         accum_out=acc[:, it["gidx"], n_acc:n_acc + 1],
                     )
@@ -370,19 +371,20 @@ def tile_globallocalattention_t_kernel(tc, q, k, v, out):
 
         def e_transpose(it):
             e_sb = e_bufs[it["buf"]]
-            eT = ps_t.tile([P, 2, 4, P], BF16, name="eT")
+            eT = ps_t.tile([P, 2, 2, P], F32, name="eT")
             for ti in range(2):
-                for j in range(4):
-                    nc.tensor.transpose(eT[:, ti, j, :], e_sb[:, ti, j, :], ident_bf[:])
+                for u in range(2):
+                    nc.tensor.transpose(eT[:, ti, u, :], e_sb[:, ti, u, :].bitcast(F32), ident_f[:])
             it["eT"] = eT
 
         def e_copy(it):
             grp = gstage.tile([P, 2, P, 4], BF16, name="grp", align_bytes=64)
-            src = it["eT"][:].rearrange("p t j q -> p t q j")
+            src = it["eT"][:].rearrange("p t u q -> p t q u")
+            dst = grp[:].rearrange("p t q j -> p (t q j)").bitcast(F32).rearrange("p (t q u) -> p t q u", t=2, u=2)
             if it["copy_v"]:
-                nc.vector.tensor_copy(out=grp[:], in_=src)
+                nc.vector.tensor_copy(out=dst, in_=src)
             else:
-                nc.scalar.copy(out=grp[:], in_=src)
+                nc.scalar.copy(out=dst, in_=src)
             it["grp"] = grp
 
         def e_quant(it):
@@ -526,10 +528,12 @@ def tile_globallocalattention_t_kernel(tc, q, k, v, out):
                     gs_pass(prev)
                 if prev and prev["kind"] == "kq":
                     s = prev["s"]
-                    nc.vector.tensor_copy(
-                        out=hd[prev["h"]]["kT"][:, 512 * s:512 * (s + 1)].rearrange("w (c j y) -> w c y j", j=4, y=32),
-                        in_=prev["banks"][0][:].rearrange("w (c y j) -> w c y j", y=32, j=4),
-                    )
+                    for u in range(2):
+                        nc.vector.tensor_copy(
+                            out=hd[prev["h"]]["kT"][:, 512 * s:512 * (s + 1)].rearrange(
+                                "w (c u y e) -> w c u y e", u=2, y=32, e=2)[:, :, u],
+                            in_=prev["banks"][0][:].rearrange("w (c y u e) -> w c u y e", y=32, u=2, e=2)[:, :, u],
+                        )
                 if qn:
                     e_quant(qn)
                 if prev and prev["kind"] == "kq":

@@ -28,7 +28,7 @@ PINNED = True
 COPY_ON_VECTOR = ()
 LOAD_AHEAD = 6
 LAGS = (1, 3, 5, 6, 8, 10, 11)
-OUT_ON_VECTOR = True
+OUT_ON_VECTOR = False
 QT_ON_VECTOR = True
 
 
@@ -165,6 +165,10 @@ def tile_globallocalattention_t_kernel(tc, q, k, v, out):
                 in_=mf[:].rearrange("t (y u e) -> t y u e", u=2, e=2),
             )
             mask_bf[kind] = mb
+
+        warm = const.tile([P, 2], F32)
+        nc.vector.memset(warm[:], 0.0)
+        nc.scalar.activation(out=warm[:, 1:2], in_=warm[:, 0:1], func=ACT.Exp)
 
         e_bufs = [fixed.tile([P, 2, 2, 2 * P], BF16, name="e_sb%d" % i) for i in range(8)]
         is_zero = {}
@@ -490,9 +494,12 @@ def tile_globallocalattention_t_kernel(tc, q, k, v, out):
 
             for t in range(len(items) + l_out + 1):
                 ahead = [i for i in (range(LOAD_AHEAD + 1) if t == 0 else [t + LOAD_AHEAD]) if at(i, ("kq",))]
-                for i in ahead:
+                for i in ahead[:2]:
                     kq_load(items[i])
-                for i in ahead:
+                for i in ahead[:2]:
+                    v_load(items[i])
+                for i in ahead[2:]:
+                    kq_load(items[i])
                     v_load(items[i])
                 cur = at(t, ("unit", "gs", "kq"))
                 prev = at(t - l_pass, ("unit", "gs", "kq"))
@@ -536,10 +543,10 @@ def tile_globallocalattention_t_kernel(tc, q, k, v, out):
                         )
                 if qn:
                     e_quant(qn)
-                if prev and prev["kind"] == "kq":
-                    kq_regroup(prev)
                 if at(t - l_pass - 1, ("kq",)):
-                    kq_vquant(items[t - l_pass - 1])
+                    kq_regroup(items[t - l_pass - 1])
+                if at(t - l_pass - 2, ("kq",)):
+                    kq_vquant(items[t - l_pass - 2])
                 if cp and cp["copy_v"]:
                     e_copy(cp)
                 if prev and prev["kind"] == "unit":
@@ -550,10 +557,10 @@ def tile_globallocalattention_t_kernel(tc, q, k, v, out):
                     fin_rinv(mx)
                 if fo and OUT_ON_VECTOR:
                     fin_out(fo)
-                if prev and prev["kind"] == "kq" and QT_ON_VECTOR:
+                if prev and prev["kind"] == "kq" and QT_ON_VECTOR and t - l_pass >= 2:
                     s = prev["s"]
                     nc.vector.tensor_copy(out=hd[prev["h"]]["qT"][:, 512 * s:512 * (s + 1)], in_=prev["banks"][1][:])
-                if prev and prev["kind"] == "kq" and not QT_ON_VECTOR:
+                if prev and prev["kind"] == "kq" and not (QT_ON_VECTOR and t - l_pass >= 2):
                     s = prev["s"]
                     nc.scalar.copy(out=hd[prev["h"]]["qT"][:, 512 * s:512 * (s + 1)], in_=prev["banks"][1][:])
                 if ex:

@@ -29,7 +29,21 @@ COPY_ON_VECTOR = ()
 LOAD_AHEAD = 6
 LAGS = (1, 3, 5, 6, 8, 10, 11)
 OUT_ON_VECTOR = False
-QT_ON_VECTOR = True
+QT_ON_VECTOR = False
+RINV_LAG = 5
+DEAL_UNITS = 44
+GF_STEP = 3
+VQ_LAG = 7
+ZERO_LAG = 0
+RG_LAG = 4
+RG_SPLIT = 4
+OUT_WINDOW = 2
+COPY_RULE = 2
+OUT_RULE = 2
+GF_COPY_V = False
+OUT_V_NEAR_GF = 0
+REGROUP = "V"
+COMB = "V"
 
 
 def unit_plan(g):
@@ -91,36 +105,31 @@ def true_ranges(flags):
 
 
 def build_items():
-    seq = [{"kind": "kq", "h": 0, "s": 0}, {"kind": "kq", "h": 0, "s": 1}, {"kind": "nop"}]
-    for h in range(H):
-        for m in range(NSLAB):
-            units = [{"kind": "unit", "h": h, "g": g} for g in range(4 * m + 1, min(4 * m + 5, NCHUNK))]
-            extra = []
-            if h == 0:
-                if m + 2 < NSLAB:
-                    extra.append({"kind": "kq", "h": 0, "s": m + 2})
-                else:
-                    extra.append({"kind": "kq", "h": 1, "s": m + 2 - NSLAB})
-                extra.append({"kind": "gs", "h": 0, "s": m})
-            else:
-                for s in (2 * m + 2, 2 * m + 3):
-                    if s < NSLAB:
-                        extra.append({"kind": "kq", "h": 1, "s": s})
-                if m < 2:
-                    extra.extend([{"kind": "gf", "h": 0, "i": 2 * m}, {"kind": "gf", "h": 0, "i": 2 * m + 1}])
-                if 2 <= m <= 5:
-                    extra.extend([{"kind": "gs", "h": 1, "s": 2 * m - 4}, {"kind": "gs", "h": 1, "s": 2 * m - 3}])
-                if m == 6:
-                    extra.extend([{"kind": "gf", "h": 1, "i": i} for i in range(4)])
-            merged = []
-            for i in range(max(len(units), len(extra))):
-                if i < len(units):
-                    merged.append(units[i])
-                if i < len(extra):
-                    merged.append(extra[i])
-            if m + 1 < NSLAB:
-                merged[-1]["variants"] = (h, m + 1)
-            seq.extend(merged)
+    units = [{"kind": "unit", "h": h, "g": g} for h in range(H) for g in range(1, NCHUNK)]
+    kq = [[{"kind": "kq", "h": h, "s": s} for s in range(NSLAB)] for h in range(H)]
+    gs = [[{"kind": "gs", "h": h, "s": s} for s in range(NSLAB)] for h in range(H)]
+    gf = [[{"kind": "gf", "h": h, "i": i} for i in range(4)] for h in range(H)]
+    extras = []
+    for s in range(2, NSLAB):
+        extras.extend([kq[0][s], gs[0][s - 2]])
+    extras.extend([kq[1][0], gs[0][6], kq[1][1], gs[0][7]])
+    for i in range(3):
+        extras.extend([kq[1][2 + 2 * i], kq[1][3 + 2 * i], gf[0][i], gs[1][i]])
+    extras.extend([gf[0][3]] + gs[1][3:])
+    seq = [kq[0][0], kq[0][1], {"kind": "nop"}]
+    dealt = 0
+    last = 0
+    for n, u in enumerate(units):
+        seq.append(u)
+        if u["g"] % 4 == 0 and u["g"] // 4 < NSLAB:
+            u["variants"] = (u["h"], u["g"] // 4)
+        while dealt < len(extras) and dealt * DEAL_UNITS < (n + 1) * len(extras):
+            seq.append(extras[dealt])
+            dealt += 1
+        if dealt == len(extras) and last < 4 and n >= DEAL_UNITS + 1 + GF_STEP * last:
+            seq.append(gf[1][last])
+            last += 1
+    assert dealt == len(extras) and last == 4
     return seq
 
 
@@ -136,16 +145,21 @@ def tile_globallocalattention_t_kernel(tc, q, k, v, out):
         raw = ctx.enter_context(tc.tile_pool(name="raw", bufs=4))
         head = ctx.enter_context(tc.tile_pool(name="head", bufs=2))
         fixed = ctx.enter_context(tc.tile_pool(name="fixed", bufs=1))
-        vstage = ctx.enter_context(tc.tile_pool(name="vstage", bufs=2))
+        vstage = ctx.enter_context(tc.tile_pool(name="vstage", bufs=4))
         vvpool = ctx.enter_context(tc.tile_pool(name="vvpool", bufs=3))
         gstage = ctx.enter_context(tc.tile_pool(name="gstage", bufs=3))
         sstage = ctx.enter_context(tc.tile_pool(name="sstage", bufs=4))
         cpool = ctx.enter_context(tc.tile_pool(name="cpool", bufs=8))
-        opool = ctx.enter_context(tc.tile_pool(name="opool", bufs=3))
+        gcpool = ctx.enter_context(tc.tile_pool(name="gcpool", bufs=4))
+        opool = ctx.enter_context(tc.tile_pool(name="opool", bufs=4))
         small = ctx.enter_context(tc.tile_pool(name="small", bufs=8))
         ps_s = ctx.enter_context(tc.psum_pool(name="ps_s", bufs=4))
         ps_t = ctx.enter_context(tc.psum_pool(name="ps_t", bufs=2))
         ps_o = ctx.enter_context(tc.psum_pool(name="ps_o", bufs=2))
+
+        warm = const.tile([P, 2], F32)
+        nc.vector.memset(warm[:], 0.0)
+        nc.scalar.activation(out=warm[:, 1:2], in_=warm[:, 0:1], func=ACT.Exp)
 
         ident_bf = const.tile([P, P], BF16)
         make_identity(nc, ident_bf[:])
@@ -166,16 +180,14 @@ def tile_globallocalattention_t_kernel(tc, q, k, v, out):
             )
             mask_bf[kind] = mb
 
-        warm = const.tile([P, 2], F32)
-        nc.vector.memset(warm[:], 0.0)
-        nc.scalar.activation(out=warm[:, 1:2], in_=warm[:, 0:1], func=ACT.Exp)
-
         e_bufs = [fixed.tile([P, 2, 2, 2 * P], BF16, name="e_sb%d" % i) for i in range(8)]
         is_zero = {}
-        s_sb = fixed.tile([P, NSLAB, 2, 2 * P], F32)
+        s_sb = [fixed.tile([P, NSLAB, 2, 2 * P], F32, name="s_sb%d" % h) for h in range(H)]
         hd = {}
         vv = {}
-        gl = {}
+        gl = {0: {}, 1: {}}
+        vq_done = []
+        kq_done = []
 
         def head_alloc(h):
             qT = head.tile([P, S], F32, name="qT")
@@ -223,10 +235,17 @@ def tile_globallocalattention_t_kernel(tc, q, k, v, out):
 
         def kq_regroup(it):
             vgrp = vstage.tile([P, 4 * D], BF16, name="vgrp", align_bytes=64)
-            nc.vector.tensor_copy(
-                out=vgrp[:].rearrange("p (c i j) -> p c j i", i=4, j=4),
-                in_=it["v_raw"][:].rearrange("p (j c i) -> p c j i", j=4, i=4),
-            )
+            dst = vgrp[:].rearrange("p (c i j) -> p c j i", i=4, j=4)
+            src = it["v_raw"][:].rearrange("p (j c i) -> p c j i", j=4, i=4)
+            if REGROUP == "V":
+                nc.vector.tensor_copy(out=dst, in_=src)
+            else:
+                w = 64 // RG_SPLIT
+                for i in range(RG_SPLIT):
+                    nc.gpsimd.tensor_scalar(
+                        out=dst[:, w * i:w * (i + 1)], in0=src[:, w * i:w * (i + 1)], scalar1=1.0, scalar2=0.0,
+                        op0=ALU.mult, op1=ALU.add,
+                    )
             it["vgrp"] = vgrp
 
         def v_slab(h, slab, m):
@@ -237,6 +256,7 @@ def tile_globallocalattention_t_kernel(tc, q, k, v, out):
         def kq_vquant(it):
             codes, scales = v_slab(it["h"], ("L", it["s"]), None)
             nc.vector.quantize_mx(out=codes.bitcast(FP8X4), scales=scales, in_=it["vgrp"][:])
+            vq_done.append((it["h"], it["s"]))
 
         def build_variants(h, m):
             t = vvpool.tile([P, 4 * VW], U32, name="vvar", align_bytes=64)
@@ -250,6 +270,7 @@ def tile_globallocalattention_t_kernel(tc, q, k, v, out):
                     else:
                         pieces.append([qd, 1, a // 4, a % 4])
                 for q0, n, s, sq in pieces:
+                    assert (h, s) in vq_done
                     nc.sync.dma_start(
                         out=t[32 * q0:32 * (q0 + n), VW * slot:VW * (slot + 1)].bitcast(I32),
                         in_=vl[32 * sq:32 * (sq + n), VW * s:VW * (s + 1)].bitcast(I32),
@@ -271,7 +292,9 @@ def tile_globallocalattention_t_kernel(tc, q, k, v, out):
             t = hd[h]
             ps = ps_s.tile([P, 512], F32, name="s_ps")
             view = ps[:].rearrange("q (u c x) -> q u c x", u=2, x=64)
+            assert (h, "q", g // 4) in kq_done
             for q0, n, a0 in qk_runs(chunks):
+                assert (h, "k", (a0 + n - 1) // 4) in kq_done
                 dst = view[:, :, q0:q0 + n, :]
                 nc.tensor.matmul(
                     out=dst, lhsT=t["qv"][:, 0, P * g:P * (g + 1)], rhs=t["kv"][:, 0, :, a0:a0 + n, :],
@@ -312,7 +335,9 @@ def tile_globallocalattention_t_kernel(tc, q, k, v, out):
         def unit_comb(it):
             negm = small.tile([P, 1], F32, name="negm")
             mn = it["mn"]
-            if it["n_mn"] == 2:
+            if it["n_mn"] == 2 and COMB == "G":
+                nc.gpsimd.tensor_scalar(out=negm[:], in0=mn[:, 0:1], scalar1=mn[:, 1:2], scalar2=None, op0=ALU.min)
+            elif it["n_mn"] == 2:
                 nc.vector.tensor_tensor(out=negm[:], in0=mn[:, 0:1], in1=mn[:, 1:2], op=ALU.min)
             else:
                 nc.vector.tensor_reduce(out=negm[:], in_=mn[:, 0:it["n_mn"]], axis=AX.X, op=ALU.min)
@@ -321,41 +346,29 @@ def tile_globallocalattention_t_kernel(tc, q, k, v, out):
         def gs_pass(it):
             s = it["s"]
             if s == 0:
-                gl["mn"] = small.tile([P, NSLAB], F32, name="gmn")
+                gl[it["h"]]["mn"] = small.tile([P, NSLAB], F32, name="gmn")
             nc.vector.tensor_scalar(
-                out=s_sb[:, s], in0=it["banks"][0][:].rearrange("q (u x) -> q u x", u=2),
+                out=s_sb[it["h"]][:, s], in0=it["banks"][0][:].rearrange("q (u x) -> q u x", u=2),
                 scalar1=-SCALE, scalar2=None, op0=ALU.mult, op1=ALU.min,
-                accum_out=gl["mn"][:, s:s + 1],
+                accum_out=gl[it["h"]]["mn"][:, s:s + 1],
             )
 
         def gs_comb(it):
-            gl["negm"] = small.tile([P, 1], F32, name="gnegm")
-            nc.vector.tensor_reduce(out=gl["negm"][:], in_=gl["mn"][:], axis=AX.X, op=ALU.min)
+            gl[it["h"]]["negm"] = small.tile([P, 1], F32, name="gnegm")
+            nc.vector.tensor_reduce(out=gl[it["h"]]["negm"][:], in_=gl[it["h"]]["mn"][:], axis=AX.X, op=ALU.min)
 
         def whole(it):
             return all([en is not None for slab, chunks, ent in it["tiles"] for en in ent])
 
         def acc_init(grp):
-            grp["acc"] = small.tile([P, 4, 4], F32, name="acc")
+            grp["acc"] = small.tile([P, 4, 4], F32, name="acc" if grp["kind"] == "unit" else "gacc")
             grp["plain"] = all([whole(it) for it in grp["members"]])
             if not grp["plain"]:
                 nc.gpsimd.memset(grp["acc"][:], 0.0)
 
-        def e_exp(it):
+        def e_zero(it):
             bi = it["buf"]
             e_sb = e_bufs[bi]
-            acc = it["group"]["acc"]
-            negm = it["negm"] if it["kind"] == "unit" else gl["negm"]
-            n_acc = 0
-            if whole(it):
-                for ti in range(2):
-                    for qd in range(4):
-                        is_zero[(bi, ti, qd)] = False
-                nc.scalar.activation(
-                    out=e_sb[:], in_=it["src2"], func=ACT.Exp, bias=negm[:, 0:1], scale=-1.0,
-                    accum_out=acc[:, it["gidx"], 0:1],
-                )
-                return
             for ti, (slab, chunks, ent) in enumerate(it["tiles"]):
                 for qd in range(4):
                     if ent[qd] is None:
@@ -364,6 +377,20 @@ def tile_globallocalattention_t_kernel(tc, q, k, v, out):
                             is_zero[(bi, ti, qd)] = True
                     else:
                         is_zero[(bi, ti, qd)] = False
+
+        def e_exp(it):
+            bi = it["buf"]
+            e_sb = e_bufs[bi]
+            acc = it["group"]["acc"]
+            negm = it["negm"] if it["kind"] == "unit" else gl[it["h"]]["negm"]
+            n_acc = 0
+            if whole(it):
+                nc.scalar.activation(
+                    out=e_sb[:], in_=it["src2"], func=ACT.Exp, bias=negm[:, 0:1], scale=-1.0,
+                    accum_out=acc[:, it["gidx"], 0:1],
+                )
+                return
+            for ti, (slab, chunks, ent) in enumerate(it["tiles"]):
                 for q0, q1 in true_ranges([en is not None for en in ent]):
                     nc.scalar.activation(
                         out=e_sb[:, ti, :, 64 * q0:64 * q1], in_=it["src"](ti)[:, :, 64 * q0:64 * q1],
@@ -381,20 +408,20 @@ def tile_globallocalattention_t_kernel(tc, q, k, v, out):
                     nc.tensor.transpose(eT[:, ti, u, :], e_sb[:, ti, u, :].bitcast(F32), ident_f[:])
             it["eT"] = eT
 
-        def e_copy(it):
+        def e_copy(it, on_v):
             grp = gstage.tile([P, 2, P, 4], BF16, name="grp", align_bytes=64)
             src = it["eT"][:].rearrange("p t u q -> p t q u")
             dst = grp[:].rearrange("p t q j -> p (t q j)").bitcast(F32).rearrange("p (t q u) -> p t q u", t=2, u=2)
-            if it["copy_v"]:
+            if on_v:
                 nc.vector.tensor_copy(out=dst, in_=src)
             else:
                 nc.scalar.copy(out=dst, in_=src)
             it["grp"] = grp
 
         def e_quant(it):
-            tag = "c" if it["kind"] == "unit" else "gc"
-            codes = cpool.tile([P, 2 * P], U32, name="%s_codes" % tag, align_bytes=64)
-            scl = cpool.tile([P, 2 * P], U8, name="%s_scl" % tag, align_bytes=64)
+            pool = cpool if it["kind"] == "unit" else gcpool
+            codes = pool.tile([P, 2 * P], U32, name="codes", align_bytes=64)
+            scl = pool.tile([P, 2 * P], U8, name="scl", align_bytes=64)
             nc.vector.quantize_mx(
                 out=codes[:].bitcast(FP8X4), scales=scl[:], in_=it["grp"][:].rearrange("p t q j -> p (t q j)")
             )
@@ -436,11 +463,11 @@ def tile_globallocalattention_t_kernel(tc, q, k, v, out):
             grp["rinv"] = rinv
             grp["n_out"] = n
 
-        def fin_out(grp):
+        def fin_out(grp, on_v):
             n = grp["n_out"]
             o_sb = opool.tile([P, 2, D], F32, name="o_sb")
             for i in range(n):
-                if OUT_ON_VECTOR:
+                if on_v[i]:
                     nc.vector.tensor_scalar(
                         out=o_sb[:, i, :], in0=grp["o_ps"][:, i, :], scalar1=grp["rinv"][:, i:i + 1], scalar2=None,
                         op0=ALU.mult,
@@ -462,7 +489,7 @@ def tile_globallocalattention_t_kernel(tc, q, k, v, out):
             if it["kind"] not in ("unit", "gf"):
                 continue
             it["buf"] = cnt % 8
-            it["copy_v"] = (cnt % 8) in COPY_ON_VECTOR
+            it["copy_v"] = (cnt % 8) in COPY_ON_VECTOR or (GF_COPY_V and it["kind"] == "gf")
             cnt += 1
             if it["kind"] == "unit":
                 key = (it["h"], "unit", (it["g"] - 1) // 2)
@@ -472,12 +499,18 @@ def tile_globallocalattention_t_kernel(tc, q, k, v, out):
                 it["tiles"] = [
                     (("L", s), None, [(4 * s + c, None) for c in range(4)]) for s in (2 * it["i"], 2 * it["i"] + 1)
                 ]
-                it["src2"] = s_sb[:, 2 * it["i"]:2 * it["i"] + 2]
+                it["src2"] = s_sb[it["h"]][:, 2 * it["i"]:2 * it["i"] + 2]
             if key not in groups:
-                groups[key] = {"kind": it["kind"], "members": []}
+                groups[key] = {"kind": it["kind"], "members": [], "out_v": OUT_ON_VECTOR}
             it["group"] = groups[key]
             it["gidx"] = len(groups[key]["members"])
             groups[key]["members"].append(it)
+
+        for i, it in enumerate(items):
+            if it["kind"] == "gf":
+                for j in range(max(i - OUT_V_NEAR_GF, 0), i):
+                    if items[j]["kind"] == "unit":
+                        items[j]["group"]["out_v"] = True
 
         def at(i, kinds):
             if 0 <= i < len(items) and items[i]["kind"] in kinds:
@@ -494,12 +527,9 @@ def tile_globallocalattention_t_kernel(tc, q, k, v, out):
 
             for t in range(len(items) + l_out + 1):
                 ahead = [i for i in (range(LOAD_AHEAD + 1) if t == 0 else [t + LOAD_AHEAD]) if at(i, ("kq",))]
-                for i in ahead[:2]:
+                for i in ahead:
                     kq_load(items[i])
-                for i in ahead[:2]:
-                    v_load(items[i])
-                for i in ahead[2:]:
-                    kq_load(items[i])
+                for i in ahead:
                     v_load(items[i])
                 cur = at(t, ("unit", "gs", "kq"))
                 prev = at(t - l_pass, ("unit", "gs", "kq"))
@@ -509,6 +539,18 @@ def tile_globallocalattention_t_kernel(tc, q, k, v, out):
                 qn = at(t - l_qn, e_kinds)
                 mx = group_done(t - l_mx)
                 fo = group_done(t - l_out)
+                rv = group_done(t - RINV_LAG)
+                v_idle = prev is None
+                v_extra = any([at(t - l_pass - d, ("kq", "gs")) is not None for d in range(OUT_WINDOW)])
+                cp_v = v_idle if COPY_RULE == 2 else False
+                if OUT_RULE == 0:
+                    fo_v = (False, False)
+                elif OUT_RULE == 1:
+                    fo_v = (True, True) if v_idle else ((False, False) if v_extra else (True, False))
+                elif OUT_RULE == 2:
+                    fo_v = (True, True) if v_idle else (False, False)
+                else:
+                    fo_v = (False, False) if v_extra else (True, True)
                 if tr:
                     e_transpose(tr)
                 if cur and cur["kind"] == "unit":
@@ -526,15 +568,18 @@ def tile_globallocalattention_t_kernel(tc, q, k, v, out):
                         kq_transpose(cur)
                     if mx:
                         fin_mx(mx)
-                nxt = at(t - l_exp + 1, e_kinds)
+                nxt = at(t - ZERO_LAG, e_kinds)
                 if nxt and nxt["gidx"] == 0:
                     acc_init(nxt["group"])
+                if nxt:
+                    e_zero(nxt)
                 if prev and prev["kind"] == "unit":
                     unit_pass(prev)
                 if prev and prev["kind"] == "gs":
                     gs_pass(prev)
                 if prev and prev["kind"] == "kq":
                     s = prev["s"]
+                    kq_done.extend([(prev["h"], "k", s), (prev["h"], "q", s)])
                     for u in range(2):
                         nc.vector.tensor_copy(
                             out=hd[prev["h"]]["kT"][:, 512 * s:512 * (s + 1)].rearrange(
@@ -543,33 +588,33 @@ def tile_globallocalattention_t_kernel(tc, q, k, v, out):
                         )
                 if qn:
                     e_quant(qn)
-                if at(t - l_pass - 1, ("kq",)):
-                    kq_regroup(items[t - l_pass - 1])
-                if at(t - l_pass - 2, ("kq",)):
-                    kq_vquant(items[t - l_pass - 2])
-                if cp and cp["copy_v"]:
-                    e_copy(cp)
+                if at(t - RG_LAG, ("kq",)):
+                    kq_regroup(items[t - RG_LAG])
+                if at(t - VQ_LAG, ("kq",)):
+                    kq_vquant(items[t - VQ_LAG])
+                if cp and cp_v:
+                    e_copy(cp, True)
                 if prev and prev["kind"] == "unit":
                     unit_comb(prev)
                 if prev and prev["kind"] == "gs" and prev["s"] == NSLAB - 1:
                     gs_comb(prev)
-                if mx:
-                    fin_rinv(mx)
-                if fo and OUT_ON_VECTOR:
-                    fin_out(fo)
+                if rv:
+                    fin_rinv(rv)
+                if fo and fo_v[0]:
+                    fin_out(fo, fo_v)
                 if prev and prev["kind"] == "kq" and QT_ON_VECTOR and t - l_pass >= 2:
                     s = prev["s"]
                     nc.vector.tensor_copy(out=hd[prev["h"]]["qT"][:, 512 * s:512 * (s + 1)], in_=prev["banks"][1][:])
                 if prev and prev["kind"] == "kq" and not (QT_ON_VECTOR and t - l_pass >= 2):
                     s = prev["s"]
                     nc.scalar.copy(out=hd[prev["h"]]["qT"][:, 512 * s:512 * (s + 1)], in_=prev["banks"][1][:])
+                if cp and not cp_v:
+                    e_copy(cp, False)
                 if ex:
                     e_exp(ex)
-                if cp and not cp["copy_v"]:
-                    e_copy(cp)
-                if fo and not OUT_ON_VECTOR:
-                    fin_out(fo)
-                i = t - l_pass - 2
+                if fo and not fo_v[0]:
+                    fin_out(fo, fo_v)
+                i = t - VQ_LAG
                 if 0 <= i < len(items) and "variants" in items[i]:
                     build_variants(items[i]["variants"][0], items[i]["variants"][1])
 

@@ -31,6 +31,12 @@ LAGS = (1, 3, 5, 6, 8, 10, 11)
 OUT_ON_VECTOR = False
 QT_ON_VECTOR = False
 RINV_LAG = 5
+PASS_MODE = "two"
+ROWS2K = False
+TAIL_SPLIT = False
+VAR_G = 0
+T_WEAVE = False
+KT_ON_SCALAR = False
 DEAL_UNITS = 44
 GF_STEP = 3
 VQ_LAG = 7
@@ -42,7 +48,7 @@ COPY_RULE = 2
 OUT_RULE = 2
 GF_COPY_V = False
 OUT_V_NEAR_GF = 0
-REGROUP = "V"
+REGROUP = "G"
 COMB = "V"
 
 
@@ -121,8 +127,8 @@ def build_items():
     last = 0
     for n, u in enumerate(units):
         seq.append(u)
-        if u["g"] % 4 == 0 and u["g"] // 4 < NSLAB:
-            u["variants"] = (u["h"], u["g"] // 4)
+        if u["g"] % 4 == VAR_G and u["g"] // 4 + (1 if VAR_G else 0) < NSLAB:
+            u["variants"] = (u["h"], u["g"] // 4 + (1 if VAR_G else 0))
         while dealt < len(extras) and dealt * DEAL_UNITS < (n + 1) * len(extras):
             seq.append(extras[dealt])
             dealt += 1
@@ -153,7 +159,7 @@ def tile_globallocalattention_t_kernel(tc, q, k, v, out):
         gcpool = ctx.enter_context(tc.tile_pool(name="gcpool", bufs=4))
         opool = ctx.enter_context(tc.tile_pool(name="opool", bufs=4))
         small = ctx.enter_context(tc.tile_pool(name="small", bufs=8))
-        ps_s = ctx.enter_context(tc.psum_pool(name="ps_s", bufs=4))
+        ps_s = ctx.enter_context(tc.psum_pool(name="ps_s", bufs=2 if PASS_MODE == "wide" else 4))
         ps_t = ctx.enter_context(tc.psum_pool(name="ps_t", bufs=2))
         ps_o = ctx.enter_context(tc.psum_pool(name="ps_o", bufs=2))
 
@@ -198,6 +204,7 @@ def tile_globallocalattention_t_kernel(tc, q, k, v, out):
                 "qT": qT, "kT": kT, "vl": vl,
                 "qv": qT[:].bitcast(BF16).rearrange("p (r e) -> p e r", e=2),
                 "kv": kT[:].bitcast(BF16).rearrange("p (c u x h) -> p h u c x", u=2, x=64, h=2),
+                "kv2": kT[:].bitcast(BF16).rearrange("p (s u c x h) -> p h s u c x", u=2, c=4, x=64, h=2),
             }
 
         def kq_load(it):
@@ -207,14 +214,18 @@ def tile_globallocalattention_t_kernel(tc, q, k, v, out):
             r0 = h * S + 512 * s
             it["k_raw"] = raw.tile([P, 4 * D], BF16, name="k_raw")
             it["q_raw"] = raw.tile([P, 4 * D], BF16, name="q_raw")
-            nc.sync.dma_start(
-                out=it["k_raw"][:].rearrange("p (t d) -> p t d", t=4),
-                in_=kf[r0:r0 + 512, :].rearrange("(t p) d -> p t d", p=P),
-            )
-            nc.sync.dma_start(
-                out=it["q_raw"][:].rearrange("p (t d) -> p t d", t=4),
-                in_=qf[r0:r0 + 512, :].rearrange("(t p) d -> p t d", p=P),
-            )
+            if ROWS2K:
+                nc.sync.dma_start(out=it["k_raw"][:], in_=kf[r0:r0 + 512, :].rearrange("(p t) d -> p (t d)", t=4))
+                nc.sync.dma_start(out=it["q_raw"][:], in_=qf[r0:r0 + 512, :].rearrange("(p t) d -> p (t d)", t=4))
+            else:
+                nc.sync.dma_start(
+                    out=it["k_raw"][:].rearrange("p (t d) -> p t d", t=4),
+                    in_=kf[r0:r0 + 512, :].rearrange("(t p) d -> p t d", p=P),
+                )
+                nc.sync.dma_start(
+                    out=it["q_raw"][:].rearrange("p (t d) -> p t d", t=4),
+                    in_=qf[r0:r0 + 512, :].rearrange("(t p) d -> p t d", p=P),
+                )
 
         def v_load(it):
             r0 = it["h"] * S + 512 * it["s"]
@@ -225,8 +236,13 @@ def tile_globallocalattention_t_kernel(tc, q, k, v, out):
 
         def kq_transpose(it):
             it["banks"] = []
-            for src in (it["k_raw"], it["q_raw"]):
-                ps = ps_s.tile([P, 512], F32, name="s_ps")
+            if PASS_MODE == "wide":
+                both = ps_s.tile([P, 1024], F32, name="s_ps")
+            for half, src in enumerate((it["k_raw"], it["q_raw"])):
+                if PASS_MODE == "wide":
+                    ps = both[:, 512 * half:512 * (half + 1)]
+                else:
+                    ps = ps_s.tile([P, 512], F32, name="s_ps")
                 for i in range(4):
                     nc.tensor.transpose(
                         ps[:, P * i:P * (i + 1)], src[:].bitcast(F32)[:, P * i:P * (i + 1)], ident_f[:]
@@ -288,51 +304,105 @@ def tile_globallocalattention_t_kernel(tc, q, k, v, out):
                     runs.append([qd, 1, a])
             return runs
 
-        def qk_bank(h, g, chunks, masks):
+        def k_cols(t, half, a0, n):
+            if ROWS2K:
+                assert a0 // 4 == (a0 + n - 1) // 4
+                return t["kv2"][:, half, a0 // 4, :, a0 % 4:a0 % 4 + n, :]
+            return t["kv"][:, half, :, a0:a0 + n, :]
+
+        def qt_copy(it, copy):
+            dst = hd[it["h"]]["qT"][:, 512 * it["s"]:512 * (it["s"] + 1)]
+            if ROWS2K:
+                copy(out=dst.rearrange("w (p t) -> w p t", t=4), in_=it["banks"][1][:].rearrange("w (t p) -> w p t", t=4))
+            else:
+                copy(out=dst, in_=it["banks"][1][:])
+
+        def kt_copy(it, copy):
+            dst = hd[it["h"]]["kT"][:, 512 * it["s"]:512 * (it["s"] + 1)]
+            if ROWS2K:
+                copy(
+                    out=dst.rearrange("w (u p e) -> w u p e", u=2, e=2),
+                    in_=it["banks"][0][:].rearrange("w (u e p) -> w u p e", u=2, e=2),
+                )
+            else:
+                for u in range(2):
+                    copy(
+                        out=dst.rearrange("w (c u y e) -> w c u y e", u=2, y=32, e=2)[:, :, u],
+                        in_=it["banks"][0][:].rearrange("w (c y u e) -> w c u y e", y=32, u=2, e=2)[:, :, u],
+                    )
+
+        def qk_bank(h, g, chunks, masks, bank=None):
             t = hd[h]
-            ps = ps_s.tile([P, 512], F32, name="s_ps")
+            ps = bank if bank is not None else ps_s.tile([P, 512], F32, name="s_ps")
             view = ps[:].rearrange("q (u c x) -> q u c x", u=2, x=64)
             assert (h, "q", g // 4) in kq_done
+            calls = []
             for q0, n, a0 in qk_runs(chunks):
                 assert (h, "k", (a0 + n - 1) // 4) in kq_done
                 dst = view[:, :, q0:q0 + n, :]
-                nc.tensor.matmul(
-                    out=dst, lhsT=t["qv"][:, 0, P * g:P * (g + 1)], rhs=t["kv"][:, 0, :, a0:a0 + n, :],
-                    start=True, stop=False,
-                )
+                calls.append({
+                    "out": dst, "lhsT": t["qv"][:, 0, P * g:P * (g + 1)], "rhs": k_cols(t, 0, a0, n),
+                    "start": True, "stop": False,
+                })
                 for qd in range(q0, q0 + n):
                     if masks[qd] is not None:
-                        nc.tensor.matmul(
-                            out=view[:, :, qd, :], lhsT=ident_bf[:],
-                            rhs=mask_bf[masks[qd]][:].rearrange("t (u x) -> t u x", u=2),
-                            start=False, stop=False,
-                        )
-                nc.tensor.matmul(
-                    out=dst, lhsT=t["qv"][:, 1, P * g:P * (g + 1)], rhs=t["kv"][:, 1, :, a0:a0 + n, :],
-                    start=False, stop=True,
-                )
-            return ps
+                        calls.append({
+                            "out": view[:, :, qd, :], "lhsT": ident_bf[:],
+                            "rhs": mask_bf[masks[qd]][:].rearrange("t (u x) -> t u x", u=2),
+                            "start": False, "stop": False,
+                        })
+                calls.append({
+                    "out": dst, "lhsT": t["qv"][:, 1, P * g:P * (g + 1)], "rhs": k_cols(t, 1, a0, n),
+                    "start": False, "stop": True,
+                })
+            return ps, calls
 
-        def unit_pass(it):
+        def run_calls(calls):
+            for c in calls:
+                if "in_" in c:
+                    nc.tensor.transpose(c["out"], c["in_"], ident_f[:])
+                else:
+                    nc.tensor.matmul(**c)
+
+        def unit_pieces(it):
             pieces = []
             for ti, (slab, chunks, ent) in enumerate(it["tiles"]):
                 for q0, q1 in true_ranges([en is not None for en in ent]):
                     pieces.append((ti, q0, q1))
-            mn = small.tile([P, 8], F32, name="mn")
-            s_u = sstage.tile([P, 2, 2, 2 * P], F32, name="s_u")
-            for i, (ti, q0, q1) in enumerate(pieces):
-                nc.vector.tensor_scalar(
-                    out=s_u[:, ti, :, 64 * q0:64 * q1],
-                    in0=it["banks"][ti][:].rearrange("q (u x) -> q u x", u=2)[:, :, 64 * q0:64 * q1],
-                    scalar1=-SCALE, scalar2=None, op0=ALU.mult, op1=ALU.min,
-                    accum_out=mn[:, i:i + 1],
-                )
-            it["mn"] = mn
+            return pieces
+
+        def unit_pass(it, first):
+            pieces = unit_pieces(it)
+            if first:
+                it["mn"] = small.tile([P, 8], F32, name="mn")
+                it["s_u"] = sstage.tile([P, 2, 2, 2 * P], F32, name="s_u")
+            mn = it["mn"]
+            s_u = it["s_u"]
+            if PASS_MODE == "wide" and whole(it):
+                if first:
+                    nc.vector.tensor_scalar(
+                        out=s_u[:].rearrange("q t u x -> q (t u x)"), in0=it["wide"][:],
+                        scalar1=-SCALE, scalar2=None, op0=ALU.mult, op1=ALU.min, accum_out=mn[:, 0:1],
+                    )
+                pieces = pieces[:1]
+            else:
+                for i, (ti, q0, q1) in enumerate(pieces):
+                    if (i == 0) != first:
+                        continue
+                    nc.vector.tensor_scalar(
+                        out=s_u[:, ti, :, 64 * q0:64 * q1],
+                        in0=it["banks"][ti][:].rearrange("q (u x) -> q u x", u=2)[:, :, 64 * q0:64 * q1],
+                        scalar1=-SCALE, scalar2=(mn[:, i - 1:i] if PASS_MODE == "chain" and i > 0 else None),
+                        op0=ALU.mult, op1=ALU.min, accum_out=mn[:, i:i + 1],
+                    )
             it["n_mn"] = len(pieces)
             it["src"] = lambda ti: s_u[:, ti]
             it["src2"] = s_u[:]
 
         def unit_comb(it):
+            if PASS_MODE == "chain" or it["n_mn"] == 1:
+                it["negm"] = it["mn"][:, it["n_mn"] - 1:it["n_mn"]]
+                return
             negm = small.tile([P, 1], F32, name="negm")
             mn = it["mn"]
             if it["n_mn"] == 2 and COMB == "G":
@@ -403,10 +473,10 @@ def tile_globallocalattention_t_kernel(tc, q, k, v, out):
         def e_transpose(it):
             e_sb = e_bufs[it["buf"]]
             eT = ps_t.tile([P, 2, 2, P], F32, name="eT")
-            for ti in range(2):
-                for u in range(2):
-                    nc.tensor.transpose(eT[:, ti, u, :], e_sb[:, ti, u, :].bitcast(F32), ident_f[:])
             it["eT"] = eT
+            return [
+                {"out": eT[:, ti, u, :], "in_": e_sb[:, ti, u, :].bitcast(F32)} for ti in range(2) for u in range(2)
+            ]
 
         def e_copy(it, on_v):
             grp = gstage.tile([P, 2, P, 4], BF16, name="grp", align_bytes=64)
@@ -542,28 +612,50 @@ def tile_globallocalattention_t_kernel(tc, q, k, v, out):
                 rv = group_done(t - RINV_LAG)
                 v_idle = prev is None
                 v_extra = any([at(t - l_pass - d, ("kq", "gs")) is not None for d in range(OUT_WINDOW)])
-                cp_v = v_idle if COPY_RULE == 2 else False
+                s_idle = ex is None
+                cp_v = (v_idle and not (s_idle and TAIL_SPLIT)) if COPY_RULE == 2 else False
                 if OUT_RULE == 0:
                     fo_v = (False, False)
                 elif OUT_RULE == 1:
                     fo_v = (True, True) if v_idle else ((False, False) if v_extra else (True, False))
+                    if v_idle and s_idle and TAIL_SPLIT:
+                        fo_v = (True, False)
                 elif OUT_RULE == 2:
                     fo_v = (True, True) if v_idle else (False, False)
                 else:
                     fo_v = (False, False) if v_extra else (True, True)
-                if tr:
-                    e_transpose(tr)
+                trs = e_transpose(tr) if tr else []
                 if cur and cur["kind"] == "unit":
                     ch = [[(en[0] if en else None) for en in ent] for slab, chunks, ent in cur["tiles"]]
                     mk = [[(en[1] if en else None) for en in ent] for slab, chunks, ent in cur["tiles"]]
-                    cur["banks"] = [qk_bank(cur["h"], cur["g"], ch[0], mk[0])]
-                    if mx:
-                        fin_mx(mx)
-                    cur["banks"].append(qk_bank(cur["h"], cur["g"], ch[1], mk[1]))
+                    if PASS_MODE == "wide":
+                        cur["wide"] = ps_s.tile([P, 1024], F32, name="s_ps")
+                        bank_a, calls_a = qk_bank(cur["h"], cur["g"], ch[0], mk[0], cur["wide"][:, 0:512])
+                        bank_b, calls_b = qk_bank(cur["h"], cur["g"], ch[1], mk[1], cur["wide"][:, 512:1024])
+                    else:
+                        bank_a, calls_a = qk_bank(cur["h"], cur["g"], ch[0], mk[0])
+                        bank_b, calls_b = qk_bank(cur["h"], cur["g"], ch[1], mk[1])
+                    cur["banks"] = [bank_a, bank_b]
+                    if T_WEAVE:
+                        run_calls(trs[0:1] + calls_a[0:1] + trs[1:2] + calls_a[1:])
+                        if mx:
+                            fin_mx(mx)
+                        run_calls(calls_b[0:1] + trs[2:3] + calls_b[1:2] + trs[3:4] + calls_b[2:])
+                    else:
+                        run_calls(trs + calls_a)
+                        if mx:
+                            fin_mx(mx)
+                        run_calls(calls_b)
                 else:
+                    run_calls(trs)
                     if cur and cur["kind"] == "gs":
                         s = cur["s"]
-                        cur["banks"] = [qk_bank(cur["h"], 0, [4 * s, 4 * s + 1, 4 * s + 2, 4 * s + 3], [None] * 4)]
+                        bank_a, calls_a = qk_bank(
+                            cur["h"], 0, [4 * s, 4 * s + 1, 4 * s + 2, 4 * s + 3], [None] * 4,
+                            ps_s.tile([P, 1024], F32, name="s_ps")[:, 0:512] if PASS_MODE == "wide" else None,
+                        )
+                        cur["banks"] = [bank_a]
+                        run_calls(calls_a)
                     if cur and cur["kind"] == "kq":
                         kq_transpose(cur)
                     if mx:
@@ -574,20 +666,19 @@ def tile_globallocalattention_t_kernel(tc, q, k, v, out):
                 if nxt:
                     e_zero(nxt)
                 if prev and prev["kind"] == "unit":
-                    unit_pass(prev)
+                    unit_pass(prev, True)
+                    if PASS_MODE != "chain":
+                        unit_pass(prev, False)
                 if prev and prev["kind"] == "gs":
                     gs_pass(prev)
                 if prev and prev["kind"] == "kq":
                     s = prev["s"]
                     kq_done.extend([(prev["h"], "k", s), (prev["h"], "q", s)])
-                    for u in range(2):
-                        nc.vector.tensor_copy(
-                            out=hd[prev["h"]]["kT"][:, 512 * s:512 * (s + 1)].rearrange(
-                                "w (c u y e) -> w c u y e", u=2, y=32, e=2)[:, :, u],
-                            in_=prev["banks"][0][:].rearrange("w (c y u e) -> w c u y e", y=32, u=2, e=2)[:, :, u],
-                        )
+                    kt_copy(prev, nc.scalar.copy if KT_ON_SCALAR else nc.vector.tensor_copy)
                 if qn:
                     e_quant(qn)
+                if prev and prev["kind"] == "unit" and PASS_MODE == "chain":
+                    unit_pass(prev, False)
                 if at(t - RG_LAG, ("kq",)):
                     kq_regroup(items[t - RG_LAG])
                 if at(t - VQ_LAG, ("kq",)):
@@ -603,11 +694,9 @@ def tile_globallocalattention_t_kernel(tc, q, k, v, out):
                 if fo and fo_v[0]:
                     fin_out(fo, fo_v)
                 if prev and prev["kind"] == "kq" and QT_ON_VECTOR and t - l_pass >= 2:
-                    s = prev["s"]
-                    nc.vector.tensor_copy(out=hd[prev["h"]]["qT"][:, 512 * s:512 * (s + 1)], in_=prev["banks"][1][:])
+                    qt_copy(prev, nc.vector.tensor_copy)
                 if prev and prev["kind"] == "kq" and not (QT_ON_VECTOR and t - l_pass >= 2):
-                    s = prev["s"]
-                    nc.scalar.copy(out=hd[prev["h"]]["qT"][:, 512 * s:512 * (s + 1)], in_=prev["banks"][1][:])
+                    qt_copy(prev, nc.scalar.copy)
                 if cp and not cp_v:
                     e_copy(cp, False)
                 if ex:

@@ -31,11 +31,14 @@ LAGS = (1, 3, 5, 6, 8, 10, 11)
 OUT_ON_VECTOR = False
 QT_ON_VECTOR = False
 RINV_LAG = 5
+QT_V_FROM = None
+GAMMA = 1.0
+QPLANES = False
 PASS_MODE = "two"
 ROWS2K = False
 TAIL_SPLIT = False
 VAR_G = 0
-T_WEAVE = False
+T_WEAVE = True
 KT_ON_SCALAR = False
 DEAL_UNITS = 44
 GF_STEP = 3
@@ -129,7 +132,7 @@ def build_items():
         seq.append(u)
         if u["g"] % 4 == VAR_G and u["g"] // 4 + (1 if VAR_G else 0) < NSLAB:
             u["variants"] = (u["h"], u["g"] // 4 + (1 if VAR_G else 0))
-        while dealt < len(extras) and dealt * DEAL_UNITS < (n + 1) * len(extras):
+        while dealt < len(extras) and DEAL_UNITS * (dealt / len(extras)) ** GAMMA < n + 1:
             seq.append(extras[dealt])
             dealt += 1
         if dealt == len(extras) and last < 4 and n >= DEAL_UNITS + 1 + GF_STEP * last:
@@ -202,7 +205,7 @@ def tile_globallocalattention_t_kernel(tc, q, k, v, out):
             nc.vector.memset(vl[:].bitcast(I32).rearrange("p (s w) -> p s w", w=VW)[:, :, D:VW], 0)
             hd[h] = {
                 "qT": qT, "kT": kT, "vl": vl,
-                "qv": qT[:].bitcast(BF16).rearrange("p (r e) -> p e r", e=2),
+                "qv": qT[:].bitcast(BF16).rearrange("p (e r) -> p e r" if QPLANES else "p (r e) -> p e r", e=2),
                 "kv": kT[:].bitcast(BF16).rearrange("p (c u x h) -> p h u c x", u=2, x=64, h=2),
                 "kv2": kT[:].bitcast(BF16).rearrange("p (s u c x h) -> p h s u c x", u=2, c=4, x=64, h=2),
             }
@@ -312,7 +315,15 @@ def tile_globallocalattention_t_kernel(tc, q, k, v, out):
 
         def qt_copy(it, copy):
             dst = hd[it["h"]]["qT"][:, 512 * it["s"]:512 * (it["s"] + 1)]
-            if ROWS2K:
+            if QPLANES:
+                for hh in range(2):
+                    pl = hd[it["h"]]["qv"][:, hh, 512 * it["s"]:512 * (it["s"] + 1)]
+                    src = it["banks"][1][:].bitcast(BF16)
+                    if ROWS2K:
+                        copy(out=pl.rearrange("w (p t) -> w p t", t=4), in_=src.rearrange("w (t p h) -> w h p t", t=4, h=2)[:, hh])
+                    else:
+                        copy(out=pl, in_=src.rearrange("w (c h) -> w h c", h=2)[:, hh])
+            elif ROWS2K:
                 copy(out=dst.rearrange("w (p t) -> w p t", t=4), in_=it["banks"][1][:].rearrange("w (t p) -> w p t", t=4))
             else:
                 copy(out=dst, in_=it["banks"][1][:])
@@ -622,6 +633,9 @@ def tile_globallocalattention_t_kernel(tc, q, k, v, out):
                         fo_v = (True, False)
                 elif OUT_RULE == 2:
                     fo_v = (True, True) if v_idle else (False, False)
+                elif OUT_RULE == 4:
+                    alt = fo is not None and fo["kind"] == "unit" and ((fo["members"][0]["g"] - 1) // 2) % 2 == 0
+                    fo_v = (True, True) if (v_idle or (alt and not v_extra)) else (False, False)
                 else:
                     fo_v = (False, False) if v_extra else (True, True)
                 trs = e_transpose(tr) if tr else []
@@ -693,9 +707,10 @@ def tile_globallocalattention_t_kernel(tc, q, k, v, out):
                     fin_rinv(rv)
                 if fo and fo_v[0]:
                     fin_out(fo, fo_v)
-                if prev and prev["kind"] == "kq" and QT_ON_VECTOR and t - l_pass >= 2:
+                qt_v = prev is not None and prev["kind"] == "kq" and ((QT_ON_VECTOR and t - l_pass >= 2) or (QT_V_FROM is not None and (prev["h"], prev["s"]) >= QT_V_FROM))
+                if qt_v:
                     qt_copy(prev, nc.vector.tensor_copy)
-                if prev and prev["kind"] == "kq" and not (QT_ON_VECTOR and t - l_pass >= 2):
+                if prev and prev["kind"] == "kq" and not qt_v:
                     qt_copy(prev, nc.scalar.copy)
                 if cp and not cp_v:
                     e_copy(cp, False)

@@ -31,18 +31,19 @@ LAGS = (1, 3, 5, 6, 8, 10, 11)
 OUT_ON_VECTOR = False
 QT_ON_VECTOR = False
 RINV_LAG = 5
+VRAW_BUFS = 4
 QT_V_FROM = None
 GAMMA = 1.0
 QPLANES = False
 PASS_MODE = "two"
-ROWS2K = False
+ROWS2K = True
 TAIL_SPLIT = False
-VAR_G = 0
+VAR_G = 2
 T_WEAVE = True
 KT_ON_SCALAR = False
 DEAL_UNITS = 44
 GF_STEP = 3
-VQ_LAG = 7
+VQ_LAG = 9
 ZERO_LAG = 0
 RG_LAG = 4
 RG_SPLIT = 4
@@ -152,9 +153,10 @@ def tile_globallocalattention_t_kernel(tc, q, k, v, out):
     with ExitStack() as ctx:
         const = ctx.enter_context(tc.tile_pool(name="const", bufs=1))
         raw = ctx.enter_context(tc.tile_pool(name="raw", bufs=4))
+        vraw = ctx.enter_context(tc.tile_pool(name="vraw", bufs=VRAW_BUFS))
         head = ctx.enter_context(tc.tile_pool(name="head", bufs=2))
         fixed = ctx.enter_context(tc.tile_pool(name="fixed", bufs=1))
-        vstage = ctx.enter_context(tc.tile_pool(name="vstage", bufs=4))
+        vstage = ctx.enter_context(tc.tile_pool(name="vstage", bufs=VRAW_BUFS))
         vvpool = ctx.enter_context(tc.tile_pool(name="vvpool", bufs=3))
         gstage = ctx.enter_context(tc.tile_pool(name="gstage", bufs=3))
         sstage = ctx.enter_context(tc.tile_pool(name="sstage", bufs=4))
@@ -170,10 +172,10 @@ def tile_globallocalattention_t_kernel(tc, q, k, v, out):
         nc.vector.memset(warm[:], 0.0)
         nc.scalar.activation(out=warm[:, 1:2], in_=warm[:, 0:1], func=ACT.Exp)
 
-        ident_bf = const.tile([P, P], BF16)
-        make_identity(nc, ident_bf[:])
         ident_f = const.tile([P, P], F32)
         make_identity(nc, ident_f[:])
+        ident_bf = const.tile([P, P], BF16)
+        make_identity(nc, ident_bf[:])
         mask_bf = {}
         for kind, sign in (("U", 1), ("L", -1)):
             mf = const.tile([P, P], F32, name="mask_f_%s" % kind)
@@ -232,7 +234,7 @@ def tile_globallocalattention_t_kernel(tc, q, k, v, out):
 
         def v_load(it):
             r0 = it["h"] * S + 512 * it["s"]
-            it["v_raw"] = raw.tile([P, 4 * D], BF16, name="v_raw")
+            it["v_raw"] = vraw.tile([P, 4 * D], BF16, name="v_raw")
             nc.sync.dma_start(
                 out=it["v_raw"][:], in_=vf[r0:r0 + 512, :].rearrange("(p j) d -> p (j d)", j=4)
             )

@@ -31,6 +31,9 @@ LAGS = (1, 3, 5, 6, 8, 10, 11)
 OUT_ON_VECTOR = False
 QT_ON_VECTOR = False
 RINV_LAG = 5
+BANKS = (4, 2, 2)
+COPY_V_H1 = ()
+KT_S_UNTIL = (0, 8)
 VRAW_BUFS = 4
 QT_V_FROM = None
 GAMMA = 1.0
@@ -164,9 +167,9 @@ def tile_globallocalattention_t_kernel(tc, q, k, v, out):
         gcpool = ctx.enter_context(tc.tile_pool(name="gcpool", bufs=4))
         opool = ctx.enter_context(tc.tile_pool(name="opool", bufs=4))
         small = ctx.enter_context(tc.tile_pool(name="small", bufs=8))
-        ps_s = ctx.enter_context(tc.psum_pool(name="ps_s", bufs=2 if PASS_MODE == "wide" else 4))
-        ps_t = ctx.enter_context(tc.psum_pool(name="ps_t", bufs=2))
-        ps_o = ctx.enter_context(tc.psum_pool(name="ps_o", bufs=2))
+        ps_s = ctx.enter_context(tc.psum_pool(name="ps_s", bufs=2 if PASS_MODE == "wide" else BANKS[0]))
+        ps_t = ctx.enter_context(tc.psum_pool(name="ps_t", bufs=BANKS[1]))
+        ps_o = ctx.enter_context(tc.psum_pool(name="ps_o", bufs=BANKS[2]))
 
         warm = const.tile([P, 2], F32)
         nc.vector.memset(warm[:], 0.0)
@@ -627,6 +630,8 @@ def tile_globallocalattention_t_kernel(tc, q, k, v, out):
                 v_extra = any([at(t - l_pass - d, ("kq", "gs")) is not None for d in range(OUT_WINDOW)])
                 s_idle = ex is None
                 cp_v = (v_idle and not (s_idle and TAIL_SPLIT)) if COPY_RULE == 2 else False
+                if cp and cp["h"] == 1 and cp["buf"] in COPY_V_H1:
+                    cp_v = True
                 if OUT_RULE == 0:
                     fo_v = (False, False)
                 elif OUT_RULE == 1:
@@ -690,7 +695,8 @@ def tile_globallocalattention_t_kernel(tc, q, k, v, out):
                 if prev and prev["kind"] == "kq":
                     s = prev["s"]
                     kq_done.extend([(prev["h"], "k", s), (prev["h"], "q", s)])
-                    kt_copy(prev, nc.scalar.copy if KT_ON_SCALAR else nc.vector.tensor_copy)
+                    kt_s = KT_ON_SCALAR or (KT_S_UNTIL is not None and (prev["h"], prev["s"]) < KT_S_UNTIL)
+                    kt_copy(prev, nc.scalar.copy if kt_s else nc.vector.tensor_copy)
                 if qn:
                     e_quant(qn)
                 if prev and prev["kind"] == "unit" and PASS_MODE == "chain":

@@ -27,10 +27,15 @@ FLOPS = 2 * 2 * P * 1024 * D * 70
 PINNED = True
 COPY_ON_VECTOR = ()
 LOAD_AHEAD = 6
-LAGS = (1, 3, 5, 6, 8, 10, 11)
+LAGS = (1, 3, 6, 7, 9, 11, 12)
 OUT_ON_VECTOR = False
 QT_ON_VECTOR = False
 RINV_LAG = 5
+SPLIT_KQ = True
+OUT_FIRST = False
+VAR_LAG = None
+TAIL_CP_S = 99
+TAIL_FO_S = 99
 BANKS = (4, 2, 2)
 COPY_V_H1 = ()
 KT_S_UNTIL = (0, 8)
@@ -44,7 +49,7 @@ TAIL_SPLIT = False
 VAR_G = 2
 T_WEAVE = True
 KT_ON_SCALAR = False
-DEAL_UNITS = 44
+DEAL_UNITS = 48
 GF_STEP = 3
 VQ_LAG = 9
 ZERO_LAG = 0
@@ -119,7 +124,7 @@ def true_ranges(flags):
 
 def build_items():
     units = [{"kind": "unit", "h": h, "g": g} for h in range(H) for g in range(1, NCHUNK)]
-    kq = [[{"kind": "kq", "h": h, "s": s} for s in range(NSLAB)] for h in range(H)]
+    kq = [[{"kind": "kq", "h": h, "s": s, "parts": "kq"} for s in range(NSLAB)] for h in range(H)]
     gs = [[{"kind": "gs", "h": h, "s": s} for s in range(NSLAB)] for h in range(H)]
     gf = [[{"kind": "gf", "h": h, "i": i} for i in range(4)] for h in range(H)]
     extras = []
@@ -130,6 +135,10 @@ def build_items():
         extras.extend([kq[1][2 + 2 * i], kq[1][3 + 2 * i], gf[0][i], gs[1][i]])
     extras.extend([gf[0][3]] + gs[1][3:])
     seq = [kq[0][0], kq[0][1], {"kind": "nop"}]
+    if SPLIT_KQ:
+        halves = lambda it: [{"kind": "kq", "h": it["h"], "s": it["s"], "parts": part} for part in "kq"]
+        extras = [x for it in extras for x in (halves(it) if it["kind"] == "kq" else [it])]
+        seq = halves(kq[0][0]) + halves(kq[0][1]) + [{"kind": "nop"}]
     dealt = 0
     last = 0
     for n, u in enumerate(units):
@@ -217,25 +226,25 @@ def tile_globallocalattention_t_kernel(tc, q, k, v, out):
 
         def kq_load(it):
             h, s = it["h"], it["s"]
-            if s == 0:
+            if s == 0 and "k" in it["parts"]:
                 head_alloc(h)
             r0 = h * S + 512 * s
-            it["k_raw"] = raw.tile([P, 4 * D], BF16, name="k_raw")
-            it["q_raw"] = raw.tile([P, 4 * D], BF16, name="q_raw")
-            if ROWS2K:
-                nc.sync.dma_start(out=it["k_raw"][:], in_=kf[r0:r0 + 512, :].rearrange("(p t) d -> p (t d)", t=4))
-                nc.sync.dma_start(out=it["q_raw"][:], in_=qf[r0:r0 + 512, :].rearrange("(p t) d -> p (t d)", t=4))
-            else:
-                nc.sync.dma_start(
-                    out=it["k_raw"][:].rearrange("p (t d) -> p t d", t=4),
-                    in_=kf[r0:r0 + 512, :].rearrange("(t p) d -> p t d", p=P),
-                )
-                nc.sync.dma_start(
-                    out=it["q_raw"][:].rearrange("p (t d) -> p t d", t=4),
-                    in_=qf[r0:r0 + 512, :].rearrange("(t p) d -> p t d", p=P),
-                )
+            for part, src in (("k", kf), ("q", qf)):
+                if part not in it["parts"]:
+                    continue
+                tl = raw.tile([P, 4 * D], BF16, name="%s_raw" % part)
+                it["%s_raw" % part] = tl
+                if ROWS2K:
+                    nc.sync.dma_start(out=tl[:], in_=src[r0:r0 + 512, :].rearrange("(p t) d -> p (t d)", t=4))
+                else:
+                    nc.sync.dma_start(
+                        out=tl[:].rearrange("p (t d) -> p t d", t=4),
+                        in_=src[r0:r0 + 512, :].rearrange("(t p) d -> p t d", p=P),
+                    )
 
         def v_load(it):
+            if "k" not in it["parts"]:
+                return
             r0 = it["h"] * S + 512 * it["s"]
             it["v_raw"] = vraw.tile([P, 4 * D], BF16, name="v_raw")
             nc.sync.dma_start(
@@ -246,7 +255,11 @@ def tile_globallocalattention_t_kernel(tc, q, k, v, out):
             it["banks"] = []
             if PASS_MODE == "wide":
                 both = ps_s.tile([P, 1024], F32, name="s_ps")
-            for half, src in enumerate((it["k_raw"], it["q_raw"])):
+            for half, part in enumerate("kq"):
+                if part not in it["parts"]:
+                    it["banks"].append(None)
+                    continue
+                src = it["%s_raw" % part]
                 if PASS_MODE == "wide":
                     ps = both[:, 512 * half:512 * (half + 1)]
                 else:
@@ -606,12 +619,20 @@ def tile_globallocalattention_t_kernel(tc, q, k, v, out):
         def stream():
             l_pass, l_exp, l_tr, l_cp, l_qn, l_mx, l_out = LAGS
             e_kinds = ("unit", "gf")
+            pending = []
 
             def group_done(i):
                 it = at(i, e_kinds)
                 return it["group"] if it and it["group"]["members"][-1] is it else None
 
             for t in range(len(items) + l_out + 1):
+                if VAR_LAG is not None:
+                    i = t - VAR_LAG
+                    if 0 <= i < len(items) and "variants" in items[i]:
+                        pending.append(items[i]["variants"])
+                    if pending and all([(pending[0][0], a // 4) in vq_done for c in variant_slabs(pending[0][1]).values() for a in c]):
+                        build_variants(pending[0][0], pending[0][1])
+                        pending.remove(pending[0])
                 ahead = [i for i in (range(LOAD_AHEAD + 1) if t == 0 else [t + LOAD_AHEAD]) if at(i, ("kq",))]
                 for i in ahead:
                     kq_load(items[i])
@@ -645,6 +666,12 @@ def tile_globallocalattention_t_kernel(tc, q, k, v, out):
                     fo_v = (True, True) if (v_idle or (alt and not v_extra)) else (False, False)
                 else:
                     fo_v = (False, False) if v_extra else (True, True)
+                if t - len(items) >= TAIL_CP_S:
+                    cp_v = False
+                if t - len(items) >= TAIL_FO_S:
+                    fo_v = (False, False)
+                if fo and OUT_FIRST:
+                    fin_out(fo, fo_v)
                 trs = e_transpose(tr) if tr else []
                 if cur and cur["kind"] == "unit":
                     ch = [[(en[0] if en else None) for en in ent] for slab, chunks, ent in cur["tiles"]]
@@ -693,17 +720,17 @@ def tile_globallocalattention_t_kernel(tc, q, k, v, out):
                 if prev and prev["kind"] == "gs":
                     gs_pass(prev)
                 if prev and prev["kind"] == "kq":
-                    s = prev["s"]
-                    kq_done.extend([(prev["h"], "k", s), (prev["h"], "q", s)])
+                    kq_done.extend([(prev["h"], part, prev["s"]) for part in prev["parts"]])
+                if prev and prev["kind"] == "kq" and "k" in prev["parts"]:
                     kt_s = KT_ON_SCALAR or (KT_S_UNTIL is not None and (prev["h"], prev["s"]) < KT_S_UNTIL)
                     kt_copy(prev, nc.scalar.copy if kt_s else nc.vector.tensor_copy)
                 if qn:
                     e_quant(qn)
                 if prev and prev["kind"] == "unit" and PASS_MODE == "chain":
                     unit_pass(prev, False)
-                if at(t - RG_LAG, ("kq",)):
+                if at(t - RG_LAG, ("kq",)) and "k" in items[t - RG_LAG]["parts"]:
                     kq_regroup(items[t - RG_LAG])
-                if at(t - VQ_LAG, ("kq",)):
+                if at(t - VQ_LAG, ("kq",)) and "k" in items[t - VQ_LAG]["parts"]:
                     kq_vquant(items[t - VQ_LAG])
                 if cp and cp_v:
                     e_copy(cp, True)
@@ -713,22 +740,24 @@ def tile_globallocalattention_t_kernel(tc, q, k, v, out):
                     gs_comb(prev)
                 if rv:
                     fin_rinv(rv)
-                if fo and fo_v[0]:
+                if fo and fo_v[0] and not OUT_FIRST:
                     fin_out(fo, fo_v)
-                qt_v = prev is not None and prev["kind"] == "kq" and ((QT_ON_VECTOR and t - l_pass >= 2) or (QT_V_FROM is not None and (prev["h"], prev["s"]) >= QT_V_FROM))
+                has_q = prev is not None and prev["kind"] == "kq" and "q" in prev["parts"]
+                qt_v = has_q and ((QT_ON_VECTOR and t - l_pass >= 2) or (QT_V_FROM is not None and (prev["h"], prev["s"]) >= QT_V_FROM))
                 if qt_v:
                     qt_copy(prev, nc.vector.tensor_copy)
-                if prev and prev["kind"] == "kq" and not qt_v:
+                if has_q and not qt_v:
                     qt_copy(prev, nc.scalar.copy)
                 if cp and not cp_v:
                     e_copy(cp, False)
                 if ex:
                     e_exp(ex)
-                if fo and not fo_v[0]:
+                if fo and not fo_v[0] and not OUT_FIRST:
                     fin_out(fo, fo_v)
-                i = t - VQ_LAG
-                if 0 <= i < len(items) and "variants" in items[i]:
-                    build_variants(items[i]["variants"][0], items[i]["variants"][1])
+                if VAR_LAG is None:
+                    i = t - VQ_LAG
+                    if 0 <= i < len(items) and "variants" in items[i]:
+                        build_variants(items[i]["variants"][0], items[i]["variants"][1])
 
         if PINNED:
             with tc.manual_schedule():

@@ -31,12 +31,14 @@ LAGS = (1, 3, 6, 7, 9, 11, 12)
 OUT_ON_VECTOR = False
 QT_ON_VECTOR = False
 RINV_LAG = 5
+OPOOL = 4
+SHARED_PSUM = True
 SPLIT_KQ = True
 OUT_FIRST = False
 VAR_LAG = None
 TAIL_CP_S = 99
 TAIL_FO_S = 99
-BANKS = (4, 2, 2)
+BANKS = (8, 0, 0)
 COPY_V_H1 = ()
 KT_S_UNTIL = (0, 8)
 VRAW_BUFS = 4
@@ -45,7 +47,7 @@ GAMMA = 1.0
 QPLANES = False
 PASS_MODE = "two"
 ROWS2K = True
-TAIL_SPLIT = False
+TAIL_SPLIT = True
 VAR_G = 2
 T_WEAVE = True
 KT_ON_SCALAR = False
@@ -174,11 +176,15 @@ def tile_globallocalattention_t_kernel(tc, q, k, v, out):
         sstage = ctx.enter_context(tc.tile_pool(name="sstage", bufs=4))
         cpool = ctx.enter_context(tc.tile_pool(name="cpool", bufs=8))
         gcpool = ctx.enter_context(tc.tile_pool(name="gcpool", bufs=4))
-        opool = ctx.enter_context(tc.tile_pool(name="opool", bufs=4))
+        opool = ctx.enter_context(tc.tile_pool(name="opool", bufs=OPOOL))
         small = ctx.enter_context(tc.tile_pool(name="small", bufs=8))
         ps_s = ctx.enter_context(tc.psum_pool(name="ps_s", bufs=2 if PASS_MODE == "wide" else BANKS[0]))
-        ps_t = ctx.enter_context(tc.psum_pool(name="ps_t", bufs=BANKS[1]))
-        ps_o = ctx.enter_context(tc.psum_pool(name="ps_o", bufs=BANKS[2]))
+        if SHARED_PSUM:
+            ps_t = ps_s
+            ps_o = ps_s
+        else:
+            ps_t = ctx.enter_context(tc.psum_pool(name="ps_t", bufs=BANKS[1]))
+            ps_o = ctx.enter_context(tc.psum_pool(name="ps_o", bufs=BANKS[2]))
 
         warm = const.tile([P, 2], F32)
         nc.vector.memset(warm[:], 0.0)
@@ -501,7 +507,7 @@ def tile_globallocalattention_t_kernel(tc, q, k, v, out):
 
         def e_transpose(it):
             e_sb = e_bufs[it["buf"]]
-            eT = ps_t.tile([P, 2, 2, P], F32, name="eT")
+            eT = ps_t.tile([P, 2, 2, P], F32, name="s_ps" if SHARED_PSUM else "eT")
             it["eT"] = eT
             return [
                 {"out": eT[:, ti, u, :], "in_": e_sb[:, ti, u, :].bitcast(F32)} for ti in range(2) for u in range(2)
@@ -528,7 +534,7 @@ def tile_globallocalattention_t_kernel(tc, q, k, v, out):
             it["scl"] = scl
 
         def fin_mx(grp):
-            o_ps = ps_o.tile([P, 2, D], F32, name="o_ps")
+            o_ps = ps_o.tile([P, 2, D], F32, name="s_ps" if SHARED_PSUM else "o_ps")
             grp["o_ps"] = o_ps
             one = grp["kind"] == "gf"
             mem = grp["members"]
@@ -684,7 +690,17 @@ def tile_globallocalattention_t_kernel(tc, q, k, v, out):
                         bank_a, calls_a = qk_bank(cur["h"], cur["g"], ch[0], mk[0])
                         bank_b, calls_b = qk_bank(cur["h"], cur["g"], ch[1], mk[1])
                     cur["banks"] = [bank_a, bank_b]
-                    if T_WEAVE:
+                    if T_WEAVE == "back":
+                        run_calls(calls_a)
+                        if mx:
+                            fin_mx(mx)
+                        run_calls(calls_b[0:1] + trs[0:1] + calls_b[1:2] + trs[1:2] + calls_b[2:3] + trs[2:3] + calls_b[3:] + trs[3:4])
+                    elif T_WEAVE == "end":
+                        run_calls(calls_a)
+                        if mx:
+                            fin_mx(mx)
+                        run_calls(calls_b + trs)
+                    elif T_WEAVE:
                         run_calls(trs[0:1] + calls_a[0:1] + trs[1:2] + calls_a[1:])
                         if mx:
                             fin_mx(mx)

from contextlib import ExitStack

import concourse.mybir as mybir
from concourse.masks import make_identity

F32 = mybir.dt.float32
BF16 = mybir.dt.bfloat16
U32 = mybir.dt.uint32
U8 = mybir.dt.uint8
I32 = mybir.dt.int32
FP8X4 = mybir.dt.float8_e4m3fn_x4
ACT = mybir.ActivationFunctionType
ALU = mybir.AluOpType
AX = mybir.AxisListType

P = 128
H = 2
S = 4096
D = 256
NCHUNK = S // P
NSLAB = S // 512
SCALE = 1.0 / 16.0
NEG = -1.0e30
VW = D + D // 4
FLOPS = 2 * 2 * P * 1024 * D * 70

PINNED = True
COPY_ON_VECTOR = ()
LOAD_AHEAD = 6
LAGS = (1, 3, 6, 7, 9, 11, 12)
OUT_ON_VECTOR = False
QT_ON_VECTOR = False
RINV_LAG = 5
OPOOL = 4
SHARED_PSUM = True
SPLIT_KQ = True
OUT_FIRST = False
VAR_LAG = None
TAIL_CP_S = 99
TAIL_FO_S = 99
BANKS = (8, 0, 0)
COPY_V_H1 = ()
KT_S_UNTIL = (0, 8)
VRAW_BUFS = 4
QT_V_FROM = None
GAMMA = 1.0
QPLANES = False
PASS_MODE = "two"
ROWS2K = True
TAIL_SPLIT = True
VAR_G = 2
T_WEAVE = True
KT_ON_SCALAR = False
DEAL_UNITS = 48
GF_STEP = 3
VQ_LAG = 9
ZERO_LAG = 0
RG_LAG = 4
RG_SPLIT = 4
OUT_WINDOW = 2
COPY_RULE = 2
OUT_RULE = 2
GF_COPY_V = False
OUT_V_NEAR_GF = 0
REGROUP = "G"
COMB = "V"


def unit_plan(g):
    want = {}
    for a in range(max(g - 3, 1), min(g + 3, NCHUNK - 1) + 1):
        want[a] = "L" if a == g - 3 else ("U" if a == g + 3 else None)
    want[0] = None
    m, r = divmod(g - 1, 4)
    nat = lambda n: [4 * n, 4 * n + 1, 4 * n + 2, 4 * n + 3]
    if m == 0:
        slabs = [(("L", 0), nat(0)), (("L", 1), nat(1))]
    elif m == 7:
        if r < 2:
            slabs = [(("L", 7), nat(7)), (("V", 0), [0, 25, 26, 27])]
        else:
            slabs = [(("L", 7), nat(7)), (("L", 0), nat(0))]
    elif r == 0:
        slabs = [(("L", m), nat(m)), (("V", 0), [4 * m + 4, 0, 4 * m - 2, 4 * m - 1])]
    elif r == 1:
        slabs = [(("L", m), nat(m)), (("V", 1), [4 * m + 4, 4 * m + 5, 0, 4 * m - 1])]
    elif r == 2:
        slabs = [(("L", m), nat(m)), (("V", 2), [4 * m + 4, 4 * m + 5, 4 * m + 6, 0])]
    else:
        slabs = [(("V", 3), [0, 4 * m + 1, 4 * m + 2, 4 * m + 3]), (("L", m + 1), nat(m + 1))]
    tiles = []
    seen = []
    for slab, chunks in slabs:
        ent = []
        for a in chunks:
            if a in want and a not in seen:
                ent.append((a, want[a]))
                seen.append(a)
            else:
                ent.append(None)
        tiles.append((slab, chunks, ent))
    assert sorted(seen) == sorted(want)
    return tiles


def variant_slabs(m):
    out = {}
    for g in range(4 * m + 1, min(4 * m + 5, NCHUNK)):
        for slab, chunks, ent in unit_plan(g):
            if slab[0] == "V":
                out[slab[1]] = chunks
    return out


def true_ranges(flags):
    out = []
    start = None
    for i, f in enumerate(list(flags) + [False]):
        if f and start is None:
            start = i
        if not f and start is not None:
            out.append((start, i))
            start = None
    return out


def build_items():
    units = [{"kind": "unit", "h": h, "g": g} for h in range(H) for g in range(1, NCHUNK)]
    kq = [[{"kind": "kq", "h": h, "s": s, "parts": "kq"} for s in range(NSLAB)] for h in range(H)]
    gs = [[{"kind": "gs", "h": h, "s": s} for s in range(NSLAB)] for h in range(H)]
    gf = [[{"kind": "gf", "h": h, "i": i} for i in range(4)] for h in range(H)]
    extras = []
    for s in range(2, NSLAB):
        extras.extend([kq[0][s], gs[0][s - 2]])
    extras.extend([kq[1][0], gs[0][6], kq[1][1], gs[0][7]])
    for i in range(3):
        extras.extend([kq[1][2 + 2 * i], kq[1][3 + 2 * i], gf[0][i], gs[1][i]])
    extras.extend([gf[0][3]] + gs[1][3:])
    seq = [kq[0][0], kq[0][1], {"kind": "nop"}]
    if SPLIT_KQ:
        halves = lambda it: [{"kind": "kq", "h": it["h"], "s": it["s"], "parts": part} for part in "kq"]
        extras = [x for it in extras for x in (halves(it) if it["kind"] == "kq" else [it])]
        seq = halves(kq[0][0]) + halves(kq[0][1]) + [{"kind": "nop"}]
    dealt = 0
    last = 0
    for n, u in enumerate(units):
        seq.append(u)
        if u["g"] % 4 == VAR_G and u["g"] // 4 + (1 if VAR_G else 0) < NSLAB:
            u["variants"] = (u["h"], u["g"] // 4 + (1 if VAR_G else 0))
        while dealt < len(extras) and DEAL_UNITS * (dealt / len(extras)) ** GAMMA < n + 1:
            seq.append(extras[dealt])
            dealt += 1
        if dealt == len(extras) and last < 4 and n >= DEAL_UNITS + 1 + GF_STEP * last:
            seq.append(gf[1][last])
            last += 1
    assert dealt == len(extras) and last == 4
    return seq


def tile_globallocalattention_t_kernel(tc, q, k, v, out):
    nc = tc.nc
    qf = q.flatten_outer_dims()
    kf = k.flatten_outer_dims()
    vf = v.flatten_outer_dims()
    of = out.flatten_outer_dims()

    with ExitStack() as ctx:
        const = ctx.enter_context(tc.tile_pool(name="const", bufs=1))
        raw = ctx.enter_context(tc.tile_pool(name="raw", bufs=4))
        vraw = ctx.enter_context(tc.tile_pool(name="vraw", bufs=VRAW_BUFS))
        head = ctx.enter_context(tc.tile_pool(name="head", bufs=2))
        fixed = ctx.enter_context(tc.tile_pool(name="fixed", bufs=1))
        vstage = ctx.enter_context(tc.tile_pool(name="vstage", bufs=VRAW_BUFS))
        vvpool = ctx.enter_context(tc.tile_pool(name="vvpool", bufs=3))
        gstage = ctx.enter_context(tc.tile_pool(name="gstage", bufs=3))
        sstage = ctx.enter_context(tc.tile_pool(name="sstage", bufs=4))
        cpool = ctx.enter_context(tc.tile_pool(name="cpool", bufs=8))
        gcpool = ctx.enter_context(tc.tile_pool(name="gcpool", bufs=4))
        opool = ctx.enter_context(tc.tile_pool(name="opool", bufs=OPOOL))
        small = ctx.enter_context(tc.tile_pool(name="small", bufs=8))
        ps_s = ctx.enter_context(tc.psum_pool(name="ps_s", bufs=2 if PASS_MODE == "wide" else BANKS[0]))
        if SHARED_PSUM:
            ps_t = ps_s
            ps_o = ps_s
        else:
            ps_t = ctx.enter_context(tc.psum_pool(name="ps_t", bufs=BANKS[1]))
            ps_o = ctx.enter_context(tc.psum_pool(name="ps_o", bufs=BANKS[2]))

        warm = const.tile([P, 2], F32)
        nc.vector.memset(warm[:], 0.0)
        nc.scalar.activation(out=warm[:, 1:2], in_=warm[:, 0:1], func=ACT.Exp)

        ident_f = const.tile([P, P], F32)
        make_identity(nc, ident_f[:])
        ident_bf = const.tile([P, P], BF16)
        make_identity(nc, ident_bf[:])
        mask_bf = {}
        for kind, sign in (("U", 1), ("L", -1)):
            mf = const.tile([P, P], F32, name="mask_f_%s" % kind)
            nc.gpsimd.memset(mf[:], 0.0)
            nc.gpsimd.affine_select(
                out=mf[:], in_=mf[:], compare_op=ALU.is_ge, fill=NEG, base=0,
                pattern=[[-sign, P]], channel_multiplier=sign,
            )
            mb = const.tile([P, P], BF16, name="mask_b_%s" % kind)
            nc.vector.tensor_copy(
                out=mb[:].rearrange("t (u y e) -> t y u e", u=2, e=2),
                in_=mf[:].rearrange("t (y u e) -> t y u e", u=2, e=2),
            )
            mask_bf[kind] = mb

        e_bufs = [fixed.tile([P, 2, 2, 2 * P], BF16, name="e_sb%d" % i) for i in range(8)]
        is_zero = {}
        s_sb = [fixed.tile([P, NSLAB, 2, 2 * P], F32, name="s_sb%d" % h) for h in range(H)]
        hd = {}
        vv = {}
        gl = {0: {}, 1: {}}
        vq_done = []
        kq_done = []

        def head_alloc(h):
            qT = head.tile([P, S], F32, name="qT")
            kT = head.tile([P, S], F32, name="kT")
            vl = head.tile([P, NSLAB * VW], U32, name="vl", align_bytes=64)
            nc.vector.memset(vl[:].bitcast(I32).rearrange("p (s w) -> p s w", w=VW)[:, :, D:VW], 0)
            hd[h] = {
                "qT": qT, "kT": kT, "vl": vl,
                "qv": qT[:].bitcast(BF16).rearrange("p (e r) -> p e r" if QPLANES else "p (r e) -> p e r", e=2),
                "kv": kT[:].bitcast(BF16).rearrange("p (c u x h) -> p h u c x", u=2, x=64, h=2),
                "kv2": kT[:].bitcast(BF16).rearrange("p (s u c x h) -> p h s u c x", u=2, c=4, x=64, h=2),
            }

        def kq_load(it):
            h, s = it["h"], it["s"]
            if s == 0 and "k" in it["parts"]:
                head_alloc(h)
            r0 = h * S + 512 * s
            for part, src in (("k", kf), ("q", qf)):
                if part not in it["parts"]:
                    continue
                tl = raw.tile([P, 4 * D], BF16, name="%s_raw" % part)
                it["%s_raw" % part] = tl
                if ROWS2K:
                    nc.sync.dma_start(out=tl[:], in_=src[r0:r0 + 512, :].rearrange("(p t) d -> p (t d)", t=4))
                else:
                    nc.sync.dma_start(
                        out=tl[:].rearrange("p (t d) -> p t d", t=4),
                        in_=src[r0:r0 + 512, :].rearrange("(t p) d -> p t d", p=P),
                    )

        def v_load(it):
            if "k" not in it["parts"]:
                return
            r0 = it["h"] * S + 512 * it["s"]
            it["v_raw"] = vraw.tile([P, 4 * D], BF16, name="v_raw")
            nc.sync.dma_start(
                out=it["v_raw"][:], in_=vf[r0:r0 + 512, :].rearrange("(p j) d -> p (j d)", j=4)
            )

        def kq_transpose(it):
            it["banks"] = []
            if PASS_MODE == "wide":
                both = ps_s.tile([P, 1024], F32, name="s_ps")
            for half, part in enumerate("kq"):
                if part not in it["parts"]:
                    it["banks"].append(None)
                    continue
                src = it["%s_raw" % part]
                if PASS_MODE == "wide":
                    ps = both[:, 512 * half:512 * (half + 1)]
                else:
                    ps = ps_s.tile([P, 512], F32, name="s_ps")
                for i in range(4):
                    nc.tensor.transpose(
                        ps[:, P * i:P * (i + 1)], src[:].bitcast(F32)[:, P * i:P * (i + 1)], ident_f[:]
                    )
                it["banks"].append(ps)

        def kq_regroup(it):
            vgrp = vstage.tile([P, 4 * D], BF16, name="vgrp", align_bytes=64)
            dst = vgrp[:].rearrange("p (c i j) -> p c j i", i=4, j=4)
            src = it["v_raw"][:].rearrange("p (j c i) -> p c j i", j=4, i=4)
            if REGROUP == "V":
                nc.vector.tensor_copy(out=dst, in_=src)
            else:
                w = 64 // RG_SPLIT
                for i in range(RG_SPLIT):
                    nc.gpsimd.tensor_scalar(
                        out=dst[:, w * i:w * (i + 1)], in0=src[:, w * i:w * (i + 1)], scalar1=1.0, scalar2=0.0,
                        op0=ALU.mult, op1=ALU.add,
                    )
            it["vgrp"] = vgrp

        def v_slab(h, slab, m):
            kind, n = slab
            t = hd[h]["vl"] if kind == "L" else vv[(h, m)]
            return t[:, VW * n:VW * n + D], t[:, VW * n + D:VW * (n + 1)].bitcast(U8)

        def kq_vquant(it):
            codes, scales = v_slab(it["h"], ("L", it["s"]), None)
            nc.vector.quantize_mx(out=codes.bitcast(FP8X4), scales=scales, in_=it["vgrp"][:])
            vq_done.append((it["h"], it["s"]))

        def build_variants(h, m):
            t = vvpool.tile([P, 4 * VW], U32, name="vvar", align_bytes=64)
            vv[(h, m)] = t
            vl = hd[h]["vl"]
            for slot, chunks in sorted(variant_slabs(m).items()):
                pieces = []
                for qd, a in enumerate(chunks):
                    if pieces and a != 0 and pieces[-1][2] == a // 4 and pieces[-1][3] + pieces[-1][1] == a % 4:
                        pieces[-1][1] += 1
                    else:
                        pieces.append([qd, 1, a // 4, a % 4])
                for q0, n, s, sq in pieces:
                    assert (h, s) in vq_done
                    nc.sync.dma_start(
                        out=t[32 * q0:32 * (q0 + n), VW * slot:VW * (slot + 1)].bitcast(I32),
                        in_=vl[32 * sq:32 * (sq + n), VW * s:VW * (s + 1)].bitcast(I32),
                    )

        def qk_runs(chunks):
            runs = []
            for qd in range(4):
                a = chunks[qd]
                if a is None:
                    continue
                if runs and runs[-1][0] + runs[-1][1] == qd and runs[-1][2] + runs[-1][1] == a:
                    runs[-1][1] += 1
                else:
                    runs.append([qd, 1, a])
            return runs

        def k_cols(t, half, a0, n):
            if ROWS2K:
                assert a0 // 4 == (a0 + n - 1) // 4
                return t["kv2"][:, half, a0 // 4, :, a0 % 4:a0 % 4 + n, :]
            return t["kv"][:, half, :, a0:a0 + n, :]

        def qt_copy(it, copy):
            dst = hd[it["h"]]["qT"][:, 512 * it["s"]:512 * (it["s"] + 1)]
            if QPLANES:
                for hh in range(2):
                    pl = hd[it["h"]]["qv"][:, hh, 512 * it["s"]:512 * (it["s"] + 1)]
                    src = it["banks"][1][:].bitcast(BF16)
                    if ROWS2K:
                        copy(out=pl.rearrange("w (p t) -> w p t", t=4), in_=src.rearrange("w (t p h) -> w h p t", t=4, h=2)[:, hh])
                    else:
                        copy(out=pl, in_=src.rearrange("w (c h) -> w h c", h=2)[:, hh])
            elif ROWS2K:
                copy(out=dst.rearrange("w (p t) -> w p t", t=4), in_=it["banks"][1][:].rearrange("w (t p) -> w p t", t=4))
            else:
                copy(out=dst, in_=it["banks"][1][:])

        def kt_copy(it, copy):
            dst = hd[it["h"]]["kT"][:, 512 * it["s"]:512 * (it["s"] + 1)]
            if ROWS2K:
                copy(
                    out=dst.rearrange("w (u p e) -> w u p e", u=2, e=2),
                    in_=it["banks"][0][:].rearrange("w (u e p) -> w u p e", u=2, e=2),
                )
            else:
                for u in range(2):
                    copy(
                        out=dst.rearrange("w (c u y e) -> w c u y e", u=2, y=32, e=2)[:, :, u],
                        in_=it["banks"][0][:].rearrange("w (c y u e) -> w c u y e", y=32, u=2, e=2)[:, :, u],
                    )

        def qk_bank(h, g, chunks, masks, bank=None):
            t = hd[h]
            ps = bank if bank is not None else ps_s.tile([P, 512], F32, name="s_ps")
            view = ps[:].rearrange("q (u c x) -> q u c x", u=2, x=64)
            assert (h, "q", g // 4) in kq_done
            calls = []
            for q0, n, a0 in qk_runs(chunks):
                assert (h, "k", (a0 + n - 1) // 4) in kq_done
                dst = view[:, :, q0:q0 + n, :]
                calls.append({
                    "out": dst, "lhsT": t["qv"][:, 0, P * g:P * (g + 1)], "rhs": k_cols(t, 0, a0, n),
                    "start": True, "stop": False,
                })
                for qd in range(q0, q0 + n):
                    if masks[qd] is not None:
                        calls.append({
                            "out": view[:, :, qd, :], "lhsT": ident_bf[:],
                            "rhs": mask_bf[masks[qd]][:].rearrange("t (u x) -> t u x", u=2),
                            "start": False, "stop": False,
                        })
                calls.append({
                    "out": dst, "lhsT": t["qv"][:, 1, P * g:P * (g + 1)], "rhs": k_cols(t, 1, a0, n),
                    "start": False, "stop": True,
                })
            return ps, calls

        def run_calls(calls):
            for c in calls:
                if "in_" in c:
                    nc.tensor.transpose(c["out"], c["in_"], ident_f[:])
                else:
                    nc.tensor.matmul(**c)

        def unit_pieces(it):
            pieces = []
            for ti, (slab, chunks, ent) in enumerate(it["tiles"]):
                for q0, q1 in true_ranges([en is not None for en in ent]):
                    pieces.append((ti, q0, q1))
            return pieces

        def unit_pass(it, first):
            pieces = unit_pieces(it)
            if first:
                it["mn"] = small.tile([P, 8], F32, name="mn")
                it["s_u"] = sstage.tile([P, 2, 2, 2 * P], F32, name="s_u")
            mn = it["mn"]
            s_u = it["s_u"]
            if PASS_MODE == "wide" and whole(it):
                if first:
                    nc.vector.tensor_scalar(
                        out=s_u[:].rearrange("q t u x -> q (t u x)"), in0=it["wide"][:],
                        scalar1=-SCALE, scalar2=None, op0=ALU.mult, op1=ALU.min, accum_out=mn[:, 0:1],
                    )
                pieces = pieces[:1]
            else:
                for i, (ti, q0, q1) in enumerate(pieces):
                    if (i == 0) != first:
                        continue
                    nc.vector.tensor_scalar(
                        out=s_u[:, ti, :, 64 * q0:64 * q1],
                        in0=it["banks"][ti][:].rearrange("q (u x) -> q u x", u=2)[:, :, 64 * q0:64 * q1],
                        scalar1=-SCALE, scalar2=(mn[:, i - 1:i] if PASS_MODE == "chain" and i > 0 else None),
                        op0=ALU.mult, op1=ALU.min, accum_out=mn[:, i:i + 1],
                    )
            it["n_mn"] = len(pieces)
            it["src"] = lambda ti: s_u[:, ti]
            it["src2"] = s_u[:]

        def unit_comb(it):
            if PASS_MODE == "chain" or it["n_mn"] == 1:
                it["negm"] = it["mn"][:, it["n_mn"] - 1:it["n_mn"]]
                return
            negm = small.tile([P, 1], F32, name="negm")
            mn = it["mn"]
            if it["n_mn"] == 2 and COMB == "G":
                nc.gpsimd.tensor_scalar(out=negm[:], in0=mn[:, 0:1], scalar1=mn[:, 1:2], scalar2=None, op0=ALU.min)
            elif it["n_mn"] == 2:
                nc.vector.tensor_tensor(out=negm[:], in0=mn[:, 0:1], in1=mn[:, 1:2], op=ALU.min)
            else:
                nc.vector.tensor_reduce(out=negm[:], in_=mn[:, 0:it["n_mn"]], axis=AX.X, op=ALU.min)
            it["negm"] = negm

        def gs_pass(it):
            s = it["s"]
            if s == 0:
                gl[it["h"]]["mn"] = small.tile([P, NSLAB], F32, name="gmn")
            nc.vector.tensor_scalar(
                out=s_sb[it["h"]][:, s], in0=it["banks"][0][:].rearrange("q (u x) -> q u x", u=2),
                scalar1=-SCALE, scalar2=None, op0=ALU.mult, op1=ALU.min,
                accum_out=gl[it["h"]]["mn"][:, s:s + 1],
            )

        def gs_comb(it):
            gl[it["h"]]["negm"] = small.tile([P, 1], F32, name="gnegm")
            nc.vector.tensor_reduce(out=gl[it["h"]]["negm"][:], in_=gl[it["h"]]["mn"][:], axis=AX.X, op=ALU.min)

        def whole(it):
            return all([en is not None for slab, chunks, ent in it["tiles"] for en in ent])

        def acc_init(grp):
            grp["acc"] = small.tile([P, 4, 4], F32, name="acc" if grp["kind"] == "unit" else "gacc")
            grp["plain"] = all([whole(it) for it in grp["members"]])
            if not grp["plain"]:
                nc.gpsimd.memset(grp["acc"][:], 0.0)

        def e_zero(it):
            bi = it["buf"]
            e_sb = e_bufs[bi]
            for ti, (slab, chunks, ent) in enumerate(it["tiles"]):
                for qd in range(4):
                    if ent[qd] is None:
                        if not is_zero.get((bi, ti, qd), False):
                            nc.gpsimd.memset(e_sb[:, ti, :, 64 * qd:64 * (qd + 1)], 0.0)
                            is_zero[(bi, ti, qd)] = True
                    else:
                        is_zero[(bi, ti, qd)] = False

        def e_exp(it):
            bi = it["buf"]
            e_sb = e_bufs[bi]
            acc = it["group"]["acc"]
            negm = it["negm"] if it["kind"] == "unit" else gl[it["h"]]["negm"]
            n_acc = 0
            if whole(it):
                nc.scalar.activation(
                    out=e_sb[:], in_=it["src2"], func=ACT.Exp, bias=negm[:, 0:1], scale=-1.0,
                    accum_out=acc[:, it["gidx"], 0:1],
                )
                return
            for ti, (slab, chunks, ent) in enumerate(it["tiles"]):
                for q0, q1 in true_ranges([en is not None for en in ent]):
                    nc.scalar.activation(
                        out=e_sb[:, ti, :, 64 * q0:64 * q1], in_=it["src"](ti)[:, :, 64 * q0:64 * q1],
                        func=ACT.Exp, bias=negm[:, 0:1], scale=-1.0,
                        accum_out=acc[:, it["gidx"], n_acc:n_acc + 1],
                    )
                    n_acc += 1
            assert n_acc <= 4

        def e_transpose(it):
            e_sb = e_bufs[it["buf"]]
            eT = ps_t.tile([P, 2, 2, P], F32, name="s_ps" if SHARED_PSUM else "eT")
            it["eT"] = eT
            return [
                {"out": eT[:, ti, u, :], "in_": e_sb[:, ti, u, :].bitcast(F32)} for ti in range(2) for u in range(2)
            ]

        def e_copy(it, on_v):
            grp = gstage.tile([P, 2, P, 4], BF16, name="grp", align_bytes=64)
            src = it["eT"][:].rearrange("p t u q -> p t q u")
            dst = grp[:].rearrange("p t q j -> p (t q j)").bitcast(F32).rearrange("p (t q u) -> p t q u", t=2, u=2)
            if on_v:
                nc.vector.tensor_copy(out=dst, in_=src)
            else:
                nc.scalar.copy(out=dst, in_=src)
            it["grp"] = grp

        def e_quant(it):
            pool = cpool if it["kind"] == "unit" else gcpool
            codes = pool.tile([P, 2 * P], U32, name="codes", align_bytes=64)
            scl = pool.tile([P, 2 * P], U8, name="scl", align_bytes=64)
            nc.vector.quantize_mx(
                out=codes[:].bitcast(FP8X4), scales=scl[:], in_=it["grp"][:].rearrange("p t q j -> p (t q j)")
            )
            it["codes"] = codes
            it["scl"] = scl

        def fin_mx(grp):
            o_ps = ps_o.tile([P, 2, D], F32, name="s_ps" if SHARED_PSUM else "o_ps")
            grp["o_ps"] = o_ps
            one = grp["kind"] == "gf"
            mem = grp["members"]
            for i, it in enumerate(mem):
                for ti in range(2):
                    m = (it["g"] - 1) // 4 if it["kind"] == "unit" else None
                    vc, vs = v_slab(it["h"], it["tiles"][ti][0], m)
                    nc.tensor.matmul_mx(
                        out=o_ps[:, 0 if one else i, :],
                        lhsT=it["codes"][:, P * ti:P * (ti + 1)].bitcast(FP8X4),
                        lhsT_scale=it["scl"][:, P * ti:P * (ti + 1)],
                        rhs=vc.bitcast(FP8X4), rhs_scale=vs,
                        start=(ti == 0 and (i == 0 or not one)),
                        stop=(ti == 1 and (i == len(mem) - 1 or not one)),
                    )

        def fin_rinv(grp):
            n = len(grp["members"])
            rinv = small.tile([P, 2], F32, name="rinv")
            if grp["kind"] == "gf" or not grp["plain"]:
                tot = small.tile([P, 2], F32, name="tot")
            if grp["kind"] == "gf":
                nc.vector.tensor_reduce(out=tot[:, 0:1], in_=grp["acc"][:, 0:n, 0:1], axis=AX.XY, op=ALU.add)
                n = 1
                nc.vector.reciprocal(out=rinv[:, 0:1], in_=tot[:, 0:1])
            elif grp["plain"]:
                nc.vector.reciprocal(out=rinv[:, 0:n], in_=grp["acc"][:, 0:n, 0])
            else:
                nc.vector.tensor_reduce(out=tot[:, 0:n], in_=grp["acc"][:, 0:n, :], axis=AX.X, op=ALU.add)
                nc.vector.reciprocal(out=rinv[:, 0:n], in_=tot[:, 0:n])
            grp["rinv"] = rinv
            grp["n_out"] = n

        def fin_out(grp, on_v):
            n = grp["n_out"]
            o_sb = opool.tile([P, 2, D], F32, name="o_sb")
            for i in range(n):
                if on_v[i]:
                    nc.vector.tensor_scalar(
                        out=o_sb[:, i, :], in0=grp["o_ps"][:, i, :], scalar1=grp["rinv"][:, i:i + 1], scalar2=None,
                        op0=ALU.mult,
                    )
                else:
                    nc.scalar.activation(
                        out=o_sb[:, i, :], in_=grp["o_ps"][:, i, :], func=ACT.Copy, scale=grp["rinv"][:, i:i + 1]
                    )
            first = grp["members"][0]
            r0 = first["h"] * S + (P * first["g"] if grp["kind"] == "unit" else 0)
            nc.sync.dma_start(
                out=of[r0:r0 + P * n, :].rearrange("(u p) d -> p u d", p=P), in_=o_sb[:, 0:n, :]
            )

        items = build_items()
        groups = {}
        cnt = 0
        for it in items:
            if it["kind"] not in ("unit", "gf"):
                continue
            it["buf"] = cnt % 8
            it["copy_v"] = (cnt % 8) in COPY_ON_VECTOR or (GF_COPY_V and it["kind"] == "gf")
            cnt += 1
            if it["kind"] == "unit":
                key = (it["h"], "unit", (it["g"] - 1) // 2)
                it["tiles"] = unit_plan(it["g"])
            else:
                key = (it["h"], "gf", 0)
                it["tiles"] = [
                    (("L", s), None, [(4 * s + c, None) for c in range(4)]) for s in (2 * it["i"], 2 * it["i"] + 1)
                ]
                it["src2"] = s_sb[it["h"]][:, 2 * it["i"]:2 * it["i"] + 2]
            if key not in groups:
                groups[key] = {"kind": it["kind"], "members": [], "out_v": OUT_ON_VECTOR}
            it["group"] = groups[key]
            it["gidx"] = len(groups[key]["members"])
            groups[key]["members"].append(it)

        for i, it in enumerate(items):
            if it["kind"] == "gf":
                for j in range(max(i - OUT_V_NEAR_GF, 0), i):
                    if items[j]["kind"] == "unit":
                        items[j]["group"]["out_v"] = True

        def at(i, kinds):
            if 0 <= i < len(items) and items[i]["kind"] in kinds:
                return items[i]
            return None

        def stream():
            l_pass, l_exp, l_tr, l_cp, l_qn, l_mx, l_out = LAGS
            e_kinds = ("unit", "gf")
            pending = []

            def group_done(i):
                it = at(i, e_kinds)
                return it["group"] if it and it["group"]["members"][-1] is it else None

            for t in range(len(items) + l_out + 1):
                if VAR_LAG is not None:
                    i = t - VAR_LAG
                    if 0 <= i < len(items) and "variants" in items[i]:
                        pending.append(items[i]["variants"])
                    if pending and all([(pending[0][0], a // 4) in vq_done for c in variant_slabs(pending[0][1]).values() for a in c]):
                        build_variants(pending[0][0], pending[0][1])
                        pending.remove(pending[0])
                ahead = [i for i in (range(LOAD_AHEAD + 1) if t == 0 else [t + LOAD_AHEAD]) if at(i, ("kq",))]
                for i in ahead:
                    kq_load(items[i])
                for i in ahead:
                    v_load(items[i])
                cur = at(t, ("unit", "gs", "kq"))
                prev = at(t - l_pass, ("unit", "gs", "kq"))
                ex = at(t - l_exp, e_kinds)
                tr = at(t - l_tr, e_kinds)
                cp = at(t - l_cp, e_kinds)
                qn = at(t - l_qn, e_kinds)
                mx = group_done(t - l_mx)
                fo = group_done(t - l_out)
                rv = group_done(t - RINV_LAG)
                v_idle = prev is None
                v_extra = any([at(t - l_pass - d, ("kq", "gs")) is not None for d in range(OUT_WINDOW)])
                s_idle = ex is None
                cp_v = (v_idle and not (s_idle and TAIL_SPLIT)) if COPY_RULE == 2 else False
                if cp and cp["h"] == 1 and cp["buf"] in COPY_V_H1:
                    cp_v = True
                if OUT_RULE == 0:
                    fo_v = (False, False)
                elif OUT_RULE == 1:
                    fo_v = (True, True) if v_idle else ((False, False) if v_extra else (True, False))
                    if v_idle and s_idle and TAIL_SPLIT:
                        fo_v = (True, False)
                elif OUT_RULE == 2:
                    fo_v = (True, True) if v_idle else (False, False)
                elif OUT_RULE == 4:
                    alt = fo is not None and fo["kind"] == "unit" and ((fo["members"][0]["g"] - 1) // 2) % 2 == 0
                    fo_v = (True, True) if (v_idle or (alt and not v_extra)) else (False, False)
                else:
                    fo_v = (False, False) if v_extra else (True, True)
                if t - len(items) >= TAIL_CP_S:
                    cp_v = False
                if t - len(items) >= TAIL_FO_S:
                    fo_v = (False, False)
                if fo and OUT_FIRST:
                    fin_out(fo, fo_v)
                trs = e_transpose(tr) if tr else []
                if cur and cur["kind"] == "unit":
                    ch = [[(en[0] if en else None) for en in ent] for slab, chunks, ent in cur["tiles"]]
                    mk = [[(en[1] if en else None) for en in ent] for slab, chunks, ent in cur["tiles"]]
                    if PASS_MODE == "wide":
                        cur["wide"] = ps_s.tile([P, 1024], F32, name="s_ps")
                        bank_a, calls_a = qk_bank(cur["h"], cur["g"], ch[0], mk[0], cur["wide"][:, 0:512])
                        bank_b, calls_b = qk_bank(cur["h"], cur["g"], ch[1], mk[1], cur["wide"][:, 512:1024])
                    else:
                        bank_a, calls_a = qk_bank(cur["h"], cur["g"], ch[0], mk[0])
                        bank_b, calls_b = qk_bank(cur["h"], cur["g"], ch[1], mk[1])
                    cur["banks"] = [bank_a, bank_b]
                    if T_WEAVE == "back":
                        run_calls(calls_a)
                        if mx:
                            fin_mx(mx)
                        run_calls(calls_b[0:1] + trs[0:1] + calls_b[1:2] + trs[1:2] + calls_b[2:3] + trs[2:3] + calls_b[3:] + trs[3:4])
                    elif T_WEAVE == "end":
                        run_calls(calls_a)
                        if mx:
                            fin_mx(mx)
                        run_calls(calls_b + trs)
                    elif T_WEAVE:
                        run_calls(trs[0:1] + calls_a[0:1] + trs[1:2] + calls_a[1:])
                        if mx:
                            fin_mx(mx)
                        run_calls(calls_b[0:1] + trs[2:3] + calls_b[1:2] + trs[3:4] + calls_b[2:])
                    else:
                        run_calls(trs + calls_a)
                        if mx:
                            fin_mx(mx)
                        run_calls(calls_b)
                else:
                    run_calls(trs)
                    if cur and cur["kind"] == "gs":
                        s = cur["s"]
                        bank_a, calls_a = qk_bank(
                            cur["h"], 0, [4 * s, 4 * s + 1, 4 * s + 2, 4 * s + 3], [None] * 4,
                            ps_s.tile([P, 1024], F32, name="s_ps")[:, 0:512] if PASS_MODE == "wide" else None,
                        )
                        cur["banks"] = [bank_a]
                        run_calls(calls_a)
                    if cur and cur["kind"] == "kq":
                        kq_transpose(cur)
                    if mx:
                        fin_mx(mx)
                nxt = at(t - ZERO_LAG, e_kinds)
                if nxt and nxt["gidx"] == 0:
                    acc_init(nxt["group"])
                if nxt:
                    e_zero(nxt)
                if prev and prev["kind"] == "unit":
                    unit_pass(prev, True)
                    if PASS_MODE != "chain":
                        unit_pass(prev, False)
                if prev and prev["kind"] == "gs":
                    gs_pass(prev)
                if prev and prev["kind"] == "kq":
                    kq_done.extend([(prev["h"], part, prev["s"]) for part in prev["parts"]])
                if prev and prev["kind"] == "kq" and "k" in prev["parts"]:
                    kt_s = KT_ON_SCALAR or (KT_S_UNTIL is not None and (prev["h"], prev["s"]) < KT_S_UNTIL)
                    kt_copy(prev, nc.scalar.copy if kt_s else nc.vector.tensor_copy)
                if qn:
                    e_quant(qn)
                if prev and prev["kind"] == "unit" and PASS_MODE == "chain":
                    unit_pass(prev, False)
                if at(t - RG_LAG, ("kq",)) and "k" in items[t - RG_LAG]["parts"]:
                    kq_regroup(items[t - RG_LAG])
                if at(t - VQ_LAG, ("kq",)) and "k" in items[t - VQ_LAG]["parts"]:
                    kq_vquant(items[t - VQ_LAG])
                if cp and cp_v:
                    e_copy(cp, True)
                if prev and prev["kind"] == "unit":
                    unit_comb(prev)
                if prev and prev["kind"] == "gs" and prev["s"] == NSLAB - 1:
                    gs_comb(prev)
                if rv:
                    fin_rinv(rv)
                if fo and fo_v[0] and not OUT_FIRST:
                    fin_out(fo, fo_v)
                has_q = prev is not None and prev["kind"] == "kq" and "q" in prev["parts"]
                qt_v = has_q and ((QT_ON_VECTOR and t - l_pass >= 2) or (QT_V_FROM is not None and (prev["h"], prev["s"]) >= QT_V_FROM))
                if qt_v:
                    qt_copy(prev, nc.vector.tensor_copy)
                if has_q and not qt_v:
                    qt_copy(prev, nc.scalar.copy)
                if cp and not cp_v:
                    e_copy(cp, False)
                if ex:
                    e_exp(ex)
                if fo and not fo_v[0] and not OUT_FIRST:
                    fin_out(fo, fo_v)
                if VAR_LAG is None:
                    i = t - VQ_LAG
                    if 0 <= i < len(items) and "variants" in items[i]:
                        build_variants(items[i]["variants"][0], items[i]["variants"][1])

        if PINNED:
            with tc.manual_schedule():
                stream()
        else:
            stream()
